import numpy as np
import ml_dtypes


def mxq(x, axis, fmt="e4m3"):
    dtype, down = {"e4m3": (ml_dtypes.float8_e4m3fn, 7), "e5m2": (ml_dtypes.float8_e5m2, 14)}[fmt]
    v = np.moveaxis(np.asarray(x, np.float32).astype(ml_dtypes.bfloat16).astype(np.float64), axis, -1)
    blocks = v.reshape(v.shape[:-1] + (-1, 32))
    amax = np.abs(blocks).max(-1, keepdims=True)
    byte = np.maximum(np.where(amax > 0, np.frexp(amax)[1] - 1 + 127, 0) - down, 1)
    scale = np.exp2(byte - 127.0)
    codes = (blocks / scale).astype(np.float32).astype(dtype).astype(np.float64)
    return np.moveaxis((codes * scale).reshape(v.shape), -1, axis)


WIDE = False


def mx_kscale(k):
    if not WIDE:
        return np.ones(k)
    levels = np.array([10, -10, 5, -5, 0])
    a = np.random.permutation(np.resize(levels, k // 512 * 4)).reshape(k // 512, 4)
    idx = np.arange(k)
    return np.exp2(a[idx // 512, idx % 128 // 32])


BF16 = ml_dtypes.bfloat16


def bf(x):
    return np.asarray(x, np.float32).astype(BF16)


def f64(x):
    return np.asarray(x).astype(np.float64)


B, C, H, W, P, DIM = 16, 8, 128, 128, 8, 512
SHIFT = P // 2
PD = 5 * C * P * P
EPS = 1e-5
XS = 0.015


def patch_shift(x, shift):
    xp = np.pad(x, ((0, 0), (0, 0), (shift, shift), (shift, shift)))
    s2 = 2 * shift
    return np.concatenate([x, xp[:, :, :-s2, :-s2], xp[:, :, :-s2, s2:], xp[:, :, s2:, :-s2], xp[:, :, s2:, s2:]], axis=1)


def patchify(x, p):
    b_, c_, hh, ww = x.shape
    h, w = hh // p, ww // p
    return x.reshape(b_, c_, h, p, w, p).transpose(0, 2, 4, 3, 5, 1).reshape(b_, h * w, p * p * c_)


def layernorm(u, g, b):
    m = u.mean(-1, keepdims=True)
    v = np.square(u - m).mean(-1, keepdims=True)
    return (u - m) / np.sqrt(v + EPS) * g + b


def setup_inputs():
    s = mx_kscale(PD)
    return {"x": bf(np.random.standard_normal((B, C, H, W)) * XS),
            "ln1_g": bf((1.0 + 0.1 * np.random.standard_normal(PD)) * s),
            "ln1_b": bf(0.1 * np.random.standard_normal(PD) * s),
            "w1": bf(np.random.standard_normal((PD, DIM)) / np.sqrt(PD) / s[:, None]),
            "b1": bf(0.3 * np.random.standard_normal(DIM))}


def reference(x, ln1_g, ln1_b, w1, b1):
    u = patchify(patch_shift(f64(x), SHIFT), P)
    z = layernorm(u, f64(ln1_g), f64(ln1_b))
    return (mxq(z, 2, "e4m3") @ mxq(f64(w1), 0, "e4m3")) + f64(b1)

@@ -1,0 +1,283 @@
+from contextlib import ExitStack
+
+import concourse.mybir as mybir
+from concourse.masks import make_identity
+
+FP8X4 = mybir.dt.float8_e4m3fn_x4
+BF16 = mybir.dt.bfloat16
+F32 = mybir.dt.float32
+U32 = mybir.dt.uint32
+U8 = mybir.dt.uint8
+ALU = mybir.AluOpType
+ACTF = mybir.ActivationFunctionType
+AX = mybir.AxisListType
+
+P = 128
+PD = 2560
+DIM = 512
+KT = PD // P
+PASSES = 5
+EPS = 1e-5
+SHIFTS = ((0, 0), (-4, -4), (-4, 4), (4, -4), (4, 4))
+FLOPS = 2 * 4096 * PD * DIM
+
+
+def tile_shiftedpatchtokenization_pa_t_kernel(tc, x, ln1_g, ln1_b, w1, b1, out):
+    nc = tc.nc
+    with ExitStack() as ctx:
+        const = ctx.enter_context(tc.tile_pool(name="const", bufs=1))
+        xpool = ctx.enter_context(tc.tile_pool(name="xpool", bufs=1))
+        wst = ctx.enter_context(tc.tile_pool(name="wst", bufs=5))
+        wgp = ctx.enter_context(tc.tile_pool(name="wgp", bufs=1))
+        sqp = ctx.enter_context(tc.tile_pool(name="sqp", bufs=2))
+        stp = ctx.enter_context(tc.tile_pool(name="stp", bufs=1))
+        npool = ctx.enter_context(tc.tile_pool(name="npool", bufs=6))
+        ppool = ctx.enter_context(tc.tile_pool(name="ppool", bufs=2))
+        gpool = ctx.enter_context(tc.tile_pool(name="gpool", bufs=2))
+        zpool = ctx.enter_context(tc.tile_pool(name="zpool", bufs=2))
+        rpool = ctx.enter_context(tc.tile_pool(name="rpool", bufs=3))
+        hop_ps = ctx.enter_context(tc.psum_pool(name="hop_ps", bufs=5))
+        acc_ps = ctx.enter_context(tc.psum_pool(name="acc_ps", bufs=2))
+        misc_ps = ctx.enter_context(tc.psum_pool(name="misc_ps", bufs=1))
+
+        xs = [xpool.tile([P, 8, 16, 128], BF16, name="x%d" % a) for a in range(2)]
+        for a in range(2):
+            nc.vector.memset(xs[a][0:8, :, 0:4, :], 0.0)
+            nc.vector.memset(xs[a][96:128, :, 12:16, :], 0.0)
+
+        def load_centre(a):
+            for bl in range(8):
+                nc.sync.dma_start(
+                    out=xs[a][bl:128:8, :, 4:12, :],
+                    in_=x[8 * a + bl].rearrange("c (i r) w -> i c r w", r=8),
+                )
+
+        def load_halos(a):
+            for bl in range(8):
+                src = x[8 * a + bl]
+                nc.sync.dma_start(
+                    out=xs[a][8 + bl:128:8, :, 0:4, :],
+                    in_=src[:, 4:124, :].rearrange("c (i r) w -> i c r w", r=8)[:, :, 0:4, :],
+                )
+                nc.sync.dma_start(
+                    out=xs[a][bl:120:8, :, 12:16, :],
+                    in_=src[:, 8:128, :].rearrange("c (i r) w -> i c r w", r=8)[:, :, 0:4, :],
+                )
+
+        load_centre(0)
+
+        ident = const.tile([P, P], F32, name="ident")
+        make_identity(nc, ident[:])
+        perm = const.tile([P, P], F32, name="perm")
+        nc.vector.tensor_copy(
+            out=perm[:].rearrange("p (b i) -> p b i", b=8),
+            in_=ident[:].rearrange("p (i b) -> p b i", b=8),
+        )
+        l1 = const.tile([P, P], F32, name="l1")
+        l0 = const.tile([P, P], F32, name="l0")
+        l1c = const.tile([P, P], F32, name="l1c")
+        l0c = const.tile([P, P], F32, name="l0c")
+        nc.vector.tensor_copy(out=l1[:], in_=ident[:])
+        nc.vector.tensor_tensor(out=l1[:, 8:128], in0=l1[:, 8:128], in1=ident[:, 0:120], op=ALU.add)
+        nc.vector.tensor_copy(out=l0[:], in_=ident[:])
+        nc.vector.tensor_tensor(out=l0[:, 0:120], in0=l0[:, 0:120], in1=ident[:, 8:128], op=ALU.add)
+        nc.vector.tensor_tensor(out=l1c[:], in0=l1[:], in1=ident[:], op=ALU.add)
+        nc.vector.tensor_tensor(out=l0c[:], in0=l0[:], in1=ident[:], op=ALU.add)
+        zt = const.tile([P, 8, 4, 8], BF16, name="zt")
+        nc.vector.memset(zt[:], 0.0)
+
+        gb_bf = const.tile([P, P], BF16, name="gb_bf")
+        nc.vector.memset(gb_bf[:], 0.0)
+        nc.sync.dma_start(out=gb_bf[0:KT, :], in_=ln1_g.rearrange("(c p) -> c p", p=P))
+        nc.sync.dma_start(out=gb_bf[32:32 + KT, :], in_=ln1_b.rearrange("(c p) -> c p", p=P))
+        gb_f = const.tile([P, P], F32, name="gb_f")
+        nc.vector.tensor_copy(out=gb_f[:], in_=gb_bf[:])
+        gb_ps = misc_ps.tile([P, 512], F32, name="misc")
+        nc.tensor.transpose(out=gb_ps[:, 0:P], in_=gb_f[:], identity=ident[:])
+        gbt = const.tile([P, P], F32, name="gbt")
+        nc.vector.tensor_copy(out=gbt[:], in_=gb_ps[:, 0:P])
+
+        b_bf = const.tile([P, DIM], BF16, name="b_bf")
+        load_halos(0)
+        nc.sync.dma_start(out=b_bf[:], in_=b1.partition_broadcast(P))
+        bias = const.tile([P, DIM], F32, name="bias")
+        nc.vector.tensor_copy(out=bias[:], in_=b_bf[:])
+
+        wc = const.tile([P, PASSES, DIM], U32, name="wc", align_bytes=64)
+        ws = const.tile([P, PASSES, DIM], U8, name="ws", align_bytes=64)
+        w_v = w1.rearrange("(g t p) n -> g p t n", t=4, p=P)
+        raws = []
+        for g in range(PASSES):
+            raw = wst.tile([P, 4, DIM], BF16, name="raw")
+            nc.sync.dma_start(out=raw[:], in_=w_v[g])
+            raws.append(raw)
+        load_centre(1)
+        load_halos(1)
+
+        def prep_w(g):
+            raw = raws[g]
+            wg = wgp.tile([P, DIM, 4], BF16, name="wg", align_bytes=64)
+            nc.vector.tensor_copy(
+                out=wg[:].rearrange("p (c i) t -> p c t i", i=4),
+                in_=raw[:].rearrange("p t (c i) -> p c t i", i=4),
+            )
+            nc.vector.quantize_mx(
+                out=wc[:, g, :].bitcast(FP8X4),
+                scales=ws[:, g, :],
+                in_=wg[:].rearrange("p w t -> p (w t)"),
+            )
+
+        mean = const.tile([P, 32], F32, name="mean")
+        rstd = const.tile([P, 32], F32, name="rstd")
+
+        def stats(a, s_lo, s_hi, j_lo, j_hi):
+            ns = s_hi - s_lo
+            nj = j_hi - j_lo
+            r1 = stp.tile([P, 2, 8, 2, ns], F32, name="r1_%d" % ns, tag="r1")
+            for ch in range(8):
+                cen = xs[a][:, ch, 4:12, 4 * s_lo:4 * s_hi]
+                sq = sqp.tile([P, 8, 4 * ns], F32, name="sq_%d" % ns, tag="sq")
+                nc.scalar.activation(out=sq[:], in_=cen, func=ACTF.Square)
+                nc.vector.tensor_reduce(
+                    out=r1[:, 0, ch, :, :],
+                    in_=cen.rearrange("p (h r) (c e) -> p h c r e", h=2, e=4),
+                    op=ALU.add, axis=AX.XY,
+                )
+                nc.vector.tensor_reduce(
+                    out=r1[:, 1, ch, :, :],
+                    in_=sq[:].rearrange("p (h r) (c e) -> p h c r e", h=2, e=4),
+                    op=ALU.add, axis=AX.XY,
+                )
+            hh = stp.tile([P, 2, 2, ns], F32, name="hh_%d" % ns, tag="hh")
+            nc.vector.tensor_reduce(
+                out=hh[:].rearrange("p s h c -> p s (h c)"),
+                in_=r1[:].rearrange("p s c h w -> p s (h w) c"),
+                op=ALU.add, axis=AX.X,
+            )
+            st = misc_ps.tile([P, 512], F32, name="misc")
+            stv = st[:, 0:4 * ns].rearrange("p (v s c) -> p v s c", v=2, s=2)
+            nc.tensor.matmul(out=stv[:, 0], lhsT=l1[:], rhs=hh[:, :, 1, :], start=True, stop=False)
+            nc.tensor.matmul(out=stv[:, 0], lhsT=l0[:], rhs=hh[:, :, 0, :], start=False, stop=True)
+            nc.tensor.matmul(out=stv[:, 1], lhsT=l1c[:], rhs=hh[:, :, 1, :], start=True, stop=False)
+            nc.tensor.matmul(out=stv[:, 1], lhsT=l0c[:], rhs=hh[:, :, 0, :], start=False, stop=True)
+            m0 = j_lo - s_lo // 2
+            winc = stv[:, 1].rearrange("p s (m e) -> p s m e", e=2)
+            win = stv[:, 0].rearrange("p s (m e) -> p s m e", e=2)
+            sa = stp.tile([P, 2, nj], F32, name="sa_%d" % nj, tag="sa")
+            nc.vector.tensor_reduce(out=sa[:], in_=winc[:, :, m0:m0 + nj, :], op=ALU.add, axis=AX.X)
+            dl = 1 if m0 == 0 else 0
+            dr = 1 if m0 + nj == ns // 2 else 0
+            nc.vector.tensor_tensor(
+                out=sa[:, :, dl:nj], in0=sa[:, :, dl:nj], in1=win[:, :, m0 + dl - 1:m0 + nj - 1, 1], op=ALU.add
+            )
+            nc.vector.tensor_tensor(
+                out=sa[:, :, 0:nj - dr], in0=sa[:, :, 0:nj - dr], in1=win[:, :, m0 + 1:m0 + nj + 1 - dr, 0], op=ALU.add
+            )
+            cols = slice(16 * a + j_lo, 16 * a + j_hi)
+            nc.vector.tensor_scalar(
+                out=mean[:, cols], in0=sa[:, 0, :], scalar1=1.0 / PD, scalar2=None, op0=ALU.mult
+            )
+            msq = stp.tile([P, nj], F32, name="msq_%d" % nj, tag="msq")
+            nc.vector.tensor_tensor(out=msq[:], in0=mean[:, cols], in1=mean[:, cols], op=ALU.mult)
+            ve = stp.tile([P, nj], F32, name="ve_%d" % nj, tag="ve")
+            nc.vector.scalar_tensor_tensor(
+                out=ve[:], in0=sa[:, 1, :], scalar=1.0 / PD, in1=msq[:], op0=ALU.mult, op1=ALU.subtract
+            )
+            nc.vector.tensor_scalar(out=ve[:], in0=ve[:], scalar1=EPS, scalar2=None, op0=ALU.add)
+            sd = stp.tile([P, nj], F32, name="sd_%d" % nj, tag="sd")
+            nc.scalar.activation(out=sd[:], in_=ve[:], func=ACTF.Sqrt)
+            r0 = stp.tile([P, nj], F32, name="r0_%d" % nj, tag="r0")
+            nc.vector.reciprocal(out=r0[:], in_=sd[:])
+            t0 = stp.tile([P, nj], F32, name="t0_%d" % nj, tag="t0")
+            nc.vector.tensor_tensor(out=t0[:], in0=r0[:], in1=r0[:], op=ALU.mult)
+            nc.vector.tensor_tensor(out=t0[:], in0=t0[:], in1=ve[:], op=ALU.mult)
+            nc.vector.tensor_scalar(out=t0[:], in0=t0[:], scalar1=-0.5, scalar2=1.5, op0=ALU.mult, op1=ALU.add)
+            nc.vector.tensor_tensor(out=rstd[:, cols], in0=r0[:], in1=t0[:], op=ALU.mult)
+
+        out_v = out.flatten_outer_dims().rearrange("(a n j) d -> a j n d", a=2, j=16)
+
+        def group(a, jq):
+            ntiles = []
+            for tau in range(4):
+                j = 4 * jq + tau
+                col = 16 * a + j
+                nt = npool.tile([P, PD], F32, name="nt")
+                nv = nt[:].rearrange("p (h w s c) -> p h w s c", h=8, w=8, s=5)
+                for s in range(5):
+                    r0 = 4 + SHIFTS[s][0]
+                    c0 = 8 * j + SHIFTS[s][1]
+                    lo = max(0, -c0)
+                    hi = min(8, 128 - c0)
+                    nc.vector.tensor_scalar(
+                        out=nv[:, :, lo:hi, s, :],
+                        in0=xs[a][:, :, r0:r0 + 8, c0 + lo:c0 + hi].rearrange("p c h w -> p h w c"),
+                        scalar1=mean[:, col:col + 1], scalar2=rstd[:, col:col + 1],
+                        op0=ALU.subtract, op1=ALU.mult,
+                    )
+                    if lo > 0:
+                        nc.vector.tensor_scalar(
+                            out=nv[:, :, 0:lo, s, :], in0=zt[:],
+                            scalar1=mean[:, col:col + 1], scalar2=rstd[:, col:col + 1],
+                            op0=ALU.subtract, op1=ALU.mult,
+                        )
+                    if hi < 8:
+                        nc.vector.tensor_scalar(
+                            out=nv[:, :, hi:8, s, :], in0=zt[:],
+                            scalar1=mean[:, col:col + 1], scalar2=rstd[:, col:col + 1],
+                            op0=ALU.subtract, op1=ALU.mult,
+                        )
+                ntiles.append(nt)
+            zc = zpool.tile([P, PASSES, 512], U32, name="zc", align_bytes=64)
+            zs = zpool.tile([P, PASSES, 512], U8, name="zs", align_bytes=64)
+            for g in range(PASSES):
+                planes = ppool.tile([P, 4, 512], BF16, name="planes")
+                for t in range(4):
+                    kt = 4 * g + t
+                    bank = hop_ps.tile([P, 512], F32, name="bank")
+                    for tau in range(4):
+                        nc.tensor.transpose(
+                            out=bank[:, tau * P:(tau + 1) * P],
+                            in_=ntiles[tau][:, kt * P:(kt + 1) * P],
+                            identity=perm[:],
+                        )
+                    nc.scalar.activation(
+                        out=planes[:, t, :], in_=bank[:], func=ACTF.Identity,
+                        scale=gbt[:, kt:kt + 1], bias=gbt[:, 32 + kt:33 + kt],
+                    )
+                grouped = gpool.tile([P, 512, 4], BF16, name="grouped", align_bytes=64)
+                nc.vector.tensor_copy(
+                    out=grouped[:].rearrange("p (c i) t -> p c t i", i=4),
+                    in_=planes[:].rearrange("p t (c i) -> p c t i", i=4),
+                )
+                nc.vector.quantize_mx(
+                    out=zc[:, g, :].bitcast(FP8X4),
+                    scales=zs[:, g, :],
+                    in_=grouped[:].rearrange("p w t -> p (w t)"),
+                )
+            for tau in range(4):
+                acc = acc_ps.tile([P, DIM], F32, name="acc")
+                for g in range(PASSES):
+                    nc.tensor.matmul_mx(
+                        out=acc[:],
+                        lhsT=zc[:, g, tau * P:(tau + 1) * P].bitcast(FP8X4),
+                        lhsT_scale=zs[:, g, tau * P:(tau + 1) * P],
+                        rhs=wc[:, g, :].bitcast(FP8X4),
+                        rhs_scale=ws[:, g, :],
+                        start=(g == 0),
+                        stop=(g == PASSES - 1),
+                    )
+                res = rpool.tile([P, DIM], F32, name="res")
+                nc.vector.tensor_tensor(out=res[:], in0=acc[:], in1=bias[:], op=ALU.add)
+                nc.sync.dma_start(out=out_v[a, 4 * jq + tau], in_=res[:])
+
+        stats(0, 0, 10, 0, 4)
+        for g in range(PASSES):
+            prep_w(g)
+        group(0, 0)
+        stats(0, 6, 32, 4, 16)
+        group(0, 1)
+        stats(1, 0, 32, 0, 16)
+        for jq in range(2, 4):
+            group(0, jq)
+        for jq in range(4):
+            group(1, jq)

@@ -208,12 +208,13 @@ def tile_shiftedpatchtokenization_pa_t_kernel(tc, x, ln1_g, ln1_b, w1, b1, out):
                     c0 = 8 * j + SHIFTS[s][1]
                     lo = max(0, -c0)
                     hi = min(8, 128 - c0)
-                    nc.vector.tensor_scalar(
-                        out=nv[:, :, lo:hi, s, :],
-                        in0=xs[a][:, :, r0:r0 + 8, c0 + lo:c0 + hi].rearrange("p c h w -> p h w c"),
-                        scalar1=mean[:, col:col + 1], scalar2=rstd[:, col:col + 1],
-                        op0=ALU.subtract, op1=ALU.mult,
-                    )
+                    for cq in range(2):
+                        nc.vector.tensor_scalar(
+                            out=nv[:, :, lo:hi, s, 4 * cq:4 * cq + 4],
+                            in0=xs[a][:, 4 * cq:4 * cq + 4, r0:r0 + 8, c0 + lo:c0 + hi].rearrange("p c h w -> p h w c"),
+                            scalar1=mean[:, col:col + 1], scalar2=rstd[:, col:col + 1],
+                            op0=ALU.subtract, op1=ALU.mult,
+                        )
                     if lo > 0:
                         nc.vector.tensor_scalar(
                             out=nv[:, :, 0:lo, s, :], in0=zt[:],

@@ -20,6 +20,8 @@ PASSES = 5
 EPS = 1e-5
 SHIFTS = ((0, 0), (-4, -4), (-4, 4), (4, -4), (4, 4))
 FLOPS = 2 * 4096 * PD * DIM
+WHO = ("v", "g", "g", "", "a")
+WHO3 = ("g", "g", "a", "v")
 
 
 def tile_shiftedpatchtokenization_pa_t_kernel(tc, x, ln1_g, ln1_b, w1, b1, out):
@@ -27,11 +29,11 @@ def tile_shiftedpatchtokenization_pa_t_kernel(tc, x, ln1_g, ln1_b, w1, b1, out):
     with ExitStack() as ctx:
         const = ctx.enter_context(tc.tile_pool(name="const", bufs=1))
         xpool = ctx.enter_context(tc.tile_pool(name="xpool", bufs=1))
-        wst = ctx.enter_context(tc.tile_pool(name="wst", bufs=5))
+        wst = ctx.enter_context(tc.tile_pool(name="wst", bufs=3))
         wgp = ctx.enter_context(tc.tile_pool(name="wgp", bufs=1))
         sqp = ctx.enter_context(tc.tile_pool(name="sqp", bufs=2))
         stp = ctx.enter_context(tc.tile_pool(name="stp", bufs=1))
-        npool = ctx.enter_context(tc.tile_pool(name="npool", bufs=6))
+        npool = ctx.enter_context(tc.tile_pool(name="npool", bufs=7))
         ppool = ctx.enter_context(tc.tile_pool(name="ppool", bufs=2))
         gpool = ctx.enter_context(tc.tile_pool(name="gpool", bufs=2))
         zpool = ctx.enter_context(tc.tile_pool(name="zpool", bufs=2))
@@ -107,10 +109,14 @@ def tile_shiftedpatchtokenization_pa_t_kernel(tc, x, ln1_g, ln1_b, w1, b1, out):
         ws = const.tile([P, PASSES, DIM], U8, name="ws", align_bytes=64)
         w_v = w1.rearrange("(g t p) n -> g p t n", t=4, p=P)
         raws = []
-        for g in range(PASSES):
+
+        def load_w(g):
             raw = wst.tile([P, 4, DIM], BF16, name="raw")
             nc.sync.dma_start(out=raw[:], in_=w_v[g])
             raws.append(raw)
+
+        for g in range(3):
+            load_w(g)
         load_centre(1)
         load_halos(1)
 
@@ -129,6 +135,7 @@ def tile_shiftedpatchtokenization_pa_t_kernel(tc, x, ln1_g, ln1_b, w1, b1, out):
 
         mean = const.tile([P, 32], F32, name="mean")
         rstd = const.tile([P, 32], F32, name="rstd")
+        nmr = const.tile([P, 32], F32, name="nmr")
 
         def stats(a, s_lo, s_hi, j_lo, j_hi):
             ns = s_hi - s_lo
@@ -193,6 +200,9 @@ def tile_shiftedpatchtokenization_pa_t_kernel(tc, x, ln1_g, ln1_b, w1, b1, out):
             nc.vector.tensor_tensor(out=t0[:], in0=t0[:], in1=ve[:], op=ALU.mult)
             nc.vector.tensor_scalar(out=t0[:], in0=t0[:], scalar1=-0.5, scalar2=1.5, op0=ALU.mult, op1=ALU.add)
             nc.vector.tensor_tensor(out=rstd[:, cols], in0=r0[:], in1=t0[:], op=ALU.mult)
+            nc.vector.scalar_tensor_tensor(
+                out=nmr[:, cols], in0=mean[:, cols], scalar=-1.0, in1=rstd[:, cols], op0=ALU.mult, op1=ALU.mult
+            )
 
         out_v = out.flatten_outer_dims().rearrange("(a n j) d -> a j n d", a=2, j=16)
 
@@ -208,25 +218,32 @@ def tile_shiftedpatchtokenization_pa_t_kernel(tc, x, ln1_g, ln1_b, w1, b1, out):
                     c0 = 8 * j + SHIFTS[s][1]
                     lo = max(0, -c0)
                     hi = min(8, 128 - c0)
-                    for cq in range(2):
-                        nc.vector.tensor_scalar(
-                            out=nv[:, :, lo:hi, s, 4 * cq:4 * cq + 4],
-                            in0=xs[a][:, 4 * cq:4 * cq + 4, r0:r0 + 8, c0 + lo:c0 + hi].rearrange("p c h w -> p h w c"),
-                            scalar1=mean[:, col:col + 1], scalar2=rstd[:, col:col + 1],
-                            op0=ALU.subtract, op1=ALU.mult,
-                        )
+                    eng = WHO[s] if s != 3 else WHO3[(4 * jq + tau) % 4]
+                    pieces = [
+                        (nv[:, :, lo:hi, s, 4 * cq:4 * cq + 4],
+                         xs[a][:, 4 * cq:4 * cq + 4, r0:r0 + 8, c0 + lo:c0 + hi].rearrange("p c h w -> p h w c"))
+                        for cq in range(2)
+                    ]
                     if lo > 0:
-                        nc.vector.tensor_scalar(
-                            out=nv[:, :, 0:lo, s, :], in0=zt[:],
-                            scalar1=mean[:, col:col + 1], scalar2=rstd[:, col:col + 1],
-                            op0=ALU.subtract, op1=ALU.mult,
-                        )
+                        pieces.append((nv[:, :, 0:lo, s, :], zt[:]))
                     if hi < 8:
-                        nc.vector.tensor_scalar(
-                            out=nv[:, :, hi:8, s, :], in0=zt[:],
-                            scalar1=mean[:, col:col + 1], scalar2=rstd[:, col:col + 1],
-                            op0=ALU.subtract, op1=ALU.mult,
-                        )
+                        pieces.append((nv[:, :, hi:8, s, :], zt[:]))
+                    for dst, src in pieces:
+                        if eng == "v":
+                            nc.vector.tensor_scalar(
+                                out=dst, in0=src, scalar1=mean[:, col:col + 1], scalar2=rstd[:, col:col + 1],
+                                op0=ALU.subtract, op1=ALU.mult,
+                            )
+                        elif eng == "g":
+                            nc.gpsimd.tensor_scalar(
+                                out=dst, in0=src, scalar1=rstd[:, col:col + 1], scalar2=nmr[:, col:col + 1],
+                                op0=ALU.mult, op1=ALU.add,
+                            )
+                        else:
+                            nc.scalar.activation(
+                                out=dst, in_=src, func=ACTF.Identity,
+                                scale=rstd[:, col:col + 1], bias=nmr[:, col:col + 1],
+                            )
                 ntiles.append(nt)
             zc = zpool.tile([P, PASSES, 512], U32, name="zc", align_bytes=64)
             zs = zpool.tile([P, PASSES, 512], U8, name="zs", align_bytes=64)
@@ -273,6 +290,8 @@ def tile_shiftedpatchtokenization_pa_t_kernel(tc, x, ln1_g, ln1_b, w1, b1, out):
 
         stats(0, 0, 10, 0, 4)
         for g in range(PASSES):
+            if g >= 3:
+                load_w(g)
             prep_w(g)
         group(0, 0)
         stats(0, 6, 32, 4, 16)

@@ -20,8 +20,8 @@ PASSES = 5
 EPS = 1e-5
 SHIFTS = ((0, 0), (-4, -4), (-4, 4), (4, -4), (4, 4))
 FLOPS = 2 * 4096 * PD * DIM
-WHO = ("v", "g", "g", "", "a")
-WHO3 = ("g", "g", "a", "v")
+T_ON_ACT = (3,)
+R_ON_ACT = (1, 3)
 
 
 def tile_shiftedpatchtokenization_pa_t_kernel(tc, x, ln1_g, ln1_b, w1, b1, out):
@@ -31,16 +31,14 @@ def tile_shiftedpatchtokenization_pa_t_kernel(tc, x, ln1_g, ln1_b, w1, b1, out):
         xpool = ctx.enter_context(tc.tile_pool(name="xpool", bufs=1))
         wst = ctx.enter_context(tc.tile_pool(name="wst", bufs=3))
         wgp = ctx.enter_context(tc.tile_pool(name="wgp", bufs=1))
-        sqp = ctx.enter_context(tc.tile_pool(name="sqp", bufs=2))
         stp = ctx.enter_context(tc.tile_pool(name="stp", bufs=1))
-        npool = ctx.enter_context(tc.tile_pool(name="npool", bufs=7))
-        ppool = ctx.enter_context(tc.tile_pool(name="ppool", bufs=2))
+        npool = ctx.enter_context(tc.tile_pool(name="npool", bufs=8))
+        ppool = ctx.enter_context(tc.tile_pool(name="ppool", bufs=3))
         gpool = ctx.enter_context(tc.tile_pool(name="gpool", bufs=2))
         zpool = ctx.enter_context(tc.tile_pool(name="zpool", bufs=2))
-        rpool = ctx.enter_context(tc.tile_pool(name="rpool", bufs=3))
-        hop_ps = ctx.enter_context(tc.psum_pool(name="hop_ps", bufs=5))
+        rpool = ctx.enter_context(tc.tile_pool(name="rpool", bufs=2))
+        hop_ps = ctx.enter_context(tc.psum_pool(name="hop_ps", bufs=6))
         acc_ps = ctx.enter_context(tc.psum_pool(name="acc_ps", bufs=2))
-        misc_ps = ctx.enter_context(tc.psum_pool(name="misc_ps", bufs=1))
 
         xs = [xpool.tile([P, 8, 16, 128], BF16, name="x%d" % a) for a in range(2)]
         for a in range(2):
@@ -94,7 +92,7 @@ def tile_shiftedpatchtokenization_pa_t_kernel(tc, x, ln1_g, ln1_b, w1, b1, out):
         nc.sync.dma_start(out=gb_bf[32:32 + KT, :], in_=ln1_b.rearrange("(c p) -> c p", p=P))
         gb_f = const.tile([P, P], F32, name="gb_f")
         nc.vector.tensor_copy(out=gb_f[:], in_=gb_bf[:])
-        gb_ps = misc_ps.tile([P, 512], F32, name="misc")
+        gb_ps = acc_ps.tile([P, 512], F32, name="acc")
         nc.tensor.transpose(out=gb_ps[:, 0:P], in_=gb_f[:], identity=ident[:])
         gbt = const.tile([P, P], F32, name="gbt")
         nc.vector.tensor_copy(out=gbt[:], in_=gb_ps[:, 0:P])
@@ -140,28 +138,25 @@ def tile_shiftedpatchtokenization_pa_t_kernel(tc, x, ln1_g, ln1_b, w1, b1, out):
         def stats(a, s_lo, s_hi, j_lo, j_hi):
             ns = s_hi - s_lo
             nj = j_hi - j_lo
-            r1 = stp.tile([P, 2, 8, 2, ns], F32, name="r1_%d" % ns, tag="r1")
-            for ch in range(8):
-                cen = xs[a][:, ch, 4:12, 4 * s_lo:4 * s_hi]
-                sq = sqp.tile([P, 8, 4 * ns], F32, name="sq_%d" % ns, tag="sq")
-                nc.scalar.activation(out=sq[:], in_=cen, func=ACTF.Square)
-                nc.vector.tensor_reduce(
-                    out=r1[:, 0, ch, :, :],
-                    in_=cen.rearrange("p (h r) (c e) -> p h c r e", h=2, e=4),
-                    op=ALU.add, axis=AX.XY,
-                )
-                nc.vector.tensor_reduce(
-                    out=r1[:, 1, ch, :, :],
-                    in_=sq[:].rearrange("p (h r) (c e) -> p h c r e", h=2, e=4),
-                    op=ALU.add, axis=AX.XY,
-                )
+            bs = stp.tile([P, 2, ns, 6], F32, name="bs_%d" % ns, tag="bs")
+            for h in range(2):
+                for c in range(ns):
+                    nc.vector.bn_stats(
+                        out=bs[:, h, c, :],
+                        in_=xs[a][:, :, 4 + 4 * h:8 + 4 * h, 4 * (s_lo + c):4 * (s_lo + c) + 4],
+                    )
             hh = stp.tile([P, 2, 2, ns], F32, name="hh_%d" % ns, tag="hh")
-            nc.vector.tensor_reduce(
-                out=hh[:].rearrange("p s h c -> p s (h c)"),
-                in_=r1[:].rearrange("p s c h w -> p s (h w) c"),
-                op=ALU.add, axis=AX.X,
+            b2 = stp.tile([P, 2, ns], F32, name="b2_%d" % ns, tag="b2")
+            c2 = stp.tile([P, 2, ns], F32, name="c2_%d" % ns, tag="c2")
+            nc.vector.tensor_tensor(out=hh[:, 0], in0=bs[:, :, :, 1], in1=bs[:, :, :, 4], op=ALU.add)
+            nc.vector.tensor_tensor(out=b2[:], in0=bs[:, :, :, 1], in1=bs[:, :, :, 1], op=ALU.mult)
+            nc.vector.tensor_tensor(out=c2[:], in0=bs[:, :, :, 4], in1=bs[:, :, :, 4], op=ALU.mult)
+            nc.vector.tensor_tensor(out=b2[:], in0=b2[:], in1=c2[:], op=ALU.add)
+            nc.vector.tensor_tensor(out=c2[:], in0=bs[:, :, :, 2], in1=bs[:, :, :, 5], op=ALU.add)
+            nc.vector.scalar_tensor_tensor(
+                out=hh[:, 1], in0=b2[:], scalar=64.0, in1=c2[:], op0=ALU.mult, op1=ALU.add
             )
-            st = misc_ps.tile([P, 512], F32, name="misc")
+            st = acc_ps.tile([P, 512], F32, name="acc")
             stv = st[:, 0:4 * ns].rearrange("p (v s c) -> p v s c", v=2, s=2)
             nc.tensor.matmul(out=stv[:, 0], lhsT=l1[:], rhs=hh[:, :, 1, :], start=True, stop=False)
             nc.tensor.matmul(out=stv[:, 0], lhsT=l0[:], rhs=hh[:, :, 0, :], start=False, stop=True)
@@ -182,7 +177,7 @@ def tile_shiftedpatchtokenization_pa_t_kernel(tc, x, ln1_g, ln1_b, w1, b1, out):
             )
             cols = slice(16 * a + j_lo, 16 * a + j_hi)
             nc.vector.tensor_scalar(
-                out=mean[:, cols], in0=sa[:, 0, :], scalar1=1.0 / PD, scalar2=None, op0=ALU.mult
+                out=mean[:, cols], in0=sa[:, 0, :], scalar1=64.0 / PD, scalar2=None, op0=ALU.mult
             )
             msq = stp.tile([P, nj], F32, name="msq_%d" % nj, tag="msq")
             nc.vector.tensor_tensor(out=msq[:], in0=mean[:, cols], in1=mean[:, cols], op=ALU.mult)
@@ -205,73 +200,84 @@ def tile_shiftedpatchtokenization_pa_t_kernel(tc, x, ln1_g, ln1_b, w1, b1, out):
             )
 
         out_v = out.flatten_outer_dims().rearrange("(a n j) d -> a j n d", a=2, j=16)
+        ntiles = {}
+        ztiles = {}
+        planes_of = {}
 
-        def group(a, jq):
-            ntiles = []
+        def norm(gi, s):
+            a = gi // 4
             for tau in range(4):
-                j = 4 * jq + tau
+                j = 4 * (gi % 4) + tau
                 col = 16 * a + j
-                nt = npool.tile([P, PD], F32, name="nt")
-                nv = nt[:].rearrange("p (h w s c) -> p h w s c", h=8, w=8, s=5)
-                for s in range(5):
-                    r0 = 4 + SHIFTS[s][0]
-                    c0 = 8 * j + SHIFTS[s][1]
-                    lo = max(0, -c0)
-                    hi = min(8, 128 - c0)
-                    eng = WHO[s] if s != 3 else WHO3[(4 * jq + tau) % 4]
-                    pieces = [
-                        (nv[:, :, lo:hi, s, 4 * cq:4 * cq + 4],
-                         xs[a][:, 4 * cq:4 * cq + 4, r0:r0 + 8, c0 + lo:c0 + hi].rearrange("p c h w -> p h w c"))
-                        for cq in range(2)
-                    ]
-                    if lo > 0:
-                        pieces.append((nv[:, :, 0:lo, s, :], zt[:]))
-                    if hi < 8:
-                        pieces.append((nv[:, :, hi:8, s, :], zt[:]))
-                    for dst, src in pieces:
-                        if eng == "v":
-                            nc.vector.tensor_scalar(
-                                out=dst, in0=src, scalar1=mean[:, col:col + 1], scalar2=rstd[:, col:col + 1],
-                                op0=ALU.subtract, op1=ALU.mult,
-                            )
-                        elif eng == "g":
-                            nc.gpsimd.tensor_scalar(
-                                out=dst, in0=src, scalar1=rstd[:, col:col + 1], scalar2=nmr[:, col:col + 1],
-                                op0=ALU.mult, op1=ALU.add,
-                            )
-                        else:
-                            nc.scalar.activation(
-                                out=dst, in_=src, func=ACTF.Identity,
-                                scale=rstd[:, col:col + 1], bias=nmr[:, col:col + 1],
-                            )
-                ntiles.append(nt)
-            zc = zpool.tile([P, PASSES, 512], U32, name="zc", align_bytes=64)
-            zs = zpool.tile([P, PASSES, 512], U8, name="zs", align_bytes=64)
-            for g in range(PASSES):
-                planes = ppool.tile([P, 4, 512], BF16, name="planes")
-                for t in range(4):
-                    kt = 4 * g + t
-                    bank = hop_ps.tile([P, 512], F32, name="bank")
-                    for tau in range(4):
-                        nc.tensor.transpose(
-                            out=bank[:, tau * P:(tau + 1) * P],
-                            in_=ntiles[tau][:, kt * P:(kt + 1) * P],
-                            identity=perm[:],
+                if s == 0:
+                    ntiles[(gi, tau)] = npool.tile([P, PD], F32, name="nt")
+                nv = ntiles[(gi, tau)][:].rearrange("p (h w s c) -> p h w s c", h=8, w=8, s=5)
+                r0 = 4 + SHIFTS[s][0]
+                c0 = 8 * j + SHIFTS[s][1]
+                lo = max(0, -c0)
+                hi = min(8, 128 - c0)
+                pieces = [
+                    (nv[:, :, lo:hi, s, 4 * cq:4 * cq + 4],
+                     xs[a][:, 4 * cq:4 * cq + 4, r0:r0 + 8, c0 + lo:c0 + hi].rearrange("p c h w -> p h w c"))
+                    for cq in range(2)
+                ]
+                if lo > 0:
+                    pieces.append((nv[:, :, 0:lo, s, :], zt[:]))
+                if hi < 8:
+                    pieces.append((nv[:, :, hi:8, s, :], zt[:]))
+                for dst, src in pieces:
+                    if s in T_ON_ACT or (gi == 0 and s == 1):
+                        nc.scalar.activation(
+                            out=dst, in_=src, func=ACTF.Identity,
+                            scale=rstd[:, col:col + 1], bias=nmr[:, col:col + 1],
                         )
-                    nc.scalar.activation(
-                        out=planes[:, t, :], in_=bank[:], func=ACTF.Identity,
-                        scale=gbt[:, kt:kt + 1], bias=gbt[:, 32 + kt:33 + kt],
+                    else:
+                        nc.vector.tensor_scalar(
+                            out=dst, in0=src, scalar1=mean[:, col:col + 1], scalar2=rstd[:, col:col + 1],
+                            op0=ALU.subtract, op1=ALU.mult,
+                        )
+
+        def hop(gi, g):
+            planes = ppool.tile([P, 4, 512], BF16, name="planes")
+            planes_of[(gi, g)] = planes
+            for t in range(4):
+                kt = 4 * g + t
+                bank = hop_ps.tile([P, 512], F32, name="bank")
+                for tau in range(4):
+                    nc.tensor.transpose(
+                        out=bank[:, tau * P:(tau + 1) * P],
+                        in_=ntiles[(gi, tau)][:, kt * P:(kt + 1) * P],
+                        identity=perm[:],
                     )
-                grouped = gpool.tile([P, 512, 4], BF16, name="grouped", align_bytes=64)
-                nc.vector.tensor_copy(
-                    out=grouped[:].rearrange("p (c i) t -> p c t i", i=4),
-                    in_=planes[:].rearrange("p t (c i) -> p c t i", i=4),
+                nc.scalar.activation(
+                    out=planes[:, t, :], in_=bank[:], func=ACTF.Identity,
+                    scale=gbt[:, kt:kt + 1], bias=gbt[:, 32 + kt:33 + kt],
                 )
-                nc.vector.quantize_mx(
-                    out=zc[:, g, :].bitcast(FP8X4),
-                    scales=zs[:, g, :],
-                    in_=grouped[:].rearrange("p w t -> p (w t)"),
+
+        def quant(gi, g):
+            if g == 0:
+                ztiles[gi] = (
+                    zpool.tile([P, PASSES, 512], U32, name="zc", align_bytes=64),
+                    zpool.tile([P, PASSES, 512], U8, name="zs", align_bytes=64),
                 )
+            zc, zs = ztiles[gi]
+            planes = planes_of[(gi, g)]
+            grouped = gpool.tile([P, 512, 4], BF16, name="grouped", align_bytes=64)
+            dst = grouped[:].rearrange("p (c i) t -> p c t i", i=4)
+            src = planes[:].rearrange("p t (c i) -> p c t i", i=4)
+            if g in R_ON_ACT:
+                nc.scalar.copy(out=dst, in_=src)
+            else:
+                nc.vector.tensor_copy(out=dst, in_=src)
+            nc.vector.quantize_mx(
+                out=zc[:, g, :].bitcast(FP8X4),
+                scales=zs[:, g, :],
+                in_=grouped[:].rearrange("p w t -> p (w t)"),
+            )
+
+        def mx(gi):
+            a = gi // 4
+            zc, zs = ztiles[gi]
             for tau in range(4):
                 acc = acc_ps.tile([P, DIM], F32, name="acc")
                 for g in range(PASSES):
@@ -286,18 +292,28 @@ def tile_shiftedpatchtokenization_pa_t_kernel(tc, x, ln1_g, ln1_b, w1, b1, out):
                     )
                 res = rpool.tile([P, DIM], F32, name="res")
                 nc.vector.tensor_tensor(out=res[:], in0=acc[:], in1=bias[:], op=ALU.add)
-                nc.sync.dma_start(out=out_v[a, 4 * jq + tau], in_=res[:])
+                nc.sync.dma_start(out=out_v[a, 4 * (gi % 4) + tau], in_=res[:])
 
+        NG = 8
         stats(0, 0, 10, 0, 4)
+        for s in range(5):
+            norm(0, s)
         for g in range(PASSES):
             if g >= 3:
                 load_w(g)
             prep_w(g)
-        group(0, 0)
         stats(0, 6, 32, 4, 16)
-        group(0, 1)
-        stats(1, 0, 32, 0, 16)
-        for jq in range(2, 4):
-            group(0, jq)
-        for jq in range(4):
-            group(1, jq)
+        for it in range(1, NG + 2):
+            if it == 2:
+                stats(1, 0, 32, 0, 16)
+            for g in range(PASSES):
+                if it - 1 < NG:
+                    hop(it - 1, g)
+                if it < NG:
+                    norm(it, g)
+                if it - 1 < NG and g >= 1:
+                    quant(it - 1, g - 1)
+            if it - 1 < NG:
+                quant(it - 1, PASSES - 1)
+            if it >= 2:
+                mx(it - 2)

@@ -22,6 +22,9 @@ SHIFTS = ((0, 0), (-4, -4), (-4, 4), (4, -4), (4, 4))
 FLOPS = 2 * 4096 * PD * DIM
 T_ON_ACT = (3,)
 R_ON_ACT = (1, 3)
+LAG_R = 1
+LAG_Q = 2
+LAG_M = 3
 
 
 def tile_shiftedpatchtokenization_pa_t_kernel(tc, x, ln1_g, ln1_b, w1, b1, out):
@@ -35,10 +38,10 @@ def tile_shiftedpatchtokenization_pa_t_kernel(tc, x, ln1_g, ln1_b, w1, b1, out):
         npool = ctx.enter_context(tc.tile_pool(name="npool", bufs=8))
         ppool = ctx.enter_context(tc.tile_pool(name="ppool", bufs=3))
         gpool = ctx.enter_context(tc.tile_pool(name="gpool", bufs=2))
-        zpool = ctx.enter_context(tc.tile_pool(name="zpool", bufs=2))
-        rpool = ctx.enter_context(tc.tile_pool(name="rpool", bufs=2))
-        hop_ps = ctx.enter_context(tc.psum_pool(name="hop_ps", bufs=6))
-        acc_ps = ctx.enter_context(tc.psum_pool(name="acc_ps", bufs=2))
+        zpool = ctx.enter_context(tc.tile_pool(name="zpool", bufs=5))
+        rpool = ctx.enter_context(tc.tile_pool(name="rpool", bufs=3))
+        hop_ps = ctx.enter_context(tc.psum_pool(name="hop_ps", bufs=4))
+        acc_ps = ctx.enter_context(tc.psum_pool(name="acc_ps", bufs=4))
 
         xs = [xpool.tile([P, 8, 16, 128], BF16, name="x%d" % a) for a in range(2)]
         for a in range(2):
@@ -66,6 +69,9 @@ def tile_shiftedpatchtokenization_pa_t_kernel(tc, x, ln1_g, ln1_b, w1, b1, out):
 
         load_centre(0)
 
+        one = const.tile([P, 1], F32, name="one")
+        nc.vector.memset(one[:], 1.0)
+        nc.scalar.activation(out=one[:], in_=one[:], func=ACTF.Sqrt)
         ident = const.tile([P, P], F32, name="ident")
         make_identity(nc, ident[:])
         perm = const.tile([P, P], F32, name="perm")
@@ -203,6 +209,8 @@ def tile_shiftedpatchtokenization_pa_t_kernel(tc, x, ln1_g, ln1_b, w1, b1, out):
         ntiles = {}
         ztiles = {}
         planes_of = {}
+        grouped_of = {}
+        accs = {}
 
         def norm(gi, s):
             a = gi // 4
@@ -254,47 +262,47 @@ def tile_shiftedpatchtokenization_pa_t_kernel(tc, x, ln1_g, ln1_b, w1, b1, out):
                     scale=gbt[:, kt:kt + 1], bias=gbt[:, 32 + kt:33 + kt],
                 )
 
-        def quant(gi, g):
-            if g == 0:
-                ztiles[gi] = (
-                    zpool.tile([P, PASSES, 512], U32, name="zc", align_bytes=64),
-                    zpool.tile([P, PASSES, 512], U8, name="zs", align_bytes=64),
-                )
-            zc, zs = ztiles[gi]
-            planes = planes_of[(gi, g)]
+        def regroup(gi, g):
             grouped = gpool.tile([P, 512, 4], BF16, name="grouped", align_bytes=64)
+            grouped_of[(gi, g)] = grouped
             dst = grouped[:].rearrange("p (c i) t -> p c t i", i=4)
-            src = planes[:].rearrange("p t (c i) -> p c t i", i=4)
+            src = planes_of[(gi, g)][:].rearrange("p t (c i) -> p c t i", i=4)
             if g in R_ON_ACT:
                 nc.scalar.copy(out=dst, in_=src)
             else:
                 nc.vector.tensor_copy(out=dst, in_=src)
+
+        def quant(gi, g):
+            zc = zpool.tile([P, 512], U32, name="zc", align_bytes=64)
+            zs = zpool.tile([P, 512], U8, name="zs", align_bytes=64)
+            ztiles[(gi, g)] = (zc, zs)
             nc.vector.quantize_mx(
-                out=zc[:, g, :].bitcast(FP8X4),
-                scales=zs[:, g, :],
-                in_=grouped[:].rearrange("p w t -> p (w t)"),
+                out=zc[:].bitcast(FP8X4), scales=zs[:],
+                in_=grouped_of[(gi, g)][:].rearrange("p w t -> p (w t)"),
             )
 
-        def mx(gi):
-            a = gi // 4
-            zc, zs = ztiles[gi]
+        def mx(gi, g):
+            zc, zs = ztiles[(gi, g)]
             for tau in range(4):
-                acc = acc_ps.tile([P, DIM], F32, name="acc")
-                for g in range(PASSES):
-                    nc.tensor.matmul_mx(
-                        out=acc[:],
-                        lhsT=zc[:, g, tau * P:(tau + 1) * P].bitcast(FP8X4),
-                        lhsT_scale=zs[:, g, tau * P:(tau + 1) * P],
-                        rhs=wc[:, g, :].bitcast(FP8X4),
-                        rhs_scale=ws[:, g, :],
-                        start=(g == 0),
-                        stop=(g == PASSES - 1),
-                    )
-                res = rpool.tile([P, DIM], F32, name="res")
-                nc.vector.tensor_tensor(out=res[:], in0=acc[:], in1=bias[:], op=ALU.add)
-                nc.sync.dma_start(out=out_v[a, 4 * (gi % 4) + tau], in_=res[:])
+                if g == 0:
+                    accs[(gi, tau)] = acc_ps.tile([P, DIM], F32, name="acc")
+                nc.tensor.matmul_mx(
+                    out=accs[(gi, tau)][:],
+                    lhsT=zc[:, tau * P:(tau + 1) * P].bitcast(FP8X4),
+                    lhsT_scale=zs[:, tau * P:(tau + 1) * P],
+                    rhs=wc[:, g, :].bitcast(FP8X4),
+                    rhs_scale=ws[:, g, :],
+                    start=(g == 0),
+                    stop=(g == PASSES - 1),
+                )
+
+        def finish(gi, tau):
+            res = rpool.tile([P, DIM], F32, name="res")
+            nc.vector.tensor_tensor(out=res[:], in0=accs[(gi, tau)][:], in1=bias[:], op=ALU.add)
+            nc.sync.dma_start(out=out_v[gi // 4, 4 * (gi % 4) + tau], in_=res[:])
 
         NG = 8
+        NS = NG * PASSES
         stats(0, 0, 10, 0, 4)
         for s in range(5):
             norm(0, s)
@@ -303,17 +311,19 @@ def tile_shiftedpatchtokenization_pa_t_kernel(tc, x, ln1_g, ln1_b, w1, b1, out):
                 load_w(g)
             prep_w(g)
         stats(0, 6, 32, 4, 16)
-        for it in range(1, NG + 2):
-            if it == 2:
+        for sl in range(NS + LAG_M + 1):
+            if sl == 5:
                 stats(1, 0, 32, 0, 16)
-            for g in range(PASSES):
-                if it - 1 < NG:
-                    hop(it - 1, g)
-                if it < NG:
-                    norm(it, g)
-                if it - 1 < NG and g >= 1:
-                    quant(it - 1, g - 1)
-            if it - 1 < NG:
-                quant(it - 1, PASSES - 1)
-            if it >= 2:
-                mx(it - 2)
+            if sl < NS:
+                hop(sl // 5, sl % 5)
+            if sl - LAG_M >= 0 and sl - LAG_M < NS:
+                mx((sl - LAG_M) // 5, (sl - LAG_M) % 5)
+            if sl + 5 < NS:
+                norm(sl // 5 + 1, sl % 5)
+            if sl - LAG_R >= 0 and sl - LAG_R < NS:
+                regroup((sl - LAG_R) // 5, (sl - LAG_R) % 5)
+            if sl - LAG_Q >= 0 and sl - LAG_Q < NS:
+                quant((sl - LAG_Q) // 5, (sl - LAG_Q) % 5)
+            if sl - LAG_M - 1 >= 0 and (sl - LAG_M - 1) % 5 == 4:
+                for tau in range(4):
+                    finish((sl - LAG_M - 1) // 5, tau)

@@ -18,10 +18,9 @@ DIM = 512
 KT = PD // P
 PASSES = 5
 EPS = 1e-5
-SHIFTS = ((0, 0), (-4, -4), (-4, 4), (4, -4), (4, 4))
+CENTRE_ON_ACT = (1, 3)
 FLOPS = 2 * 4096 * PD * DIM
-T_ON_ACT = (3,)
-R_ON_ACT = (1, 3)
+NORM_STEP = {0: 0, 1: 1, 2: 2, 4: 3}
 LAG_R = 1
 LAG_Q = 2
 LAG_M = 3
@@ -30,6 +29,7 @@ LAG_M = 3
 def tile_shiftedpatchtokenization_pa_t_kernel(tc, x, ln1_g, ln1_b, w1, b1, out):
     nc = tc.nc
     with ExitStack() as ctx:
+        ctx.enter_context(tc.manual_schedule(engines={mybir.EngineType.SP}))
         const = ctx.enter_context(tc.tile_pool(name="const", bufs=1))
         xpool = ctx.enter_context(tc.tile_pool(name="xpool", bufs=1))
         wst = ctx.enter_context(tc.tile_pool(name="wst", bufs=3))
@@ -44,30 +44,30 @@ def tile_shiftedpatchtokenization_pa_t_kernel(tc, x, ln1_g, ln1_b, w1, b1, out):
         acc_ps = ctx.enter_context(tc.psum_pool(name="acc_ps", bufs=4))
 
         xs = [xpool.tile([P, 8, 16, 128], BF16, name="x%d" % a) for a in range(2)]
-        for a in range(2):
-            nc.vector.memset(xs[a][0:8, :, 0:4, :], 0.0)
-            nc.vector.memset(xs[a][96:128, :, 12:16, :], 0.0)
+        for a, eng in ((0, nc.vector), (1, nc.gpsimd)):
+            xz = xs[a][:].rearrange("p c r w -> p c (r w)").bitcast(U32)
+            eng.memset(xz[0:8, :, 0:256], 0)
+            eng.memset(xz[96:128, :, 768:1024], 0)
 
-        def load_centre(a):
-            for bl in range(8):
-                nc.sync.dma_start(
-                    out=xs[a][bl:128:8, :, 4:12, :],
-                    in_=x[8 * a + bl].rearrange("c (i r) w -> i c r w", r=8),
-                )
+        x_v = x.rearrange("(a b) c (i r) w -> a c i b (r w)", a=2, r=8)
+        x_off = x[:, :, 4:124, :].rearrange("(a b) c (i r) w -> a c i b (r w)", a=2, r=8)
+        x_edge = x.rearrange("(a b) c h w -> a b c (h w)", a=2)
+        xc = xpool.tile([P, 8, 8, 128], BF16, name="xc")
 
-        def load_halos(a):
-            for bl in range(8):
-                src = x[8 * a + bl]
-                nc.sync.dma_start(
-                    out=xs[a][8 + bl:128:8, :, 0:4, :],
-                    in_=src[:, 4:124, :].rearrange("c (i r) w -> i c r w", r=8)[:, :, 0:4, :],
-                )
-                nc.sync.dma_start(
-                    out=xs[a][bl:120:8, :, 12:16, :],
-                    in_=src[:, 8:128, :].rearrange("c (i r) w -> i c r w", r=8)[:, :, 0:4, :],
-                )
+        def load_own():
+            for c in range(8):
+                nc.sync.dma_start(out=xc[:, c].rearrange("p r w -> p (r w)"), in_=x_v[0, c])
 
-        load_centre(0)
+        def load_windows(a):
+            for c in range(8):
+                rows = xs[a][:, c].rearrange("p r w -> p (r w)")
+                nc.sync.dma_start(out=rows[8:128, 0:1024], in_=x_off[a, c])
+                nc.sync.dma_start(out=rows[0:120, 1024:2048], in_=x_off[a, c])
+            flat = xs[a][:].rearrange("p c r w -> p c (r w)")
+            nc.sync.dma_start(out=flat[0:8, :, 512:1024], in_=x_edge[a, :, :, 0:512])
+            nc.sync.dma_start(out=flat[120:128, :, 1024:1536], in_=x_edge[a, :, :, 124 * 128:128 * 128])
+
+        load_own()
 
         one = const.tile([P, 1], F32, name="one")
         nc.vector.memset(one[:], 1.0)
@@ -75,7 +75,7 @@ def tile_shiftedpatchtokenization_pa_t_kernel(tc, x, ln1_g, ln1_b, w1, b1, out):
         ident = const.tile([P, P], F32, name="ident")
         make_identity(nc, ident[:])
         perm = const.tile([P, P], F32, name="perm")
-        nc.vector.tensor_copy(
+        nc.gpsimd.tensor_copy(
             out=perm[:].rearrange("p (b i) -> p b i", b=8),
             in_=ident[:].rearrange("p (i b) -> p b i", b=8),
         )
@@ -83,17 +83,17 @@ def tile_shiftedpatchtokenization_pa_t_kernel(tc, x, ln1_g, ln1_b, w1, b1, out):
         l0 = const.tile([P, P], F32, name="l0")
         l1c = const.tile([P, P], F32, name="l1c")
         l0c = const.tile([P, P], F32, name="l0c")
-        nc.vector.tensor_copy(out=l1[:], in_=ident[:])
-        nc.vector.tensor_tensor(out=l1[:, 8:128], in0=l1[:, 8:128], in1=ident[:, 0:120], op=ALU.add)
-        nc.vector.tensor_copy(out=l0[:], in_=ident[:])
-        nc.vector.tensor_tensor(out=l0[:, 0:120], in0=l0[:, 0:120], in1=ident[:, 8:128], op=ALU.add)
-        nc.vector.tensor_tensor(out=l1c[:], in0=l1[:], in1=ident[:], op=ALU.add)
-        nc.vector.tensor_tensor(out=l0c[:], in0=l0[:], in1=ident[:], op=ALU.add)
+        nc.gpsimd.tensor_copy(out=l1[:], in_=ident[:])
+        nc.gpsimd.tensor_tensor(out=l1[:, 8:128], in0=l1[:, 8:128], in1=ident[:, 0:120], op=ALU.add)
+        nc.gpsimd.tensor_copy(out=l0[:], in_=ident[:])
+        nc.gpsimd.tensor_tensor(out=l0[:, 0:120], in0=l0[:, 0:120], in1=ident[:, 8:128], op=ALU.add)
+        nc.gpsimd.tensor_tensor(out=l1c[:], in0=l1[:], in1=ident[:], op=ALU.add)
+        nc.gpsimd.tensor_tensor(out=l0c[:], in0=l0[:], in1=ident[:], op=ALU.add)
         zt = const.tile([P, 8, 4, 8], BF16, name="zt")
-        nc.vector.memset(zt[:], 0.0)
+        nc.gpsimd.memset(zt[:], 0.0)
 
         gb_bf = const.tile([P, P], BF16, name="gb_bf")
-        nc.vector.memset(gb_bf[:], 0.0)
+        nc.gpsimd.memset(gb_bf[:], 0.0)
         nc.sync.dma_start(out=gb_bf[0:KT, :], in_=ln1_g.rearrange("(c p) -> c p", p=P))
         nc.sync.dma_start(out=gb_bf[32:32 + KT, :], in_=ln1_b.rearrange("(c p) -> c p", p=P))
         gb_f = const.tile([P, P], F32, name="gb_f")
@@ -103,11 +103,8 @@ def tile_shiftedpatchtokenization_pa_t_kernel(tc, x, ln1_g, ln1_b, w1, b1, out):
         gbt = const.tile([P, P], F32, name="gbt")
         nc.vector.tensor_copy(out=gbt[:], in_=gb_ps[:, 0:P])
 
+        load_windows(0)
         b_bf = const.tile([P, DIM], BF16, name="b_bf")
-        load_halos(0)
-        nc.sync.dma_start(out=b_bf[:], in_=b1.partition_broadcast(P))
-        bias = const.tile([P, DIM], F32, name="bias")
-        nc.vector.tensor_copy(out=bias[:], in_=b_bf[:])
 
         wc = const.tile([P, PASSES, DIM], U32, name="wc", align_bytes=64)
         ws = const.tile([P, PASSES, DIM], U8, name="ws", align_bytes=64)
@@ -121,16 +118,19 @@ def tile_shiftedpatchtokenization_pa_t_kernel(tc, x, ln1_g, ln1_b, w1, b1, out):
 
         for g in range(3):
             load_w(g)
-        load_centre(1)
-        load_halos(1)
+        nc.sync.dma_start(out=b_bf[:], in_=b1.partition_broadcast(P))
+        bias = const.tile([P, DIM], F32, name="bias")
+        nc.vector.tensor_copy(out=bias[:], in_=b_bf[:])
 
         def prep_w(g):
             raw = raws[g]
             wg = wgp.tile([P, DIM, 4], BF16, name="wg", align_bytes=64)
-            nc.vector.tensor_copy(
-                out=wg[:].rearrange("p (c i) t -> p c t i", i=4),
-                in_=raw[:].rearrange("p t (c i) -> p c t i", i=4),
-            )
+            dst = wg[:].rearrange("p (c i) t -> p c t i", i=4)
+            src = raw[:].rearrange("p t (c i) -> p c t i", i=4)
+            if g % 2 == 0:
+                nc.scalar.copy(out=dst, in_=src)
+            else:
+                nc.vector.tensor_copy(out=dst, in_=src)
             nc.vector.quantize_mx(
                 out=wc[:, g, :].bitcast(FP8X4),
                 scales=ws[:, g, :],
@@ -141,55 +141,60 @@ def tile_shiftedpatchtokenization_pa_t_kernel(tc, x, ln1_g, ln1_b, w1, b1, out):
         rstd = const.tile([P, 32], F32, name="rstd")
         nmr = const.tile([P, 32], F32, name="nmr")
 
-        def stats(a, s_lo, s_hi, j_lo, j_hi):
-            ns = s_hi - s_lo
-            nj = j_hi - j_lo
-            bs = stp.tile([P, 2, ns, 6], F32, name="bs_%d" % ns, tag="bs")
+        own = (xc, xs[1][:, :, 4:12, :])
+        bs = [const.tile([P, 2, 16, 6], F32, name="bs%d" % a) for a in range(2)]
+
+        def sums(a, j_lo, j_hi):
             for h in range(2):
-                for c in range(ns):
+                for j in range(j_lo, j_hi):
                     nc.vector.bn_stats(
-                        out=bs[:, h, c, :],
-                        in_=xs[a][:, :, 4 + 4 * h:8 + 4 * h, 4 * (s_lo + c):4 * (s_lo + c) + 4],
+                        out=bs[a][:, h, j, :],
+                        in_=own[a][:, :, 4 * h:4 * h + 4, 8 * j:8 * j + 8].rearrange(
+                            "p c r (e w) -> p c r w e", e=2
+                        ),
                     )
-            hh = stp.tile([P, 2, 2, ns], F32, name="hh_%d" % ns, tag="hh")
-            b2 = stp.tile([P, 2, ns], F32, name="b2_%d" % ns, tag="b2")
-            c2 = stp.tile([P, 2, ns], F32, name="c2_%d" % ns, tag="c2")
-            nc.vector.tensor_tensor(out=hh[:, 0], in0=bs[:, :, :, 1], in1=bs[:, :, :, 4], op=ALU.add)
-            nc.vector.tensor_tensor(out=b2[:], in0=bs[:, :, :, 1], in1=bs[:, :, :, 1], op=ALU.mult)
-            nc.vector.tensor_tensor(out=c2[:], in0=bs[:, :, :, 4], in1=bs[:, :, :, 4], op=ALU.mult)
-            nc.vector.tensor_tensor(out=b2[:], in0=b2[:], in1=c2[:], op=ALU.add)
-            nc.vector.tensor_tensor(out=c2[:], in0=bs[:, :, :, 2], in1=bs[:, :, :, 5], op=ALU.add)
+
+        def squares(a, j_lo, j_hi):
+            nj = j_hi - j_lo
+            v = bs[a][:, :, j_lo:j_hi, :].rearrange("p h j (e v) -> p h (j e) v", e=2)
+            sq = stp.tile([P, 2, 2 * nj], F32, name="sq_%d" % nj, tag="sq")
+            nc.vector.tensor_tensor(out=sq[:], in0=v[:, :, :, 1], in1=v[:, :, :, 1], op=ALU.mult)
             nc.vector.scalar_tensor_tensor(
-                out=hh[:, 1], in0=b2[:], scalar=64.0, in1=c2[:], op0=ALU.mult, op1=ALU.add
+                out=v[:, :, :, 2], in0=sq[:], scalar=128.0, in1=v[:, :, :, 2], op0=ALU.mult, op1=ALU.add
             )
+
+        def stats(a, j_lo, j_hi):
+            nj = j_hi - j_lo
+            bv = bs[a][:].rearrange("p h j (e v) -> p h j e v", e=2)
             st = acc_ps.tile([P, 512], F32, name="acc")
-            stv = st[:, 0:4 * ns].rearrange("p (v s c) -> p v s c", v=2, s=2)
-            nc.tensor.matmul(out=stv[:, 0], lhsT=l1[:], rhs=hh[:, :, 1, :], start=True, stop=False)
-            nc.tensor.matmul(out=stv[:, 0], lhsT=l0[:], rhs=hh[:, :, 0, :], start=False, stop=True)
-            nc.tensor.matmul(out=stv[:, 1], lhsT=l1c[:], rhs=hh[:, :, 1, :], start=True, stop=False)
-            nc.tensor.matmul(out=stv[:, 1], lhsT=l0c[:], rhs=hh[:, :, 0, :], start=False, stop=True)
-            m0 = j_lo - s_lo // 2
-            winc = stv[:, 1].rearrange("p s (m e) -> p s m e", e=2)
-            win = stv[:, 0].rearrange("p s (m e) -> p s m e", e=2)
-            sa = stp.tile([P, 2, nj], F32, name="sa_%d" % nj, tag="sa")
-            nc.vector.tensor_reduce(out=sa[:], in_=winc[:, :, m0:m0 + nj, :], op=ALU.add, axis=AX.X)
-            dl = 1 if m0 == 0 else 0
-            dr = 1 if m0 + nj == ns // 2 else 0
+            sv = st[:, 0:2 * nj].rearrange("p (j v) -> p j v", v=2)
+            pair = stp.tile([P, 2, nj, 2], F32, name="pair_%d" % nj, tag="pair")
+            near = stp.tile([P, 2, nj, 2], F32, name="near_%d" % nj, tag="near")
             nc.vector.tensor_tensor(
-                out=sa[:, :, dl:nj], in0=sa[:, :, dl:nj], in1=win[:, :, m0 + dl - 1:m0 + nj - 1, 1], op=ALU.add
+                out=pair[:], in0=bv[:, :, j_lo:j_hi, 0, 1:3], in1=bv[:, :, j_lo:j_hi, 1, 1:3], op=ALU.add
             )
+            left = max(j_lo, 1)
+            right = min(j_hi, 15)
             nc.vector.tensor_tensor(
-                out=sa[:, :, 0:nj - dr], in0=sa[:, :, 0:nj - dr], in1=win[:, :, m0 + 1:m0 + nj + 1 - dr, 0], op=ALU.add
+                out=near[:, :, left - j_lo:right - j_lo, :], in0=bv[:, :, left - 1:right - 1, 1, 1:3],
+                in1=bv[:, :, left + 1:right + 1, 0, 1:3], op=ALU.add,
             )
+            if j_lo == 0:
+                nc.vector.tensor_copy(out=near[:, :, 0, :], in_=bv[:, :, 1, 0, 1:3])
+            if j_hi == 16:
+                nc.vector.tensor_copy(out=near[:, :, nj - 1, :], in_=bv[:, :, 14, 1, 1:3])
+            terms = ((l1c, pair, 1), (l0c, pair, 0), (l1, near, 1), (l0, near, 0))
+            for n, (lhs, part, h) in enumerate(terms):
+                nc.tensor.matmul(out=sv, lhsT=lhs[:], rhs=part[:, h], start=(n == 0), stop=(n == 3))
             cols = slice(16 * a + j_lo, 16 * a + j_hi)
             nc.vector.tensor_scalar(
-                out=mean[:, cols], in0=sa[:, 0, :], scalar1=64.0 / PD, scalar2=None, op0=ALU.mult
+                out=mean[:, cols], in0=sv[:, :, 0], scalar1=128.0 / PD, scalar2=None, op0=ALU.mult
             )
             msq = stp.tile([P, nj], F32, name="msq_%d" % nj, tag="msq")
             nc.vector.tensor_tensor(out=msq[:], in0=mean[:, cols], in1=mean[:, cols], op=ALU.mult)
             ve = stp.tile([P, nj], F32, name="ve_%d" % nj, tag="ve")
             nc.vector.scalar_tensor_tensor(
-                out=ve[:], in0=sa[:, 1, :], scalar=1.0 / PD, in1=msq[:], op0=ALU.mult, op1=ALU.subtract
+                out=ve[:], in0=sv[:, :, 1], scalar=1.0 / PD, in1=msq[:], op0=ALU.mult, op1=ALU.subtract
             )
             nc.vector.tensor_scalar(out=ve[:], in0=ve[:], scalar1=EPS, scalar2=None, op0=ALU.add)
             sd = stp.tile([P, nj], F32, name="sd_%d" % nj, tag="sd")
@@ -197,10 +202,13 @@ def tile_shiftedpatchtokenization_pa_t_kernel(tc, x, ln1_g, ln1_b, w1, b1, out):
             r0 = stp.tile([P, nj], F32, name="r0_%d" % nj, tag="r0")
             nc.vector.reciprocal(out=r0[:], in_=sd[:])
             t0 = stp.tile([P, nj], F32, name="t0_%d" % nj, tag="t0")
-            nc.vector.tensor_tensor(out=t0[:], in0=r0[:], in1=r0[:], op=ALU.mult)
+            nc.vector.scalar_tensor_tensor(
+                out=t0[:], in0=r0[:], scalar=-0.5, in1=r0[:], op0=ALU.mult, op1=ALU.mult
+            )
             nc.vector.tensor_tensor(out=t0[:], in0=t0[:], in1=ve[:], op=ALU.mult)
-            nc.vector.tensor_scalar(out=t0[:], in0=t0[:], scalar1=-0.5, scalar2=1.5, op0=ALU.mult, op1=ALU.add)
-            nc.vector.tensor_tensor(out=rstd[:, cols], in0=r0[:], in1=t0[:], op=ALU.mult)
+            nc.vector.scalar_tensor_tensor(
+                out=rstd[:, cols], in0=t0[:], scalar=1.5, in1=r0[:], op0=ALU.add, op1=ALU.mult
+            )
             nc.vector.scalar_tensor_tensor(
                 out=nmr[:, cols], in0=mean[:, cols], scalar=-1.0, in1=rstd[:, cols], op0=ALU.mult, op1=ALU.mult
             )
@@ -212,38 +220,46 @@ def tile_shiftedpatchtokenization_pa_t_kernel(tc, x, ln1_g, ln1_b, w1, b1, out):
         grouped_of = {}
         accs = {}
 
-        def norm(gi, s):
+        def affine(on_act, dst, src, col):
+            if on_act:
+                nc.scalar.activation(
+                    out=dst, in_=src, func=ACTF.Identity,
+                    scale=rstd[:, col:col + 1], bias=nmr[:, col:col + 1],
+                )
+            else:
+                nc.vector.tensor_scalar(
+                    out=dst, in0=src, scalar1=mean[:, col:col + 1], scalar2=rstd[:, col:col + 1],
+                    op0=ALU.subtract, op1=ALU.mult,
+                )
+
+        def norm(gi, tau):
             a = gi // 4
-            for tau in range(4):
-                j = 4 * (gi % 4) + tau
-                col = 16 * a + j
-                if s == 0:
-                    ntiles[(gi, tau)] = npool.tile([P, PD], F32, name="nt")
-                nv = ntiles[(gi, tau)][:].rearrange("p (h w s c) -> p h w s c", h=8, w=8, s=5)
-                r0 = 4 + SHIFTS[s][0]
-                c0 = 8 * j + SHIFTS[s][1]
+            j = 4 * (gi % 4) + tau
+            col = 16 * a + j
+            nt = npool.tile([P, PD], F32, name="nt")
+            ntiles[(gi, tau)] = nt
+            nv = nt[:].rearrange("p (h w s c) -> p h w s c", h=8, w=8, s=5)
+            for cq in range(2):
+                affine(
+                    tau in CENTRE_ON_ACT, nv[:, :, :, 0, 4 * cq:4 * cq + 4],
+                    xs[a][:, 4 * cq:4 * cq + 4, 4:12, 8 * j:8 * j + 8].rearrange("p c h w -> p h w c"), col,
+                )
+            for dx in range(2):
+                c0 = 8 * j - 4 + 8 * dx
                 lo = max(0, -c0)
                 hi = min(8, 128 - c0)
-                pieces = [
-                    (nv[:, :, lo:hi, s, 4 * cq:4 * cq + 4],
-                     xs[a][:, 4 * cq:4 * cq + 4, r0:r0 + 8, c0 + lo:c0 + hi].rearrange("p c h w -> p h w c"))
-                    for cq in range(2)
-                ]
-                if lo > 0:
-                    pieces.append((nv[:, :, 0:lo, s, :], zt[:]))
-                if hi < 8:
-                    pieces.append((nv[:, :, hi:8, s, :], zt[:]))
-                for dst, src in pieces:
-                    if s in T_ON_ACT or (gi == 0 and s == 1):
-                        nc.scalar.activation(
-                            out=dst, in_=src, func=ACTF.Identity,
-                            scale=rstd[:, col:col + 1], bias=nmr[:, col:col + 1],
-                        )
+                for cq in range(2):
+                    src = xs[a][:, 4 * cq:4 * cq + 4, :, c0 + lo:c0 + hi].rearrange("p c (d h) w -> p d h w c", d=2)
+                    dst = nv[:, :, lo:hi, 1 + dx:5:2, 4 * cq:4 * cq + 4].rearrange("p h w d c -> p d h w c")
+                    if hi - lo == 8:
+                        affine(dx == 0, dst, src, col)
                     else:
-                        nc.vector.tensor_scalar(
-                            out=dst, in0=src, scalar1=mean[:, col:col + 1], scalar2=rstd[:, col:col + 1],
-                            op0=ALU.subtract, op1=ALU.mult,
-                        )
+                        for d in range(2):
+                            affine(dx == 0, dst[:, d], src[:, d], col)
+                if lo > 0 or hi < 8:
+                    pad = slice(0, lo) if lo > 0 else slice(hi, 8)
+                    for d in range(2):
+                        affine(dx == 0, nv[:, :, pad, 1 + 2 * d + dx, :], zt[:], col)
 
         def hop(gi, g):
             planes = ppool.tile([P, 4, 512], BF16, name="planes")
@@ -267,10 +283,7 @@ def tile_shiftedpatchtokenization_pa_t_kernel(tc, x, ln1_g, ln1_b, w1, b1, out):
             grouped_of[(gi, g)] = grouped
             dst = grouped[:].rearrange("p (c i) t -> p c t i", i=4)
             src = planes_of[(gi, g)][:].rearrange("p t (c i) -> p c t i", i=4)
-            if g in R_ON_ACT:
-                nc.scalar.copy(out=dst, in_=src)
-            else:
-                nc.vector.tensor_copy(out=dst, in_=src)
+            nc.vector.tensor_copy(out=dst, in_=src)
 
         def quant(gi, g):
             zc = zpool.tile([P, 512], U32, name="zc", align_bytes=64)
@@ -303,23 +316,31 @@ def tile_shiftedpatchtokenization_pa_t_kernel(tc, x, ln1_g, ln1_b, w1, b1, out):
 
         NG = 8
         NS = NG * PASSES
-        stats(0, 0, 10, 0, 4)
-        for s in range(5):
-            norm(0, s)
+        sums(0, 0, 5)
+        squares(0, 0, 5)
+        stats(0, 0, 4)
+        for tau in range(4):
+            norm(0, tau)
         for g in range(PASSES):
             if g >= 3:
                 load_w(g)
             prep_w(g)
-        stats(0, 6, 32, 4, 16)
+        load_windows(1)
+        sums(0, 5, 16)
+        squares(0, 5, 16)
+        stats(0, 4, 16)
         for sl in range(NS + LAG_M + 1):
-            if sl == 5:
-                stats(1, 0, 32, 0, 16)
+            if 3 <= sl < 11:
+                sums(1, 2 * (sl - 3), 2 * (sl - 3) + 2)
+            if sl == 11:
+                squares(1, 0, 16)
+                stats(1, 0, 16)
             if sl < NS:
                 hop(sl // 5, sl % 5)
             if sl - LAG_M >= 0 and sl - LAG_M < NS:
                 mx((sl - LAG_M) // 5, (sl - LAG_M) % 5)
-            if sl + 5 < NS:
-                norm(sl // 5 + 1, sl % 5)
+            if sl + 5 < NS and sl % 5 in NORM_STEP:
+                norm(sl // 5 + 1, NORM_STEP[sl % 5])
             if sl - LAG_R >= 0 and sl - LAG_R < NS:
                 regroup((sl - LAG_R) // 5, (sl - LAG_R) % 5)
             if sl - LAG_Q >= 0 and sl - LAG_Q < NS:

@@ -10,7 +10,6 @@ U32 = mybir.dt.uint32
 U8 = mybir.dt.uint8
 ALU = mybir.AluOpType
 ACTF = mybir.ActivationFunctionType
-AX = mybir.AxisListType
 
 P = 128
 PD = 2560
@@ -18,9 +17,9 @@ DIM = 512
 KT = PD // P
 PASSES = 5
 EPS = 1e-5
-CENTRE_ON_ACT = (1, 3)
 FLOPS = 2 * 4096 * PD * DIM
-NORM_STEP = {0: 0, 1: 1, 2: 2, 4: 3}
+NG = 8
+NS = NG * PASSES
 LAG_R = 1
 LAG_Q = 2
 LAG_M = 3
@@ -29,322 +28,364 @@ LAG_M = 3
 def tile_shiftedpatchtokenization_pa_t_kernel(tc, x, ln1_g, ln1_b, w1, b1, out):
     nc = tc.nc
     with ExitStack() as ctx:
-        ctx.enter_context(tc.manual_schedule(engines={mybir.EngineType.SP}))
+        ctx.enter_context(tc.manual_schedule())
         const = ctx.enter_context(tc.tile_pool(name="const", bufs=1))
         xpool = ctx.enter_context(tc.tile_pool(name="xpool", bufs=1))
-        wst = ctx.enter_context(tc.tile_pool(name="wst", bufs=3))
-        wgp = ctx.enter_context(tc.tile_pool(name="wgp", bufs=1))
-        stp = ctx.enter_context(tc.tile_pool(name="stp", bufs=1))
+        wst = ctx.enter_context(tc.tile_pool(name="wst", bufs=4))
+        wgp = ctx.enter_context(tc.tile_pool(name="wgp", bufs=2))
         npool = ctx.enter_context(tc.tile_pool(name="npool", bufs=8))
         ppool = ctx.enter_context(tc.tile_pool(name="ppool", bufs=3))
         gpool = ctx.enter_context(tc.tile_pool(name="gpool", bufs=2))
-        zpool = ctx.enter_context(tc.tile_pool(name="zpool", bufs=5))
-        rpool = ctx.enter_context(tc.tile_pool(name="rpool", bufs=3))
         hop_ps = ctx.enter_context(tc.psum_pool(name="hop_ps", bufs=4))
         acc_ps = ctx.enter_context(tc.psum_pool(name="acc_ps", bufs=4))
 
         xs = [xpool.tile([P, 8, 16, 128], BF16, name="x%d" % a) for a in range(2)]
-        for a, eng in ((0, nc.vector), (1, nc.gpsimd)):
-            xz = xs[a][:].rearrange("p c r w -> p c (r w)").bitcast(U32)
-            eng.memset(xz[0:8, :, 0:256], 0)
-            eng.memset(xz[96:128, :, 768:1024], 0)
-
         x_v = x.rearrange("(a b) c (i r) w -> a c i b (r w)", a=2, r=8)
-        x_off = x[:, :, 4:124, :].rearrange("(a b) c (i r) w -> a c i b (r w)", a=2, r=8)
-        x_edge = x.rearrange("(a b) c h w -> a b c (h w)", a=2)
-        xc = xpool.tile([P, 8, 8, 128], BF16, name="xc")
 
-        def load_own():
+        def clear_edges(a):
             for c in range(8):
-                nc.sync.dma_start(out=xc[:, c].rearrange("p r w -> p (r w)"), in_=x_v[0, c])
+                xz = xs[a][:, c].rearrange("p r w -> p (r w)").bitcast(U32)
+                nc.gpsimd.memset(xz[0:8, 0:256], 0)
+                nc.gpsimd.memset(xz[96:128, 768:1024], 0)
 
         def load_windows(a):
             for c in range(8):
                 rows = xs[a][:, c].rearrange("p r w -> p (r w)")
-                nc.sync.dma_start(out=rows[8:128, 0:1024], in_=x_off[a, c])
-                nc.sync.dma_start(out=rows[0:120, 1024:2048], in_=x_off[a, c])
-            flat = xs[a][:].rearrange("p c r w -> p c (r w)")
-            nc.sync.dma_start(out=flat[0:8, :, 512:1024], in_=x_edge[a, :, :, 0:512])
-            nc.sync.dma_start(out=flat[120:128, :, 1024:1536], in_=x_edge[a, :, :, 124 * 128:128 * 128])
+                nc.sync.dma_start(out=rows[:, 512:1536], in_=x_v[a, c])
+                nc.sync.dma_start(out=rows[8:128, 0:512], in_=x_v[a, c, 0:15, :, 512:1024])
+                nc.sync.dma_start(out=rows[0:120, 1536:2048], in_=x_v[a, c, 1:16, :, 0:512])
 
-        load_own()
+        with tc.tile_pool(name="xcpool", bufs=1) as xcpool:
+            xc = xcpool.tile([P, 8, 8, 128], BF16, name="xc")
+            for c in range(8):
+                nc.sync.dma_start(out=xc[:, c].rearrange("p r w -> p (r w)"), in_=x_v[0, c])
 
-        one = const.tile([P, 1], F32, name="one")
-        nc.vector.memset(one[:], 1.0)
-        nc.scalar.activation(out=one[:], in_=one[:], func=ACTF.Sqrt)
-        ident = const.tile([P, P], F32, name="ident")
-        make_identity(nc, ident[:])
-        perm = const.tile([P, P], F32, name="perm")
-        nc.gpsimd.tensor_copy(
-            out=perm[:].rearrange("p (b i) -> p b i", b=8),
-            in_=ident[:].rearrange("p (i b) -> p b i", b=8),
-        )
-        l1 = const.tile([P, P], F32, name="l1")
-        l0 = const.tile([P, P], F32, name="l0")
-        l1c = const.tile([P, P], F32, name="l1c")
-        l0c = const.tile([P, P], F32, name="l0c")
-        nc.gpsimd.tensor_copy(out=l1[:], in_=ident[:])
-        nc.gpsimd.tensor_tensor(out=l1[:, 8:128], in0=l1[:, 8:128], in1=ident[:, 0:120], op=ALU.add)
-        nc.gpsimd.tensor_copy(out=l0[:], in_=ident[:])
-        nc.gpsimd.tensor_tensor(out=l0[:, 0:120], in0=l0[:, 0:120], in1=ident[:, 8:128], op=ALU.add)
-        nc.gpsimd.tensor_tensor(out=l1c[:], in0=l1[:], in1=ident[:], op=ALU.add)
-        nc.gpsimd.tensor_tensor(out=l0c[:], in0=l0[:], in1=ident[:], op=ALU.add)
-        zt = const.tile([P, 8, 4, 8], BF16, name="zt")
-        nc.gpsimd.memset(zt[:], 0.0)
+            wc = const.tile([P, PASSES, DIM], U32, name="wc", align_bytes=64)
+            ws = const.tile([P, PASSES, DIM], U8, name="ws", align_bytes=64)
+            w_v = w1.rearrange("(g t p) n -> g p t n", t=4, p=P)
+            raws = []
+            wgs = []
 
-        gb_bf = const.tile([P, P], BF16, name="gb_bf")
-        nc.gpsimd.memset(gb_bf[:], 0.0)
-        nc.sync.dma_start(out=gb_bf[0:KT, :], in_=ln1_g.rearrange("(c p) -> c p", p=P))
-        nc.sync.dma_start(out=gb_bf[32:32 + KT, :], in_=ln1_b.rearrange("(c p) -> c p", p=P))
-        gb_f = const.tile([P, P], F32, name="gb_f")
-        nc.vector.tensor_copy(out=gb_f[:], in_=gb_bf[:])
-        gb_ps = acc_ps.tile([P, 512], F32, name="acc")
-        nc.tensor.transpose(out=gb_ps[:, 0:P], in_=gb_f[:], identity=ident[:])
-        gbt = const.tile([P, P], F32, name="gbt")
-        nc.vector.tensor_copy(out=gbt[:], in_=gb_ps[:, 0:P])
+            def load_w(g):
+                raw = wst.tile([P, 4, DIM], BF16, name="raw")
+                nc.sync.dma_start(out=raw[:], in_=w_v[g])
+                raws.append(raw)
 
-        load_windows(0)
-        b_bf = const.tile([P, DIM], BF16, name="b_bf")
+            def regroup_w(g, on_act):
+                wg = wgp.tile([P, DIM, 4], BF16, name="wg", align_bytes=64)
+                dst = wg[:].rearrange("p (c i) t -> p c t i", i=4)
+                src = raws[g][:].rearrange("p t (c i) -> p c t i", i=4)
+                if on_act:
+                    nc.scalar.copy(out=dst, in_=src)
+                else:
+                    nc.vector.tensor_copy(out=dst, in_=src)
+                wgs.append(wg)
 
-        wc = const.tile([P, PASSES, DIM], U32, name="wc", align_bytes=64)
-        ws = const.tile([P, PASSES, DIM], U8, name="ws", align_bytes=64)
-        w_v = w1.rearrange("(g t p) n -> g p t n", t=4, p=P)
-        raws = []
+            def quant_w(g):
+                nc.vector.quantize_mx(
+                    out=wc[:, g, :].bitcast(FP8X4), scales=ws[:, g, :], in_=wgs[g][:].rearrange("p w t -> p (w t)"),
+                )
 
-        def load_w(g):
-            raw = wst.tile([P, 4, DIM], BF16, name="raw")
-            nc.sync.dma_start(out=raw[:], in_=w_v[g])
-            raws.append(raw)
-
-        for g in range(3):
-            load_w(g)
-        nc.sync.dma_start(out=b_bf[:], in_=b1.partition_broadcast(P))
-        bias = const.tile([P, DIM], F32, name="bias")
-        nc.vector.tensor_copy(out=bias[:], in_=b_bf[:])
-
-        def prep_w(g):
-            raw = raws[g]
-            wg = wgp.tile([P, DIM, 4], BF16, name="wg", align_bytes=64)
-            dst = wg[:].rearrange("p (c i) t -> p c t i", i=4)
-            src = raw[:].rearrange("p t (c i) -> p c t i", i=4)
-            if g % 2 == 0:
-                nc.scalar.copy(out=dst, in_=src)
-            else:
-                nc.vector.tensor_copy(out=dst, in_=src)
-            nc.vector.quantize_mx(
-                out=wc[:, g, :].bitcast(FP8X4),
-                scales=ws[:, g, :],
-                in_=wg[:].rearrange("p w t -> p (w t)"),
+            one = const.tile([P, 1], F32, name="one")
+            nc.vector.memset(one[:], 1.0)
+            nc.scalar.activation(out=one[:], in_=one[:], func=ACTF.Sqrt)
+            gb_bf = const.tile([P, P], BF16, name="gb_bf")
+            nc.gpsimd.memset(gb_bf[:], 0.0)
+            nc.sync.dma_start(out=gb_bf[0:KT, :], in_=ln1_g.rearrange("(c p) -> c p", p=P))
+            nc.sync.dma_start(out=gb_bf[32:32 + KT, :], in_=ln1_b.rearrange("(c p) -> c p", p=P))
+            clear_edges(0)
+            ident = const.tile([P, P], F32, name="ident")
+            make_identity(nc, ident[:])
+            l1 = const.tile([P, P], F32, name="l1")
+            l0 = const.tile([P, P], F32, name="l0")
+            l1c = const.tile([P, P], F32, name="l1c")
+            l0c = const.tile([P, P], F32, name="l0c")
+            nc.gpsimd.tensor_copy(out=l1[:], in_=ident[:])
+            nc.gpsimd.tensor_tensor(out=l1[:, 8:128], in0=l1[:, 8:128], in1=ident[:, 0:120], op=ALU.add)
+            nc.gpsimd.tensor_copy(out=l0[:], in_=ident[:])
+            nc.gpsimd.tensor_tensor(out=l0[:, 0:120], in0=l0[:, 0:120], in1=ident[:, 8:128], op=ALU.add)
+            nc.gpsimd.tensor_tensor(out=l1c[:], in0=l1[:], in1=ident[:], op=ALU.add)
+            nc.gpsimd.tensor_tensor(out=l0c[:], in0=l0[:], in1=ident[:], op=ALU.add)
+            perm = const.tile([P, P], F32, name="perm")
+            nc.gpsimd.tensor_copy(
+                out=perm[:].rearrange("p (b i) -> p b i", b=8),
+                in_=ident[:].rearrange("p (i b) -> p b i", b=8),
             )
+            zt = const.tile([P, 8, 4, 8], BF16, name="zt")
+            nc.gpsimd.memset(zt[:], 0.0)
+            clear_edges(1)
 
-        mean = const.tile([P, 32], F32, name="mean")
-        rstd = const.tile([P, 32], F32, name="rstd")
-        nmr = const.tile([P, 32], F32, name="nmr")
+            gb_f = const.tile([P, P], F32, name="gb_f")
+            gbt = const.tile([P, P], F32, name="gbt")
+            b_bf = const.tile([P, DIM], BF16, name="b_bf")
+            bias = const.tile([P, DIM], F32, name="bias")
+            load_windows(0)
+            for g in range(3):
+                load_w(g)
+            nc.sync.dma_start(out=b_bf[:], in_=b1.partition_broadcast(P))
+            load_windows(1)
 
-        own = (xc, xs[1][:, :, 4:12, :])
-        bs = [const.tile([P, 2, 16, 6], F32, name="bs%d" % a) for a in range(2)]
+            mean = const.tile([P, 32], F32, name="mean")
+            rstd = const.tile([P, 32], F32, name="rstd")
+            nmr = const.tile([P, 32], F32, name="nmr")
+            own = (xc, xs[1][:, :, 4:12, :])
+            bs = [const.tile([P, 2, 16, 6], F32, name="bs%d" % a) for a in range(2)]
+            sq = const.tile([P, 2, 2, 32], F32, name="sq")
+            pair = const.tile([P, 2, 2, 16, 2], F32, name="pair")
+            near = const.tile([P, 2, 2, 16, 2], F32, name="near")
+            msq = const.tile([P, 32], F32, name="msq")
+            ve = const.tile([P, 32], F32, name="ve")
+            sd = const.tile([P, 32], F32, name="sd")
+            r0 = const.tile([P, 32], F32, name="r0")
+            t0 = const.tile([P, 32], F32, name="t0")
 
-        def sums(a, j_lo, j_hi):
-            for h in range(2):
-                for j in range(j_lo, j_hi):
+            def sums(a, j):
+                def one_row(h):
                     nc.vector.bn_stats(
                         out=bs[a][:, h, j, :],
-                        in_=own[a][:, :, 4 * h:4 * h + 4, 8 * j:8 * j + 8].rearrange(
-                            "p c r (e w) -> p c r w e", e=2
-                        ),
+                        in_=own[a][:, :, 4 * h:4 * h + 4, 8 * j:8 * j + 8].rearrange("p c r (e w) -> p c r w e", e=2),
+                    )
+                return [lambda: one_row(0), lambda: one_row(1)]
+
+            def many_sums(a, j_lo, j_hi):
+                return [call for j in range(j_lo, j_hi) for call in sums(a, j)]
+
+            def stats(a, j_lo, j_hi, s_lo, s_hi):
+                nj = j_hi - j_lo
+                new = bs[a][:, :, s_lo:s_hi, :].rearrange("p h j (e v) -> p h (j e) v", e=2)
+                sqv = sq[:, a, :, 2 * s_lo:2 * s_hi]
+                bv = bs[a][:].rearrange("p h j (e v) -> p h j e v", e=2)
+                pv = pair[:, a, :, j_lo:j_hi, :]
+                nv = near[:, a, :, :, :]
+                left = max(j_lo, 1)
+                right = min(j_hi, 15)
+                cols = slice(16 * a + j_lo, 16 * a + j_hi)
+                psum = {}
+
+                def near_inner():
+                    nc.vector.tensor_tensor(
+                        out=nv[:, :, left:right, :], in0=bv[:, :, left - 1:right - 1, 1, 1:3],
+                        in1=bv[:, :, left + 1:right + 1, 0, 1:3], op=ALU.add,
+                    )
+                    if j_lo == 0:
+                        nc.vector.tensor_copy(out=nv[:, :, 0, :], in_=bv[:, :, 1, 0, 1:3])
+                    if j_hi == 16:
+                        nc.vector.tensor_copy(out=nv[:, :, 15, :], in_=bv[:, :, 14, 1, 1:3])
+
+                def windows():
+                    st = hop_ps.tile([P, 512], F32, name="bank")
+                    sv = st[:, 0:2 * nj].rearrange("p (j v) -> p j v", v=2)
+                    terms = ((l1c, pair, 1), (l0c, pair, 0), (l1, near, 1), (l0, near, 0))
+                    for n, (lhs, part, h) in enumerate(terms):
+                        nc.tensor.matmul(
+                            out=sv, lhsT=lhs[:], rhs=part[:, a, h, j_lo:j_hi, :], start=(n == 0), stop=(n == 3),
+                        )
+                    psum["sv"] = sv
+
+                return [
+                    lambda: nc.vector.tensor_tensor(out=sqv, in0=new[:, :, :, 1], in1=new[:, :, :, 1], op=ALU.mult),
+                    lambda: nc.vector.scalar_tensor_tensor(
+                        out=new[:, :, :, 2], in0=sqv, scalar=128.0, in1=new[:, :, :, 2], op0=ALU.mult, op1=ALU.add
+                    ),
+                    lambda: nc.vector.tensor_tensor(
+                        out=pv, in0=bv[:, :, j_lo:j_hi, 0, 1:3], in1=bv[:, :, j_lo:j_hi, 1, 1:3], op=ALU.add
+                    ),
+                    near_inner,
+                    windows,
+                    lambda: nc.vector.tensor_scalar(
+                        out=mean[:, cols], in0=psum["sv"][:, :, 0], scalar1=128.0 / PD, scalar2=None, op0=ALU.mult
+                    ),
+                    lambda: nc.vector.tensor_tensor(out=msq[:, cols], in0=mean[:, cols], in1=mean[:, cols], op=ALU.mult),
+                    lambda: nc.vector.scalar_tensor_tensor(
+                        out=ve[:, cols], in0=psum["sv"][:, :, 1], scalar=1.0 / PD, in1=msq[:, cols],
+                        op0=ALU.mult, op1=ALU.subtract,
+                    ),
+                    lambda: nc.vector.tensor_scalar(
+                        out=ve[:, cols], in0=ve[:, cols], scalar1=EPS, scalar2=None, op0=ALU.add
+                    ),
+                    lambda: nc.scalar.activation(out=sd[:, cols], in_=ve[:, cols], func=ACTF.Sqrt),
+                    lambda: nc.vector.reciprocal(out=r0[:, cols], in_=sd[:, cols]),
+                    lambda: nc.vector.scalar_tensor_tensor(
+                        out=t0[:, cols], in0=r0[:, cols], scalar=-0.5, in1=r0[:, cols], op0=ALU.mult, op1=ALU.mult
+                    ),
+                    lambda: nc.vector.tensor_tensor(out=t0[:, cols], in0=t0[:, cols], in1=ve[:, cols], op=ALU.mult),
+                    lambda: nc.vector.scalar_tensor_tensor(
+                        out=rstd[:, cols], in0=t0[:, cols], scalar=1.5, in1=r0[:, cols], op0=ALU.add, op1=ALU.mult
+                    ),
+                    lambda: nc.vector.scalar_tensor_tensor(
+                        out=nmr[:, cols], in0=mean[:, cols], scalar=-1.0, in1=rstd[:, cols], op0=ALU.mult, op1=ALU.mult
+                    ),
+                ]
+
+            out_v = out.flatten_outer_dims().rearrange("(a n j) d -> a j n d", a=2, j=16)
+            ntiles = {}
+            ztiles = {}
+            planes_of = {}
+            grouped_of = {}
+            accs = {}
+
+            def affine(on_act, dst, src, col):
+                if on_act:
+                    nc.scalar.activation(
+                        out=dst, in_=src, func=ACTF.Identity,
+                        scale=rstd[:, col:col + 1], bias=nmr[:, col:col + 1],
+                    )
+                else:
+                    nc.vector.tensor_scalar(
+                        out=dst, in0=src, scalar1=mean[:, col:col + 1], scalar2=rstd[:, col:col + 1],
+                        op0=ALU.subtract, op1=ALU.mult,
                     )
 
-        def squares(a, j_lo, j_hi):
-            nj = j_hi - j_lo
-            v = bs[a][:, :, j_lo:j_hi, :].rearrange("p h j (e v) -> p h (j e) v", e=2)
-            sq = stp.tile([P, 2, 2 * nj], F32, name="sq_%d" % nj, tag="sq")
-            nc.vector.tensor_tensor(out=sq[:], in0=v[:, :, :, 1], in1=v[:, :, :, 1], op=ALU.mult)
-            nc.vector.scalar_tensor_tensor(
-                out=v[:, :, :, 2], in0=sq[:], scalar=128.0, in1=v[:, :, :, 2], op0=ALU.mult, op1=ALU.add
-            )
-
-        def stats(a, j_lo, j_hi):
-            nj = j_hi - j_lo
-            bv = bs[a][:].rearrange("p h j (e v) -> p h j e v", e=2)
-            st = acc_ps.tile([P, 512], F32, name="acc")
-            sv = st[:, 0:2 * nj].rearrange("p (j v) -> p j v", v=2)
-            pair = stp.tile([P, 2, nj, 2], F32, name="pair_%d" % nj, tag="pair")
-            near = stp.tile([P, 2, nj, 2], F32, name="near_%d" % nj, tag="near")
-            nc.vector.tensor_tensor(
-                out=pair[:], in0=bv[:, :, j_lo:j_hi, 0, 1:3], in1=bv[:, :, j_lo:j_hi, 1, 1:3], op=ALU.add
-            )
-            left = max(j_lo, 1)
-            right = min(j_hi, 15)
-            nc.vector.tensor_tensor(
-                out=near[:, :, left - j_lo:right - j_lo, :], in0=bv[:, :, left - 1:right - 1, 1, 1:3],
-                in1=bv[:, :, left + 1:right + 1, 0, 1:3], op=ALU.add,
-            )
-            if j_lo == 0:
-                nc.vector.tensor_copy(out=near[:, :, 0, :], in_=bv[:, :, 1, 0, 1:3])
-            if j_hi == 16:
-                nc.vector.tensor_copy(out=near[:, :, nj - 1, :], in_=bv[:, :, 14, 1, 1:3])
-            terms = ((l1c, pair, 1), (l0c, pair, 0), (l1, near, 1), (l0, near, 0))
-            for n, (lhs, part, h) in enumerate(terms):
-                nc.tensor.matmul(out=sv, lhsT=lhs[:], rhs=part[:, h], start=(n == 0), stop=(n == 3))
-            cols = slice(16 * a + j_lo, 16 * a + j_hi)
-            nc.vector.tensor_scalar(
-                out=mean[:, cols], in0=sv[:, :, 0], scalar1=128.0 / PD, scalar2=None, op0=ALU.mult
-            )
-            msq = stp.tile([P, nj], F32, name="msq_%d" % nj, tag="msq")
-            nc.vector.tensor_tensor(out=msq[:], in0=mean[:, cols], in1=mean[:, cols], op=ALU.mult)
-            ve = stp.tile([P, nj], F32, name="ve_%d" % nj, tag="ve")
-            nc.vector.scalar_tensor_tensor(
-                out=ve[:], in0=sv[:, :, 1], scalar=1.0 / PD, in1=msq[:], op0=ALU.mult, op1=ALU.subtract
-            )
-            nc.vector.tensor_scalar(out=ve[:], in0=ve[:], scalar1=EPS, scalar2=None, op0=ALU.add)
-            sd = stp.tile([P, nj], F32, name="sd_%d" % nj, tag="sd")
-            nc.scalar.activation(out=sd[:], in_=ve[:], func=ACTF.Sqrt)
-            r0 = stp.tile([P, nj], F32, name="r0_%d" % nj, tag="r0")
-            nc.vector.reciprocal(out=r0[:], in_=sd[:])
-            t0 = stp.tile([P, nj], F32, name="t0_%d" % nj, tag="t0")
-            nc.vector.scalar_tensor_tensor(
-                out=t0[:], in0=r0[:], scalar=-0.5, in1=r0[:], op0=ALU.mult, op1=ALU.mult
-            )
-            nc.vector.tensor_tensor(out=t0[:], in0=t0[:], in1=ve[:], op=ALU.mult)
-            nc.vector.scalar_tensor_tensor(
-                out=rstd[:, cols], in0=t0[:], scalar=1.5, in1=r0[:], op0=ALU.add, op1=ALU.mult
-            )
-            nc.vector.scalar_tensor_tensor(
-                out=nmr[:, cols], in0=mean[:, cols], scalar=-1.0, in1=rstd[:, cols], op0=ALU.mult, op1=ALU.mult
-            )
-
-        out_v = out.flatten_outer_dims().rearrange("(a n j) d -> a j n d", a=2, j=16)
-        ntiles = {}
-        ztiles = {}
-        planes_of = {}
-        grouped_of = {}
-        accs = {}
-
-        def affine(on_act, dst, src, col):
-            if on_act:
-                nc.scalar.activation(
-                    out=dst, in_=src, func=ACTF.Identity,
-                    scale=rstd[:, col:col + 1], bias=nmr[:, col:col + 1],
-                )
-            else:
-                nc.vector.tensor_scalar(
-                    out=dst, in0=src, scalar1=mean[:, col:col + 1], scalar2=rstd[:, col:col + 1],
-                    op0=ALU.subtract, op1=ALU.mult,
-                )
-
-        def norm(gi, tau):
-            a = gi // 4
-            j = 4 * (gi % 4) + tau
-            col = 16 * a + j
-            nt = npool.tile([P, PD], F32, name="nt")
-            ntiles[(gi, tau)] = nt
-            nv = nt[:].rearrange("p (h w s c) -> p h w s c", h=8, w=8, s=5)
-            for cq in range(2):
-                affine(
-                    tau in CENTRE_ON_ACT, nv[:, :, :, 0, 4 * cq:4 * cq + 4],
-                    xs[a][:, 4 * cq:4 * cq + 4, 4:12, 8 * j:8 * j + 8].rearrange("p c h w -> p h w c"), col,
-                )
-            for dx in range(2):
-                c0 = 8 * j - 4 + 8 * dx
-                lo = max(0, -c0)
-                hi = min(8, 128 - c0)
-                for cq in range(2):
-                    src = xs[a][:, 4 * cq:4 * cq + 4, :, c0 + lo:c0 + hi].rearrange("p c (d h) w -> p d h w c", d=2)
-                    dst = nv[:, :, lo:hi, 1 + dx:5:2, 4 * cq:4 * cq + 4].rearrange("p h w d c -> p d h w c")
-                    if hi - lo == 8:
-                        affine(dx == 0, dst, src, col)
-                    else:
+            def norm(gi, tau):
+                a = gi // 4
+                j = 4 * (gi % 4) + tau
+                col = 16 * a + j
+                ntiles[(gi, tau)] = npool.tile([P, PD], F32, name="nt")
+                nv = ntiles[(gi, tau)][:].rearrange("p (h w s c) -> p h w s c", h=8, w=8, s=5)
+                for dx in range(2):
+                    c0 = 8 * j - 4 + 8 * dx
+                    lo = max(0, -c0)
+                    hi = min(8, 128 - c0)
+                    for cq in range(2):
+                        src = xs[a][:, 4 * cq:4 * cq + 4, :, c0 + lo:c0 + hi].rearrange("p c (d h) w -> p d h w c", d=2)
+                        dst = nv[:, :, lo:hi, 1 + dx:5:2, 4 * cq:4 * cq + 4].rearrange("p h w d c -> p d h w c")
+                        if hi - lo == 8:
+                            affine(dx == 0, dst, src, col)
+                        else:
+                            for d in range(2):
+                                affine(dx == 0, dst[:, d], src[:, d], col)
+                    if lo > 0 or hi < 8:
+                        pad = slice(0, lo) if lo > 0 else slice(hi, 8)
                         for d in range(2):
-                            affine(dx == 0, dst[:, d], src[:, d], col)
-                if lo > 0 or hi < 8:
-                    pad = slice(0, lo) if lo > 0 else slice(hi, 8)
-                    for d in range(2):
-                        affine(dx == 0, nv[:, :, pad, 1 + 2 * d + dx, :], zt[:], col)
-
-        def hop(gi, g):
-            planes = ppool.tile([P, 4, 512], BF16, name="planes")
-            planes_of[(gi, g)] = planes
-            for t in range(4):
-                kt = 4 * g + t
-                bank = hop_ps.tile([P, 512], F32, name="bank")
-                for tau in range(4):
-                    nc.tensor.transpose(
-                        out=bank[:, tau * P:(tau + 1) * P],
-                        in_=ntiles[(gi, tau)][:, kt * P:(kt + 1) * P],
-                        identity=perm[:],
+                            affine(dx == 0, nv[:, :, pad, 1 + 2 * d + dx, :], zt[:], col)
+                for cq in range(2):
+                    affine(
+                        1 <= gi <= 3, nv[:, :, :, 0, 4 * cq:4 * cq + 4],
+                        xs[a][:, 4 * cq:4 * cq + 4, 4:12, 8 * j:8 * j + 8].rearrange("p c h w -> p h w c"), col,
                     )
-                nc.scalar.activation(
-                    out=planes[:, t, :], in_=bank[:], func=ACTF.Identity,
-                    scale=gbt[:, kt:kt + 1], bias=gbt[:, 32 + kt:33 + kt],
+
+            def hop(gi, g, half):
+                if half == 0:
+                    planes_of[(gi, g)] = ppool.tile([P, 4, 512], BF16, name="planes")
+                planes = planes_of[(gi, g)]
+                for t in range(2 * half, 2 * half + 2):
+                    kt = 4 * g + t
+                    bank = hop_ps.tile([P, 512], F32, name="bank")
+                    for tau in range(4):
+                        nc.tensor.transpose(
+                            out=bank[:, tau * P:(tau + 1) * P],
+                            in_=ntiles[(gi, tau)][:, kt * P:(kt + 1) * P],
+                            identity=perm[:],
+                        )
+                    nc.scalar.activation(
+                        out=planes[:, t, :], in_=bank[:], func=ACTF.Identity,
+                        scale=gbt[:, kt:kt + 1], bias=gbt[:, 32 + kt:33 + kt],
+                    )
+
+            def regroup(gi, g):
+                grouped = gpool.tile([P, 512, 4], BF16, name="grouped", align_bytes=64)
+                grouped_of[(gi, g)] = grouped
+                dst = grouped[:].rearrange("p (c i) t -> p c t i", i=4)
+                src = planes_of[(gi, g)][:].rearrange("p t (c i) -> p c t i", i=4)
+                nc.vector.tensor_copy(out=dst, in_=src)
+
+            def quant(gi, g):
+                zc = zpool.tile([P, 512], U32, name="zc", align_bytes=64)
+                zs = zpool.tile([P, 512], U8, name="zs", align_bytes=64)
+                ztiles[(gi, g)] = (zc, zs)
+                nc.vector.quantize_mx(
+                    out=zc[:].bitcast(FP8X4), scales=zs[:],
+                    in_=grouped_of[(gi, g)][:].rearrange("p w t -> p (w t)"),
                 )
 
-        def regroup(gi, g):
-            grouped = gpool.tile([P, 512, 4], BF16, name="grouped", align_bytes=64)
-            grouped_of[(gi, g)] = grouped
-            dst = grouped[:].rearrange("p (c i) t -> p c t i", i=4)
-            src = planes_of[(gi, g)][:].rearrange("p t (c i) -> p c t i", i=4)
-            nc.vector.tensor_copy(out=dst, in_=src)
+            def mx(gi, g, half):
+                zc, zs = ztiles[(gi, g)]
+                for tau in range(2 * half, 2 * half + 2):
+                    if g == 0:
+                        accs[(gi, tau)] = acc_ps.tile([P, DIM], F32, name="acc")
+                    nc.tensor.matmul_mx(
+                        out=accs[(gi, tau)][:],
+                        lhsT=zc[:, tau * P:(tau + 1) * P].bitcast(FP8X4),
+                        lhsT_scale=zs[:, tau * P:(tau + 1) * P],
+                        rhs=wc[:, g, :].bitcast(FP8X4),
+                        rhs_scale=ws[:, g, :],
+                        start=(g == 0),
+                        stop=(g == PASSES - 1),
+                    )
 
-        def quant(gi, g):
-            zc = zpool.tile([P, 512], U32, name="zc", align_bytes=64)
-            zs = zpool.tile([P, 512], U8, name="zs", align_bytes=64)
-            ztiles[(gi, g)] = (zc, zs)
-            nc.vector.quantize_mx(
-                out=zc[:].bitcast(FP8X4), scales=zs[:],
-                in_=grouped_of[(gi, g)][:].rearrange("p w t -> p (w t)"),
-            )
+            def finish(gi, tau):
+                res = rpool.tile([P, DIM], F32, name="res")
+                nc.vector.tensor_tensor(out=res[:], in0=accs[(gi, tau)][:], in1=bias[:], op=ALU.add)
+                nc.sync.dma_start(out=out_v[gi // 4, 4 * (gi % 4) + tau], in_=res[:])
 
-        def mx(gi, g):
-            zc, zs = ztiles[(gi, g)]
+            rest = many_sums(0, 5, 16)
+            for call in many_sums(0, 0, 5):
+                call()
+            first = stats(0, 0, 4, 0, 5)
+            for call in first[0:5]:
+                call()
+            nc.vector.tensor_copy(out=gb_f[:], in_=gb_bf[:])
+            gb_ps = hop_ps.tile([P, 512], F32, name="bank")
+            nc.tensor.transpose(out=gb_ps[:, 0:P], in_=gb_f[:], identity=ident[:])
+            for n in range(4):
+                rest[n]()
+            first[5]()
+            first[6]()
+            first[7]()
+            first[8]()
+            first[9]()
+            nc.vector.tensor_copy(out=gbt[:], in_=gb_ps[:, 0:P])
+            rest[4]()
+            for call in first[10:]:
+                call()
             for tau in range(4):
-                if g == 0:
-                    accs[(gi, tau)] = acc_ps.tile([P, DIM], F32, name="acc")
-                nc.tensor.matmul_mx(
-                    out=accs[(gi, tau)][:],
-                    lhsT=zc[:, tau * P:(tau + 1) * P].bitcast(FP8X4),
-                    lhsT_scale=zs[:, tau * P:(tau + 1) * P],
-                    rhs=wc[:, g, :].bitcast(FP8X4),
-                    rhs_scale=ws[:, g, :],
-                    start=(g == 0),
-                    stop=(g == PASSES - 1),
-                )
+                norm(0, tau)
+            for n in range(5, 22):
+                rest[n]()
+        zpool = ctx.enter_context(tc.tile_pool(name="zpool", bufs=5))
+        rpool = ctx.enter_context(tc.tile_pool(name="rpool", bufs=4))
 
-        def finish(gi, tau):
-            res = rpool.tile([P, DIM], F32, name="res")
-            nc.vector.tensor_tensor(out=res[:], in0=accs[(gi, tau)][:], in1=bias[:], op=ALU.add)
-            nc.sync.dma_start(out=out_v[gi // 4, 4 * (gi % 4) + tau], in_=res[:])
-
-        NG = 8
-        NS = NG * PASSES
-        sums(0, 0, 5)
-        squares(0, 0, 5)
-        stats(0, 0, 4)
-        for tau in range(4):
-            norm(0, tau)
-        for g in range(PASSES):
-            if g >= 3:
-                load_w(g)
-            prep_w(g)
-        load_windows(1)
-        sums(0, 5, 16)
-        squares(0, 5, 16)
-        stats(0, 4, 16)
+        fill = {}
+        for n in range(8):
+            fill[5 + n] = many_sums(1, 2 * n, 2 * n + 2)
+        chains = {3: stats(0, 4, 16, 5, 16), 13: stats(1, 0, 16, 0, 16)}
         for sl in range(NS + LAG_M + 1):
-            if 3 <= sl < 11:
-                sums(1, 2 * (sl - 3), 2 * (sl - 3) + 2)
-            if sl == 11:
-                squares(1, 0, 16)
-                stats(1, 0, 16)
-            if sl < NS:
-                hop(sl // 5, sl % 5)
-            if sl - LAG_M >= 0 and sl - LAG_M < NS:
-                mx((sl - LAG_M) // 5, (sl - LAG_M) % 5)
-            if sl + 5 < NS and sl % 5 in NORM_STEP:
-                norm(sl // 5 + 1, NORM_STEP[sl % 5])
-            if sl - LAG_R >= 0 and sl - LAG_R < NS:
-                regroup((sl - LAG_R) // 5, (sl - LAG_R) % 5)
-            if sl - LAG_Q >= 0 and sl - LAG_Q < NS:
-                quant((sl - LAG_Q) // 5, (sl - LAG_Q) % 5)
+            for half in range(2):
+                if sl < NS:
+                    hop(sl // 5, sl % 5, half)
+                if 0 <= sl - LAG_M < NS:
+                    mx((sl - LAG_M) // 5, (sl - LAG_M) % 5, half)
             if sl - LAG_M - 1 >= 0 and (sl - LAG_M - 1) % 5 == 4:
                 for tau in range(4):
                     finish((sl - LAG_M - 1) // 5, tau)
+            if sl == 0:
+                nc.vector.tensor_copy(out=bias[:], in_=b_bf[:])
+            if sl < PASSES:
+                if sl == 1:
+                    load_w(3)
+                elif sl == 2:
+                    load_w(4)
+                regroup_w(sl, sl < 4)
+                if sl > 0:
+                    quant_w(sl - 1)
+            elif sl == PASSES:
+                quant_w(PASSES - 1)
+            if 0 <= sl - LAG_Q < NS:
+                quant((sl - LAG_Q) // 5, (sl - LAG_Q) % 5)
+            for call in fill.get(sl, []):
+                call()
+            for call in chains.get(sl, []):
+                call()
+            if sl == 3:
+                norm(1, 0)
+                norm(1, 1)
+            elif sl == 4:
+                norm(1, 2)
+                norm(1, 3)
+            elif sl == 5:
+                norm(2, 0)
+                norm(2, 1)
+            elif 5 < sl < 34 and sl % 5 != 3:
+                norm((sl + 1) // 5 + 1, (sl + 1) % 5)
+            if 0 <= sl - LAG_R < NS:
+                regroup((sl - LAG_R) // 5, (sl - LAG_R) % 5)

@@ -31,8 +31,8 @@ def tile_shiftedpatchtokenization_pa_t_kernel(tc, x, ln1_g, ln1_b, w1, b1, out):
         ctx.enter_context(tc.manual_schedule())
         const = ctx.enter_context(tc.tile_pool(name="const", bufs=1))
         xpool = ctx.enter_context(tc.tile_pool(name="xpool", bufs=1))
-        wst = ctx.enter_context(tc.tile_pool(name="wst", bufs=4))
-        wgp = ctx.enter_context(tc.tile_pool(name="wgp", bufs=2))
+        wst = ctx.enter_context(tc.tile_pool(name="wst", bufs=3))
+        wgp = ctx.enter_context(tc.tile_pool(name="wgp", bufs=3))
         npool = ctx.enter_context(tc.tile_pool(name="npool", bufs=8))
         ppool = ctx.enter_context(tc.tile_pool(name="ppool", bufs=3))
         gpool = ctx.enter_context(tc.tile_pool(name="gpool", bufs=2))
@@ -48,10 +48,9 @@ def tile_shiftedpatchtokenization_pa_t_kernel(tc, x, ln1_g, ln1_b, w1, b1, out):
                 nc.gpsimd.memset(xz[0:8, 0:256], 0)
                 nc.gpsimd.memset(xz[96:128, 768:1024], 0)
 
-        def load_windows(a):
+        def load_halos(a):
             for c in range(8):
                 rows = xs[a][:, c].rearrange("p r w -> p (r w)")
-                nc.sync.dma_start(out=rows[:, 512:1536], in_=x_v[a, c])
                 nc.sync.dma_start(out=rows[8:128, 0:512], in_=x_v[a, c, 0:15, :, 512:1024])
                 nc.sync.dma_start(out=rows[0:120, 1536:2048], in_=x_v[a, c, 1:16, :, 0:512])
 
@@ -111,19 +110,25 @@ def tile_shiftedpatchtokenization_pa_t_kernel(tc, x, ln1_g, ln1_b, w1, b1, out):
                 out=perm[:].rearrange("p (b i) -> p b i", b=8),
                 in_=ident[:].rearrange("p (i b) -> p b i", b=8),
             )
+            gb_f = const.tile([P, P], F32, name="gb_f")
+            nc.gpsimd.tensor_copy(out=gb_f[:], in_=gb_bf[:])
             zt = const.tile([P, 8, 4, 8], BF16, name="zt")
             nc.gpsimd.memset(zt[:], 0.0)
             clear_edges(1)
 
-            gb_f = const.tile([P, P], F32, name="gb_f")
             gbt = const.tile([P, P], F32, name="gbt")
             b_bf = const.tile([P, DIM], BF16, name="b_bf")
             bias = const.tile([P, DIM], F32, name="bias")
-            load_windows(0)
+            load_halos(0)
             for g in range(3):
                 load_w(g)
             nc.sync.dma_start(out=b_bf[:], in_=b1.partition_broadcast(P))
-            load_windows(1)
+            nc.gpsimd.tensor_copy(out=bias[:], in_=b_bf[:])
+            for c in range(8):
+                nc.sync.dma_start(out=xs[1][:, c, 4:12, :].rearrange("p r w -> p (r w)"), in_=x_v[1, c])
+            load_halos(1)
+            for c in range(6):
+                nc.scalar.copy(out=xs[0][:, c, 4:12, :], in_=xc[:, c])
 
             mean = const.tile([P, 32], F32, name="mean")
             rstd = const.tile([P, 32], F32, name="rstd")
@@ -264,23 +269,22 @@ def tile_shiftedpatchtokenization_pa_t_kernel(tc, x, ln1_g, ln1_b, w1, b1, out):
                         xs[a][:, 4 * cq:4 * cq + 4, 4:12, 8 * j:8 * j + 8].rearrange("p c h w -> p h w c"), col,
                     )
 
-            def hop(gi, g, half):
-                if half == 0:
+            def hop(gi, g, t):
+                if t == 0:
                     planes_of[(gi, g)] = ppool.tile([P, 4, 512], BF16, name="planes")
                 planes = planes_of[(gi, g)]
-                for t in range(2 * half, 2 * half + 2):
-                    kt = 4 * g + t
-                    bank = hop_ps.tile([P, 512], F32, name="bank")
-                    for tau in range(4):
-                        nc.tensor.transpose(
-                            out=bank[:, tau * P:(tau + 1) * P],
-                            in_=ntiles[(gi, tau)][:, kt * P:(kt + 1) * P],
-                            identity=perm[:],
-                        )
-                    nc.scalar.activation(
-                        out=planes[:, t, :], in_=bank[:], func=ACTF.Identity,
-                        scale=gbt[:, kt:kt + 1], bias=gbt[:, 32 + kt:33 + kt],
+                kt = 4 * g + t
+                bank = hop_ps.tile([P, 512], F32, name="bank")
+                for tau in range(4):
+                    nc.tensor.transpose(
+                        out=bank[:, tau * P:(tau + 1) * P],
+                        in_=ntiles[(gi, tau)][:, kt * P:(kt + 1) * P],
+                        identity=perm[:],
                     )
+                nc.scalar.activation(
+                    out=planes[:, t, :], in_=bank[:], func=ACTF.Identity,
+                    scale=gbt[:, kt:kt + 1], bias=gbt[:, 32 + kt:33 + kt],
+                )
 
             def regroup(gi, g):
                 grouped = gpool.tile([P, 512, 4], BF16, name="grouped", align_bytes=64)
@@ -298,20 +302,19 @@ def tile_shiftedpatchtokenization_pa_t_kernel(tc, x, ln1_g, ln1_b, w1, b1, out):
                     in_=grouped_of[(gi, g)][:].rearrange("p w t -> p (w t)"),
                 )
 
-            def mx(gi, g, half):
+            def mx(gi, g, tau):
                 zc, zs = ztiles[(gi, g)]
-                for tau in range(2 * half, 2 * half + 2):
-                    if g == 0:
-                        accs[(gi, tau)] = acc_ps.tile([P, DIM], F32, name="acc")
-                    nc.tensor.matmul_mx(
-                        out=accs[(gi, tau)][:],
-                        lhsT=zc[:, tau * P:(tau + 1) * P].bitcast(FP8X4),
-                        lhsT_scale=zs[:, tau * P:(tau + 1) * P],
-                        rhs=wc[:, g, :].bitcast(FP8X4),
-                        rhs_scale=ws[:, g, :],
-                        start=(g == 0),
-                        stop=(g == PASSES - 1),
-                    )
+                if g == 0:
+                    accs[(gi, tau)] = acc_ps.tile([P, DIM], F32, name="acc")
+                nc.tensor.matmul_mx(
+                    out=accs[(gi, tau)][:],
+                    lhsT=zc[:, tau * P:(tau + 1) * P].bitcast(FP8X4),
+                    lhsT_scale=zs[:, tau * P:(tau + 1) * P],
+                    rhs=wc[:, g, :].bitcast(FP8X4),
+                    rhs_scale=ws[:, g, :],
+                    start=(g == 0),
+                    stop=(g == PASSES - 1),
+                )
 
             def finish(gi, tau):
                 res = rpool.tile([P, DIM], F32, name="res")
@@ -324,23 +327,21 @@ def tile_shiftedpatchtokenization_pa_t_kernel(tc, x, ln1_g, ln1_b, w1, b1, out):
             first = stats(0, 0, 4, 0, 5)
             for call in first[0:5]:
                 call()
-            nc.vector.tensor_copy(out=gb_f[:], in_=gb_bf[:])
             gb_ps = hop_ps.tile([P, 512], F32, name="bank")
             nc.tensor.transpose(out=gb_ps[:, 0:P], in_=gb_f[:], identity=ident[:])
-            for n in range(4):
+            for c in range(6, 8):
+                nc.vector.tensor_copy(out=xs[0][:, c, 4:12, :], in_=xc[:, c])
+            for n in range(2):
                 rest[n]()
-            first[5]()
-            first[6]()
-            first[7]()
-            first[8]()
-            first[9]()
-            nc.vector.tensor_copy(out=gbt[:], in_=gb_ps[:, 0:P])
-            rest[4]()
+            for call in first[5:10]:
+                call()
+            rest[2]()
+            nc.scalar.copy(out=gbt[:], in_=gb_ps[:, 0:P])
             for call in first[10:]:
                 call()
             for tau in range(4):
                 norm(0, tau)
-            for n in range(5, 22):
+            for n in range(3, 22):
                 rest[n]()
         zpool = ctx.enter_context(tc.tile_pool(name="zpool", bufs=5))
         rpool = ctx.enter_context(tc.tile_pool(name="rpool", bufs=4))
@@ -348,33 +349,32 @@ def tile_shiftedpatchtokenization_pa_t_kernel(tc, x, ln1_g, ln1_b, w1, b1, out):
         fill = {}
         for n in range(8):
             fill[5 + n] = many_sums(1, 2 * n, 2 * n + 2)
-        chains = {3: stats(0, 4, 16, 5, 16), 13: stats(1, 0, 16, 0, 16)}
+        chains = {2: stats(0, 4, 16, 5, 16), 12: stats(1, 0, 16, 0, 16)}
         for sl in range(NS + LAG_M + 1):
-            for half in range(2):
+            for t in range(4):
                 if sl < NS:
-                    hop(sl // 5, sl % 5, half)
+                    hop(sl // 5, sl % 5, t)
                 if 0 <= sl - LAG_M < NS:
-                    mx((sl - LAG_M) // 5, (sl - LAG_M) % 5, half)
+                    mx((sl - LAG_M) // 5, (sl - LAG_M) % 5, t)
             if sl - LAG_M - 1 >= 0 and (sl - LAG_M - 1) % 5 == 4:
                 for tau in range(4):
                     finish((sl - LAG_M - 1) // 5, tau)
-            if sl == 0:
-                nc.vector.tensor_copy(out=bias[:], in_=b_bf[:])
+            chain = chains.get(sl - 1, [])
+            for call in chain[5:10]:
+                call()
             if sl < PASSES:
-                if sl == 1:
-                    load_w(3)
-                elif sl == 2:
-                    load_w(4)
+                if 1 <= sl <= 2:
+                    load_w(sl + 2)
                 regroup_w(sl, sl < 4)
-                if sl > 0:
-                    quant_w(sl - 1)
-            elif sl == PASSES:
-                quant_w(PASSES - 1)
+            if 2 <= sl < PASSES + 2:
+                quant_w(sl - 2)
             if 0 <= sl - LAG_Q < NS:
                 quant((sl - LAG_Q) // 5, (sl - LAG_Q) % 5)
             for call in fill.get(sl, []):
                 call()
-            for call in chains.get(sl, []):
+            if chain:
+                regroup((sl - LAG_R) // 5, (sl - LAG_R) % 5)
+            for call in chain[10:]:
                 call()
             if sl == 3:
                 norm(1, 0)
@@ -387,5 +387,7 @@ def tile_shiftedpatchtokenization_pa_t_kernel(tc, x, ln1_g, ln1_b, w1, b1, out):
                 norm(2, 1)
             elif 5 < sl < 34 and sl % 5 != 3:
                 norm((sl + 1) // 5 + 1, (sl + 1) % 5)
-            if 0 <= sl - LAG_R < NS:
+            for call in chains.get(sl, [])[0:5]:
+                call()
+            if 0 <= sl - LAG_R < NS and not chain:
                 regroup((sl - LAG_R) // 5, (sl - LAG_R) % 5)

@@ -20,6 +20,7 @@ EPS = 1e-5
 FLOPS = 2 * 4096 * PD * DIM
 NG = 8
 NS = NG * PASSES
+IDLE_COLS = 384
 LAG_R = 1
 LAG_Q = 2
 LAG_M = 3
@@ -275,6 +276,11 @@ def tile_shiftedpatchtokenization_pa_t_kernel(tc, x, ln1_g, ln1_b, w1, b1, out):
                 planes = planes_of[(gi, g)]
                 kt = 4 * g + t
                 bank = hop_ps.tile([P, 512], F32, name="bank")
+                if t % 2 == 0:
+                    nc.tensor.matmul(
+                        out=bank[:, 0:IDLE_COLS], lhsT=xs[0][:, 0, 4, :],
+                        rhs=xs[0][:, 0, 5:8, :].rearrange("p r w -> p (r w)"), start=True, stop=True,
+                    )
                 for tau in range(4):
                     nc.tensor.transpose(
                         out=bank[:, tau * P:(tau + 1) * P],
@@ -354,7 +360,8 @@ def tile_shiftedpatchtokenization_pa_t_kernel(tc, x, ln1_g, ln1_b, w1, b1, out):
             for t in range(4):
                 if sl < NS:
                     hop(sl // 5, sl % 5, t)
-                if 0 <= sl - LAG_M < NS:
+                if t % 2 == 1 and 0 <= sl - LAG_M < NS:
+                    mx((sl - LAG_M) // 5, (sl - LAG_M) % 5, t - 1)
                     mx((sl - LAG_M) // 5, (sl - LAG_M) % 5, t)
             if sl - LAG_M - 1 >= 0 and (sl - LAG_M - 1) % 5 == 4:
                 for tau in range(4):

@@ -20,7 +20,6 @@ EPS = 1e-5
 FLOPS = 2 * 4096 * PD * DIM
 NG = 8
 NS = NG * PASSES
-IDLE_COLS = 384
 LAG_R = 1
 LAG_Q = 2
 LAG_M = 3
@@ -135,8 +134,10 @@ def tile_shiftedpatchtokenization_pa_t_kernel(tc, x, ln1_g, ln1_b, w1, b1, out):
             rstd = const.tile([P, 32], F32, name="rstd")
             nmr = const.tile([P, 32], F32, name="nmr")
             own = (xc, xs[1][:, :, 4:12, :])
-            bs = [const.tile([P, 2, 16, 6], F32, name="bs%d" % a) for a in range(2)]
+            bs = [const.tile([P, 2, 32, 6], F32, name="bs%d" % a) for a in range(2)]
+            hh = [const.tile([P, 2, 32, 2], F32, name="hh%d" % a) for a in range(2)]
             sq = const.tile([P, 2, 2, 32], F32, name="sq")
+            s2 = const.tile([P, 2, 2, 32], F32, name="s2")
             pair = const.tile([P, 2, 2, 16, 2], F32, name="pair")
             near = const.tile([P, 2, 2, 16, 2], F32, name="near")
             msq = const.tile([P, 32], F32, name="msq")
@@ -146,21 +147,23 @@ def tile_shiftedpatchtokenization_pa_t_kernel(tc, x, ln1_g, ln1_b, w1, b1, out):
             t0 = const.tile([P, 32], F32, name="t0")
 
             def sums(a, j):
-                def one_row(h):
+                def one_block(h, s):
                     nc.vector.bn_stats(
-                        out=bs[a][:, h, j, :],
-                        in_=own[a][:, :, 4 * h:4 * h + 4, 8 * j:8 * j + 8].rearrange("p c r (e w) -> p c r w e", e=2),
+                        out=bs[a][:, h, s, :], in_=own[a][:, :, 4 * h:4 * h + 4, 4 * s:4 * s + 4],
                     )
-                return [lambda: one_row(0), lambda: one_row(1)]
+                return [lambda h=h, s=s: one_block(h, s) for h in range(2) for s in (2 * j, 2 * j + 1)]
 
             def many_sums(a, j_lo, j_hi):
                 return [call for j in range(j_lo, j_hi) for call in sums(a, j)]
 
             def stats(a, j_lo, j_hi, s_lo, s_hi):
                 nj = j_hi - j_lo
-                new = bs[a][:, :, s_lo:s_hi, :].rearrange("p h j (e v) -> p h (j e) v", e=2)
-                sqv = sq[:, a, :, 2 * s_lo:2 * s_hi]
-                bv = bs[a][:].rearrange("p h j (e v) -> p h j e v", e=2)
+                fresh = slice(2 * s_lo, 2 * s_hi)
+                new = bs[a][:, :, fresh, :]
+                sums_of = hh[a][:, :, fresh, :]
+                sqv = sq[:, a, :, fresh]
+                s2v = s2[:, a, :, fresh]
+                bv = hh[a][:].rearrange("p h (j e) v -> p h j e v", e=2)
                 pv = pair[:, a, :, j_lo:j_hi, :]
                 nv = near[:, a, :, :, :]
                 left = max(j_lo, 1)
@@ -168,15 +171,28 @@ def tile_shiftedpatchtokenization_pa_t_kernel(tc, x, ln1_g, ln1_b, w1, b1, out):
                 cols = slice(16 * a + j_lo, 16 * a + j_hi)
                 psum = {}
 
+                def squares():
+                    nc.vector.tensor_tensor(out=sqv, in0=new[:, :, :, 1], in1=new[:, :, :, 1], op=ALU.mult)
+                    nc.vector.tensor_tensor(out=s2v, in0=new[:, :, :, 4], in1=new[:, :, :, 4], op=ALU.mult)
+                    nc.vector.tensor_tensor(
+                        out=sums_of[:, :, :, 0], in0=new[:, :, :, 1], in1=new[:, :, :, 4], op=ALU.add
+                    )
+                    nc.vector.scalar_tensor_tensor(
+                        out=sqv, in0=sqv, scalar=64.0, in1=new[:, :, :, 2], op0=ALU.mult, op1=ALU.add
+                    )
+                    nc.vector.scalar_tensor_tensor(
+                        out=sums_of[:, :, :, 1], in0=s2v, scalar=64.0, in1=new[:, :, :, 5], op0=ALU.mult, op1=ALU.add
+                    )
+
                 def near_inner():
                     nc.vector.tensor_tensor(
-                        out=nv[:, :, left:right, :], in0=bv[:, :, left - 1:right - 1, 1, 1:3],
-                        in1=bv[:, :, left + 1:right + 1, 0, 1:3], op=ALU.add,
+                        out=nv[:, :, left:right, :], in0=bv[:, :, left - 1:right - 1, 1, :],
+                        in1=bv[:, :, left + 1:right + 1, 0, :], op=ALU.add,
                     )
                     if j_lo == 0:
-                        nc.vector.tensor_copy(out=nv[:, :, 0, :], in_=bv[:, :, 1, 0, 1:3])
+                        nc.vector.tensor_copy(out=nv[:, :, 0, :], in_=bv[:, :, 1, 0, :])
                     if j_hi == 16:
-                        nc.vector.tensor_copy(out=nv[:, :, 15, :], in_=bv[:, :, 14, 1, 1:3])
+                        nc.vector.tensor_copy(out=nv[:, :, 15, :], in_=bv[:, :, 14, 1, :])
 
                 def windows():
                     st = hop_ps.tile([P, 512], F32, name="bank")
@@ -189,17 +205,17 @@ def tile_shiftedpatchtokenization_pa_t_kernel(tc, x, ln1_g, ln1_b, w1, b1, out):
                     psum["sv"] = sv
 
                 return [
-                    lambda: nc.vector.tensor_tensor(out=sqv, in0=new[:, :, :, 1], in1=new[:, :, :, 1], op=ALU.mult),
-                    lambda: nc.vector.scalar_tensor_tensor(
-                        out=new[:, :, :, 2], in0=sqv, scalar=128.0, in1=new[:, :, :, 2], op0=ALU.mult, op1=ALU.add
+                    squares,
+                    lambda: nc.vector.tensor_tensor(
+                        out=sums_of[:, :, :, 1], in0=sums_of[:, :, :, 1], in1=sqv, op=ALU.add
                     ),
                     lambda: nc.vector.tensor_tensor(
-                        out=pv, in0=bv[:, :, j_lo:j_hi, 0, 1:3], in1=bv[:, :, j_lo:j_hi, 1, 1:3], op=ALU.add
+                        out=pv, in0=bv[:, :, j_lo:j_hi, 0, :], in1=bv[:, :, j_lo:j_hi, 1, :], op=ALU.add
                     ),
                     near_inner,
                     windows,
                     lambda: nc.vector.tensor_scalar(
-                        out=mean[:, cols], in0=psum["sv"][:, :, 0], scalar1=128.0 / PD, scalar2=None, op0=ALU.mult
+                        out=mean[:, cols], in0=psum["sv"][:, :, 0], scalar1=64.0 / PD, scalar2=None, op0=ALU.mult
                     ),
                     lambda: nc.vector.tensor_tensor(out=msq[:, cols], in0=mean[:, cols], in1=mean[:, cols], op=ALU.mult),
                     lambda: nc.vector.scalar_tensor_tensor(
@@ -276,11 +292,6 @@ def tile_shiftedpatchtokenization_pa_t_kernel(tc, x, ln1_g, ln1_b, w1, b1, out):
                 planes = planes_of[(gi, g)]
                 kt = 4 * g + t
                 bank = hop_ps.tile([P, 512], F32, name="bank")
-                if t % 2 == 0:
-                    nc.tensor.matmul(
-                        out=bank[:, 0:IDLE_COLS], lhsT=xs[0][:, 0, 4, :],
-                        rhs=xs[0][:, 0, 5:8, :].rearrange("p r w -> p (r w)"), start=True, stop=True,
-                    )
                 for tau in range(4):
                     nc.tensor.transpose(
                         out=bank[:, tau * P:(tau + 1) * P],
@@ -337,18 +348,19 @@ def tile_shiftedpatchtokenization_pa_t_kernel(tc, x, ln1_g, ln1_b, w1, b1, out):
             nc.tensor.transpose(out=gb_ps[:, 0:P], in_=gb_f[:], identity=ident[:])
             for c in range(6, 8):
                 nc.vector.tensor_copy(out=xs[0][:, c, 4:12, :], in_=xc[:, c])
-            for n in range(2):
+            for n in range(4):
                 rest[n]()
             for call in first[5:10]:
                 call()
-            rest[2]()
+            rest[4]()
+            rest[5]()
             nc.scalar.copy(out=gbt[:], in_=gb_ps[:, 0:P])
             for call in first[10:]:
                 call()
             for tau in range(4):
                 norm(0, tau)
-            for n in range(3, 22):
-                rest[n]()
+            for call in rest[6:]:
+                call()
         zpool = ctx.enter_context(tc.tile_pool(name="zpool", bufs=5))
         rpool = ctx.enter_context(tc.tile_pool(name="rpool", bufs=4))
 

@@ -124,9 +124,6 @@ def tile_shiftedpatchtokenization_pa_t_kernel(tc, x, ln1_g, ln1_b, w1, b1, out):
                 load_w(g)
             nc.sync.dma_start(out=b_bf[:], in_=b1.partition_broadcast(P))
             nc.gpsimd.tensor_copy(out=bias[:], in_=b_bf[:])
-            for c in range(8):
-                nc.sync.dma_start(out=xs[1][:, c, 4:12, :].rearrange("p r w -> p (r w)"), in_=x_v[1, c])
-            load_halos(1)
             for c in range(6):
                 nc.scalar.copy(out=xs[0][:, c, 4:12, :], in_=xc[:, c])
 
@@ -258,6 +255,11 @@ def tile_shiftedpatchtokenization_pa_t_kernel(tc, x, ln1_g, ln1_b, w1, b1, out):
                         op0=ALU.subtract, op1=ALU.mult,
                     )
 
+            def on_act(gi, tau, part):
+                if part == 0:
+                    return gi < 4 or tau < 3
+                return part == 2 and 2 <= gi <= 3
+
             def norm(gi, tau):
                 a = gi // 4
                 j = 4 * (gi % 4) + tau
@@ -272,17 +274,17 @@ def tile_shiftedpatchtokenization_pa_t_kernel(tc, x, ln1_g, ln1_b, w1, b1, out):
                         src = xs[a][:, 4 * cq:4 * cq + 4, :, c0 + lo:c0 + hi].rearrange("p c (d h) w -> p d h w c", d=2)
                         dst = nv[:, :, lo:hi, 1 + dx:5:2, 4 * cq:4 * cq + 4].rearrange("p h w d c -> p d h w c")
                         if hi - lo == 8:
-                            affine(dx == 0, dst, src, col)
+                            affine(on_act(gi, tau, dx), dst, src, col)
                         else:
                             for d in range(2):
-                                affine(dx == 0, dst[:, d], src[:, d], col)
+                                affine(on_act(gi, tau, dx), dst[:, d], src[:, d], col)
                     if lo > 0 or hi < 8:
                         pad = slice(0, lo) if lo > 0 else slice(hi, 8)
                         for d in range(2):
-                            affine(dx == 0, nv[:, :, pad, 1 + 2 * d + dx, :], zt[:], col)
+                            affine(on_act(gi, tau, dx), nv[:, :, pad, 1 + 2 * d + dx, :], zt[:], col)
                 for cq in range(2):
                     affine(
-                        1 <= gi <= 3, nv[:, :, :, 0, 4 * cq:4 * cq + 4],
+                        on_act(gi, tau, 2), nv[:, :, :, 0, 4 * cq:4 * cq + 4],
                         xs[a][:, 4 * cq:4 * cq + 4, 4:12, 8 * j:8 * j + 8].rearrange("p c h w -> p h w c"), col,
                     )
 
@@ -384,14 +386,17 @@ def tile_shiftedpatchtokenization_pa_t_kernel(tc, x, ln1_g, ln1_b, w1, b1, out):
             if sl < PASSES:
                 if 1 <= sl <= 2:
                     load_w(sl + 2)
-                regroup_w(sl, sl < 4)
+                if sl == 2:
+                    for c in range(8):
+                        nc.sync.dma_start(out=xs[1][:, c, 4:12, :].rearrange("p r w -> p (r w)"), in_=x_v[1, c])
+                    load_halos(1)
+                regroup_w(sl, sl < 2)
             if 2 <= sl < PASSES + 2:
                 quant_w(sl - 2)
-            if 0 <= sl - LAG_Q < NS:
-                quant((sl - LAG_Q) // 5, (sl - LAG_Q) % 5)
             for call in fill.get(sl, []):
                 call()
             if chain:
+                quant((sl - LAG_Q) // 5, (sl - LAG_Q) % 5)
                 regroup((sl - LAG_R) // 5, (sl - LAG_R) % 5)
             for call in chain[10:]:
                 call()
@@ -408,5 +413,7 @@ def tile_shiftedpatchtokenization_pa_t_kernel(tc, x, ln1_g, ln1_b, w1, b1, out):
                 norm((sl + 1) // 5 + 1, (sl + 1) % 5)
             for call in chains.get(sl, [])[0:5]:
                 call()
+            if 0 <= sl - LAG_Q < NS and not chain:
+                quant((sl - LAG_Q) // 5, (sl - LAG_Q) % 5)
             if 0 <= sl - LAG_R < NS and not chain:
                 regroup((sl - LAG_R) // 5, (sl - LAG_R) % 5)

@@ -10,6 +10,7 @@ U32 = mybir.dt.uint32
 U8 = mybir.dt.uint8
 ALU = mybir.AluOpType
 ACTF = mybir.ActivationFunctionType
+AX = mybir.AxisListType
 
 P = 128
 PD = 2560
@@ -20,6 +21,8 @@ EPS = 1e-5
 FLOPS = 2 * 4096 * PD * DIM
 NG = 8
 NS = NG * PASSES
+WHOLE = slice(0, 512)
+HALVES = (slice(0, 256), slice(256, 512))
 LAG_R = 1
 LAG_Q = 2
 LAG_M = 3
@@ -119,13 +122,16 @@ def tile_shiftedpatchtokenization_pa_t_kernel(tc, x, ln1_g, ln1_b, w1, b1, out):
             gbt = const.tile([P, P], F32, name="gbt")
             b_bf = const.tile([P, DIM], BF16, name="b_bf")
             bias = const.tile([P, DIM], F32, name="bias")
+            load_w(0)
             load_halos(0)
-            for g in range(3):
-                load_w(g)
+            load_w(1)
+            load_w(2)
             nc.sync.dma_start(out=b_bf[:], in_=b1.partition_broadcast(P))
             nc.gpsimd.tensor_copy(out=bias[:], in_=b_bf[:])
             for c in range(6):
                 nc.scalar.copy(out=xs[0][:, c, 4:12, :], in_=xc[:, c])
+            regroup_w(0, True)
+            load_w(3)
 
             mean = const.tile([P, 32], F32, name="mean")
             rstd = const.tile([P, 32], F32, name="rstd")
@@ -133,15 +139,12 @@ def tile_shiftedpatchtokenization_pa_t_kernel(tc, x, ln1_g, ln1_b, w1, b1, out):
             own = (xc, xs[1][:, :, 4:12, :])
             bs = [const.tile([P, 2, 32, 6], F32, name="bs%d" % a) for a in range(2)]
             hh = [const.tile([P, 2, 32, 2], F32, name="hh%d" % a) for a in range(2)]
-            sq = const.tile([P, 2, 2, 32], F32, name="sq")
-            s2 = const.tile([P, 2, 2, 32], F32, name="s2")
+            sq = const.tile([P, 2, 2, 64], F32, name="sq")
             pair = const.tile([P, 2, 2, 16, 2], F32, name="pair")
             near = const.tile([P, 2, 2, 16, 2], F32, name="near")
             msq = const.tile([P, 32], F32, name="msq")
             ve = const.tile([P, 32], F32, name="ve")
             sd = const.tile([P, 32], F32, name="sd")
-            r0 = const.tile([P, 32], F32, name="r0")
-            t0 = const.tile([P, 32], F32, name="t0")
 
             def sums(a, j):
                 def one_block(h, s):
@@ -156,10 +159,8 @@ def tile_shiftedpatchtokenization_pa_t_kernel(tc, x, ln1_g, ln1_b, w1, b1, out):
             def stats(a, j_lo, j_hi, s_lo, s_hi):
                 nj = j_hi - j_lo
                 fresh = slice(2 * s_lo, 2 * s_hi)
-                new = bs[a][:, :, fresh, :]
-                sums_of = hh[a][:, :, fresh, :]
-                sqv = sq[:, a, :, fresh]
-                s2v = s2[:, a, :, fresh]
+                new = bs[a][:, :, fresh, :].rearrange("p h s (o v) -> p h (s o) v", o=2)
+                sqv = sq[:, a, :, 4 * s_lo:4 * s_hi]
                 bv = hh[a][:].rearrange("p h (j e) v -> p h j e v", e=2)
                 pv = pair[:, a, :, j_lo:j_hi, :]
                 nv = near[:, a, :, :, :]
@@ -168,20 +169,7 @@ def tile_shiftedpatchtokenization_pa_t_kernel(tc, x, ln1_g, ln1_b, w1, b1, out):
                 cols = slice(16 * a + j_lo, 16 * a + j_hi)
                 psum = {}
 
-                def squares():
-                    nc.vector.tensor_tensor(out=sqv, in0=new[:, :, :, 1], in1=new[:, :, :, 1], op=ALU.mult)
-                    nc.vector.tensor_tensor(out=s2v, in0=new[:, :, :, 4], in1=new[:, :, :, 4], op=ALU.mult)
-                    nc.vector.tensor_tensor(
-                        out=sums_of[:, :, :, 0], in0=new[:, :, :, 1], in1=new[:, :, :, 4], op=ALU.add
-                    )
-                    nc.vector.scalar_tensor_tensor(
-                        out=sqv, in0=sqv, scalar=64.0, in1=new[:, :, :, 2], op0=ALU.mult, op1=ALU.add
-                    )
-                    nc.vector.scalar_tensor_tensor(
-                        out=sums_of[:, :, :, 1], in0=s2v, scalar=64.0, in1=new[:, :, :, 5], op0=ALU.mult, op1=ALU.add
-                    )
-
-                def near_inner():
+                def neighbours():
                     nc.vector.tensor_tensor(
                         out=nv[:, :, left:right, :], in0=bv[:, :, left - 1:right - 1, 1, :],
                         in1=bv[:, :, left + 1:right + 1, 0, :], op=ALU.add,
@@ -202,14 +190,19 @@ def tile_shiftedpatchtokenization_pa_t_kernel(tc, x, ln1_g, ln1_b, w1, b1, out):
                     psum["sv"] = sv
 
                 return [
-                    squares,
-                    lambda: nc.vector.tensor_tensor(
-                        out=sums_of[:, :, :, 1], in0=sums_of[:, :, :, 1], in1=sqv, op=ALU.add
+                    lambda: nc.vector.tensor_tensor(out=sqv, in0=new[:, :, :, 1], in1=new[:, :, :, 1], op=ALU.mult),
+                    lambda: nc.vector.scalar_tensor_tensor(
+                        out=new[:, :, :, 2], in0=sqv, scalar=64.0, in1=new[:, :, :, 2], op0=ALU.mult, op1=ALU.add
+                    ),
+                    lambda: nc.vector.tensor_reduce(
+                        out=hh[a][:, :, fresh, :],
+                        in_=bs[a][:, :, fresh, :].rearrange("p h s (o v) -> p h s v o", o=2)[:, :, :, 1:3, :],
+                        op=ALU.add, axis=AX.X,
                     ),
                     lambda: nc.vector.tensor_tensor(
                         out=pv, in0=bv[:, :, j_lo:j_hi, 0, :], in1=bv[:, :, j_lo:j_hi, 1, :], op=ALU.add
                     ),
-                    near_inner,
+                    neighbours,
                     windows,
                     lambda: nc.vector.tensor_scalar(
                         out=mean[:, cols], in0=psum["sv"][:, :, 0], scalar1=64.0 / PD, scalar2=None, op0=ALU.mult
@@ -219,18 +212,8 @@ def tile_shiftedpatchtokenization_pa_t_kernel(tc, x, ln1_g, ln1_b, w1, b1, out):
                         out=ve[:, cols], in0=psum["sv"][:, :, 1], scalar=1.0 / PD, in1=msq[:, cols],
                         op0=ALU.mult, op1=ALU.subtract,
                     ),
-                    lambda: nc.vector.tensor_scalar(
-                        out=ve[:, cols], in0=ve[:, cols], scalar1=EPS, scalar2=None, op0=ALU.add
-                    ),
-                    lambda: nc.scalar.activation(out=sd[:, cols], in_=ve[:, cols], func=ACTF.Sqrt),
-                    lambda: nc.vector.reciprocal(out=r0[:, cols], in_=sd[:, cols]),
-                    lambda: nc.vector.scalar_tensor_tensor(
-                        out=t0[:, cols], in0=r0[:, cols], scalar=-0.5, in1=r0[:, cols], op0=ALU.mult, op1=ALU.mult
-                    ),
-                    lambda: nc.vector.tensor_tensor(out=t0[:, cols], in0=t0[:, cols], in1=ve[:, cols], op=ALU.mult),
-                    lambda: nc.vector.scalar_tensor_tensor(
-                        out=rstd[:, cols], in0=t0[:, cols], scalar=1.5, in1=r0[:, cols], op0=ALU.add, op1=ALU.mult
-                    ),
+                    lambda: nc.scalar.activation(out=sd[:, cols], in_=ve[:, cols], func=ACTF.Sqrt, bias=EPS),
+                    lambda: nc.vector.reciprocal(out=rstd[:, cols], in_=sd[:, cols]),
                     lambda: nc.vector.scalar_tensor_tensor(
                         out=nmr[:, cols], in0=mean[:, cols], scalar=-1.0, in1=rstd[:, cols], op0=ALU.mult, op1=ALU.mult
                     ),
@@ -305,20 +288,23 @@ def tile_shiftedpatchtokenization_pa_t_kernel(tc, x, ln1_g, ln1_b, w1, b1, out):
                     scale=gbt[:, kt:kt + 1], bias=gbt[:, 32 + kt:33 + kt],
                 )
 
-            def regroup(gi, g):
-                grouped = gpool.tile([P, 512, 4], BF16, name="grouped", align_bytes=64)
-                grouped_of[(gi, g)] = grouped
-                dst = grouped[:].rearrange("p (c i) t -> p c t i", i=4)
-                src = planes_of[(gi, g)][:].rearrange("p t (c i) -> p c t i", i=4)
+            def regroup(gi, g, cols):
+                if cols.start == 0:
+                    grouped_of[(gi, g)] = gpool.tile([P, 512, 4], BF16, name="grouped", align_bytes=64)
+                dst = grouped_of[(gi, g)][:, cols, :].rearrange("p (c i) t -> p c t i", i=4)
+                src = planes_of[(gi, g)][:, :, cols].rearrange("p t (c i) -> p c t i", i=4)
                 nc.vector.tensor_copy(out=dst, in_=src)
 
-            def quant(gi, g):
-                zc = zpool.tile([P, 512], U32, name="zc", align_bytes=64)
-                zs = zpool.tile([P, 512], U8, name="zs", align_bytes=64)
-                ztiles[(gi, g)] = (zc, zs)
+            def quant(gi, g, cols):
+                if cols.start == 0:
+                    ztiles[(gi, g)] = (
+                        zpool.tile([P, 512], U32, name="zc", align_bytes=64),
+                        zpool.tile([P, 512], U8, name="zs", align_bytes=64),
+                    )
+                zc, zs = ztiles[(gi, g)]
                 nc.vector.quantize_mx(
-                    out=zc[:].bitcast(FP8X4), scales=zs[:],
-                    in_=grouped_of[(gi, g)][:].rearrange("p w t -> p (w t)"),
+                    out=zc[:, cols].bitcast(FP8X4), scales=zs[:, cols],
+                    in_=grouped_of[(gi, g)][:, cols, :].rearrange("p w t -> p (w t)"),
                 )
 
             def mx(gi, g, tau):
@@ -344,7 +330,7 @@ def tile_shiftedpatchtokenization_pa_t_kernel(tc, x, ln1_g, ln1_b, w1, b1, out):
             for call in many_sums(0, 0, 5):
                 call()
             first = stats(0, 0, 4, 0, 5)
-            for call in first[0:5]:
+            for call in first[0:6]:
                 call()
             gb_ps = hop_ps.tile([P, 512], F32, name="bank")
             nc.tensor.transpose(out=gb_ps[:, 0:P], in_=gb_f[:], identity=ident[:])
@@ -352,7 +338,7 @@ def tile_shiftedpatchtokenization_pa_t_kernel(tc, x, ln1_g, ln1_b, w1, b1, out):
                 nc.vector.tensor_copy(out=xs[0][:, c, 4:12, :], in_=xc[:, c])
             for n in range(4):
                 rest[n]()
-            for call in first[5:10]:
+            for call in first[6:10]:
                 call()
             rest[4]()
             rest[5]()
@@ -381,23 +367,22 @@ def tile_shiftedpatchtokenization_pa_t_kernel(tc, x, ln1_g, ln1_b, w1, b1, out):
                 for tau in range(4):
                     finish((sl - LAG_M - 1) // 5, tau)
             chain = chains.get(sl - 1, [])
-            for call in chain[5:10]:
+            for call in chain[6:10]:
                 call()
-            if sl < PASSES:
-                if 1 <= sl <= 2:
-                    load_w(sl + 2)
-                if sl == 2:
-                    for c in range(8):
-                        nc.sync.dma_start(out=xs[1][:, c, 4:12, :].rearrange("p r w -> p (r w)"), in_=x_v[1, c])
-                    load_halos(1)
-                regroup_w(sl, sl < 2)
-            if 2 <= sl < PASSES + 2:
-                quant_w(sl - 2)
+            if sl == 1:
+                load_w(4)
+                for c in range(8):
+                    nc.sync.dma_start(out=xs[1][:, c, 4:12, :].rearrange("p r w -> p (r w)"), in_=x_v[1, c])
+                load_halos(1)
+            if sl < PASSES - 1:
+                regroup_w(sl + 1, sl < 2)
+            if 1 <= sl <= PASSES:
+                quant_w(sl - 1)
             for call in fill.get(sl, []):
                 call()
             if chain:
-                quant((sl - LAG_Q) // 5, (sl - LAG_Q) % 5)
-                regroup((sl - LAG_R) // 5, (sl - LAG_R) % 5)
+                quant((sl - LAG_Q) // 5, (sl - LAG_Q) % 5, WHOLE)
+                regroup((sl - LAG_R) // 5, (sl - LAG_R) % 5, WHOLE)
             for call in chain[10:]:
                 call()
             if sl == 3:
@@ -411,9 +396,14 @@ def tile_shiftedpatchtokenization_pa_t_kernel(tc, x, ln1_g, ln1_b, w1, b1, out):
                 norm(2, 1)
             elif 5 < sl < 34 and sl % 5 != 3:
                 norm((sl + 1) // 5 + 1, (sl + 1) % 5)
-            for call in chains.get(sl, [])[0:5]:
+            for call in chains.get(sl, [])[0:6]:
                 call()
-            if 0 <= sl - LAG_Q < NS and not chain:
-                quant((sl - LAG_Q) // 5, (sl - LAG_Q) % 5)
-            if 0 <= sl - LAG_R < NS and not chain:
-                regroup((sl - LAG_R) // 5, (sl - LAG_R) % 5)
+            if 0 <= sl - LAG_Q < NS - 1 and not chain:
+                quant((sl - LAG_Q) // 5, (sl - LAG_Q) % 5, WHOLE)
+            if 0 <= sl - LAG_R < NS - 1 and not chain:
+                regroup((sl - LAG_R) // 5, (sl - LAG_R) % 5, WHOLE)
+            if sl - LAG_R == NS - 1:
+                for cols in HALVES:
+                    regroup(NG - 1, PASSES - 1, cols)
+                for cols in HALVES:
+                    quant(NG - 1, PASSES - 1, cols)

@@ -21,11 +21,12 @@ EPS = 1e-5
 FLOPS = 2 * 4096 * PD * DIM
 NG = 8
 NS = NG * PASSES
+CHAIN_T = {3: 0, 13: 2}
 WHOLE = slice(0, 512)
 HALVES = (slice(0, 256), slice(256, 512))
 LAG_R = 1
 LAG_Q = 2
-LAG_M = 3
+LAG_M = 4
 
 
 def tile_shiftedpatchtokenization_pa_t_kernel(tc, x, ln1_g, ln1_b, w1, b1, out):
@@ -238,38 +239,60 @@ def tile_shiftedpatchtokenization_pa_t_kernel(tc, x, ln1_g, ln1_b, w1, b1, out):
                         op0=ALU.subtract, op1=ALU.mult,
                     )
 
-            def on_act(gi, tau, part):
-                if part == 0:
-                    return gi < 4 or tau < 3
-                return part == 2 and 2 <= gi <= 3
-
-            def norm(gi, tau):
-                a = gi // 4
-                j = 4 * (gi % 4) + tau
-                col = 16 * a + j
-                ntiles[(gi, tau)] = npool.tile([P, PD], F32, name="nt")
+            def window(gi, tau):
+                if (gi, tau) not in ntiles:
+                    ntiles[(gi, tau)] = npool.tile([P, PD], F32, name="nt")
                 nv = ntiles[(gi, tau)][:].rearrange("p (h w s c) -> p h w s c", h=8, w=8, s=5)
-                for dx in range(2):
-                    c0 = 8 * j - 4 + 8 * dx
-                    lo = max(0, -c0)
-                    hi = min(8, 128 - c0)
-                    for cq in range(2):
-                        src = xs[a][:, 4 * cq:4 * cq + 4, :, c0 + lo:c0 + hi].rearrange("p c (d h) w -> p d h w c", d=2)
-                        dst = nv[:, :, lo:hi, 1 + dx:5:2, 4 * cq:4 * cq + 4].rearrange("p h w d c -> p d h w c")
-                        if hi - lo == 8:
-                            affine(on_act(gi, tau, dx), dst, src, col)
-                        else:
-                            for d in range(2):
-                                affine(on_act(gi, tau, dx), dst[:, d], src[:, d], col)
-                    if lo > 0 or hi < 8:
-                        pad = slice(0, lo) if lo > 0 else slice(hi, 8)
-                        for d in range(2):
-                            affine(on_act(gi, tau, dx), nv[:, :, pad, 1 + 2 * d + dx, :], zt[:], col)
+                return gi // 4, 4 * (gi % 4) + tau, 4 * gi + tau, nv
+
+            def side(gi, tau, dx, cq, on_act):
+                a, j, col, nv = window(gi, tau)
+                c0 = 8 * j - 4 + 8 * dx
+                lo = max(0, -c0)
+                hi = min(8, 128 - c0)
+                src = xs[a][:, 4 * cq:4 * cq + 4, :, c0 + lo:c0 + hi].rearrange("p c (d h) w -> p d h w c", d=2)
+                dst = nv[:, :, lo:hi, 1 + dx:5:2, 4 * cq:4 * cq + 4].rearrange("p h w d c -> p d h w c")
+                if hi - lo == 8:
+                    affine(on_act, dst, src, col)
+                else:
+                    pad = slice(0, lo) if lo > 0 else slice(hi, 8)
+                    for d in range(2):
+                        affine(on_act, dst[:, d], src[:, d], col)
+                        affine(
+                            on_act, nv[:, :, pad, 1 + 2 * d + dx, 4 * cq:4 * cq + 4], zt[:, :, :, 4 * cq:4 * cq + 4], col,
+                        )
+
+            def centre(gi, tau, cq, on_act):
+                a, j, col, nv = window(gi, tau)
+                affine(
+                    on_act, nv[:, :, :, 0, 4 * cq:4 * cq + 4],
+                    xs[a][:, 4 * cq:4 * cq + 4, 4:12, 8 * j:8 * j + 8].rearrange("p c h w -> p h w c"), col,
+                )
+
+            def left_on_act(gi, tau):
+                return gi < 4 or tau != 1
+
+            def centre_on_act(gi, tau):
+                return gi == 3
+
+            def norm_vector(gi, tau):
                 for cq in range(2):
-                    affine(
-                        on_act(gi, tau, 2), nv[:, :, :, 0, 4 * cq:4 * cq + 4],
-                        xs[a][:, 4 * cq:4 * cq + 4, 4:12, 8 * j:8 * j + 8].rearrange("p c h w -> p h w c"), col,
-                    )
+                    side(gi, tau, 1, cq, False)
+                for cq in range(2):
+                    if not left_on_act(gi, tau):
+                        side(gi, tau, 0, cq, False)
+                for cq in range(2):
+                    if not centre_on_act(gi, tau):
+                        centre(gi, tau, cq, False)
+
+            def norm_scalar(gi, n, parts):
+                pieces = [(tau, cq) for tau in range(4) for cq in range(2)]
+                for of_act, piece in ((left_on_act, lambda tau, cq: side(gi, tau, 0, cq, True)),
+                                      (centre_on_act, lambda tau, cq: centre(gi, tau, cq, True))):
+                    mine = [(tau, cq) for tau, cq in pieces if of_act(gi, tau)]
+                    for i, (tau, cq) in enumerate(mine):
+                        if i * parts // len(mine) == n:
+                            piece(tau, cq)
 
             def hop(gi, g, t):
                 if t == 0:
@@ -346,7 +369,8 @@ def tile_shiftedpatchtokenization_pa_t_kernel(tc, x, ln1_g, ln1_b, w1, b1, out):
             for call in first[10:]:
                 call()
             for tau in range(4):
-                norm(0, tau)
+                norm_vector(0, tau)
+                norm_scalar(0, tau, 4)
             for call in rest[6:]:
                 call()
         zpool = ctx.enter_context(tc.tile_pool(name="zpool", bufs=5))
@@ -357,18 +381,21 @@ def tile_shiftedpatchtokenization_pa_t_kernel(tc, x, ln1_g, ln1_b, w1, b1, out):
             fill[5 + n] = many_sums(1, 2 * n, 2 * n + 2)
         chains = {2: stats(0, 4, 16, 5, 16), 12: stats(1, 0, 16, 0, 16)}
         for sl in range(NS + LAG_M + 1):
+            chain = chains.get(sl - 1, [])
             for t in range(4):
+                if t == CHAIN_T.get(sl, 4):
+                    chain[5]()
                 if sl < NS:
                     hop(sl // 5, sl % 5, t)
-                if t % 2 == 1 and 0 <= sl - LAG_M < NS:
+                if t == 1 and 0 <= sl - LAG_M < NS and sl < 34:
                     mx((sl - LAG_M) // 5, (sl - LAG_M) % 5, t - 1)
                     mx((sl - LAG_M) // 5, (sl - LAG_M) % 5, t)
+                if t == 3 and 0 <= sl - LAG_M < NS:
+                    for tau in range(2 if sl < 34 else 0, 4):
+                        mx((sl - LAG_M) // 5, (sl - LAG_M) % 5, tau)
             if sl - LAG_M - 1 >= 0 and (sl - LAG_M - 1) % 5 == 4:
                 for tau in range(4):
                     finish((sl - LAG_M - 1) // 5, tau)
-            chain = chains.get(sl - 1, [])
-            for call in chain[6:10]:
-                call()
             if sl == 1:
                 load_w(4)
                 for c in range(8):
@@ -378,6 +405,8 @@ def tile_shiftedpatchtokenization_pa_t_kernel(tc, x, ln1_g, ln1_b, w1, b1, out):
                 regroup_w(sl + 1, sl < 2)
             if 1 <= sl <= PASSES:
                 quant_w(sl - 1)
+            for call in chain[6:10]:
+                call()
             for call in fill.get(sl, []):
                 call()
             if chain:
@@ -385,23 +414,32 @@ def tile_shiftedpatchtokenization_pa_t_kernel(tc, x, ln1_g, ln1_b, w1, b1, out):
                 regroup((sl - LAG_R) // 5, (sl - LAG_R) % 5, WHOLE)
             for call in chain[10:]:
                 call()
-            if sl == 3:
-                norm(1, 0)
-                norm(1, 1)
-            elif sl == 4:
-                norm(1, 2)
-                norm(1, 3)
-            elif sl == 5:
-                norm(2, 0)
-                norm(2, 1)
-            elif 5 < sl < 34 and sl % 5 != 3:
-                norm((sl + 1) // 5 + 1, (sl + 1) % 5)
-            for call in chains.get(sl, [])[0:6]:
+            if sl in (3, 4):
+                for tau in (2 * sl - 6, 2 * sl - 5):
+                    norm_vector(1, tau)
+                    norm_scalar(1, tau, 4)
+            elif 4 < sl < 34:
+                nxt = (sl + 1) // 5 + 1
+                n = (sl + 1) % 5
+                if sl == 5:
+                    norm_vector(nxt, 0)
+                    norm_scalar(nxt, 0, 5)
+                if 0 < n < 4:
+                    norm_vector(nxt, n)
+                norm_scalar(nxt, n, 5)
+            opening = chains.get(sl, [])
+            for call in opening[0:1]:
                 call()
             if 0 <= sl - LAG_Q < NS - 1 and not chain:
                 quant((sl - LAG_Q) // 5, (sl - LAG_Q) % 5, WHOLE)
+            for call in opening[1:2]:
+                call()
             if 0 <= sl - LAG_R < NS - 1 and not chain:
                 regroup((sl - LAG_R) // 5, (sl - LAG_R) % 5, WHOLE)
+            for call in opening[2:5]:
+                call()
+            if 5 < sl < 34 and sl % 5 == 4:
+                norm_vector((sl + 1) // 5 + 1, 0)
             if sl - LAG_R == NS - 1:
                 for cols in HALVES:
                     regroup(NG - 1, PASSES - 1, cols)

@@ -154,14 +154,25 @@ def tile_shiftedpatchtokenization_pa_t_kernel(tc, x, ln1_g, ln1_b, w1, b1, out):
                     )
                 return [lambda h=h, s=s: one_block(h, s) for h in range(2) for s in (2 * j, 2 * j + 1)]
 
+            bs_first = const.tile([P, 2, 10, 2, 6], F32, name="bs_first")
+
+            def first_sums(cq):
+                for h in range(2):
+                    for s in range(10):
+                        nc.vector.bn_stats(
+                            out=bs_first[:, h, s, cq, :],
+                            in_=xc[:, 4 * cq:4 * cq + 4, 4 * h:4 * h + 4, 4 * s:4 * s + 4],
+                        )
+
             def many_sums(a, j_lo, j_hi):
                 return [call for j in range(j_lo, j_hi) for call in sums(a, j)]
 
-            def stats(a, j_lo, j_hi, s_lo, s_hi):
+            def stats(a, j_lo, j_hi, s_lo, s_hi, blocks, count):
                 nj = j_hi - j_lo
                 fresh = slice(2 * s_lo, 2 * s_hi)
-                new = bs[a][:, :, fresh, :].rearrange("p h s (o v) -> p h (s o) v", o=2)
-                sqv = sq[:, a, :, 4 * s_lo:4 * s_hi]
+                split = blocks.shape[3] // 3
+                new = blocks.rearrange("p h s (o v) -> p h (s o) v", v=3)
+                sqv = sq[:, a, :, split * 2 * s_lo:split * 2 * s_hi]
                 bv = hh[a][:].rearrange("p h (j e) v -> p h j e v", e=2)
                 pv = pair[:, a, :, j_lo:j_hi, :]
                 nv = near[:, a, :, :, :]
@@ -193,11 +204,11 @@ def tile_shiftedpatchtokenization_pa_t_kernel(tc, x, ln1_g, ln1_b, w1, b1, out):
                 return [
                     lambda: nc.vector.tensor_tensor(out=sqv, in0=new[:, :, :, 1], in1=new[:, :, :, 1], op=ALU.mult),
                     lambda: nc.vector.scalar_tensor_tensor(
-                        out=new[:, :, :, 2], in0=sqv, scalar=64.0, in1=new[:, :, :, 2], op0=ALU.mult, op1=ALU.add
+                        out=new[:, :, :, 2], in0=sqv, scalar=float(count), in1=new[:, :, :, 2], op0=ALU.mult, op1=ALU.add
                     ),
                     lambda: nc.vector.tensor_reduce(
                         out=hh[a][:, :, fresh, :],
-                        in_=bs[a][:, :, fresh, :].rearrange("p h s (o v) -> p h s v o", o=2)[:, :, :, 1:3, :],
+                        in_=blocks.rearrange("p h s (o v) -> p h s v o", v=3)[:, :, :, 1:3, :],
                         op=ALU.add, axis=AX.X,
                     ),
                     lambda: nc.vector.tensor_tensor(
@@ -206,7 +217,7 @@ def tile_shiftedpatchtokenization_pa_t_kernel(tc, x, ln1_g, ln1_b, w1, b1, out):
                     neighbours,
                     windows,
                     lambda: nc.vector.tensor_scalar(
-                        out=mean[:, cols], in0=psum["sv"][:, :, 0], scalar1=64.0 / PD, scalar2=None, op0=ALU.mult
+                        out=mean[:, cols], in0=psum["sv"][:, :, 0], scalar1=float(count) / PD, scalar2=None, op0=ALU.mult
                     ),
                     lambda: nc.vector.tensor_tensor(out=msq[:, cols], in0=mean[:, cols], in1=mean[:, cols], op=ALU.mult),
                     lambda: nc.vector.scalar_tensor_tensor(
@@ -270,7 +281,7 @@ def tile_shiftedpatchtokenization_pa_t_kernel(tc, x, ln1_g, ln1_b, w1, b1, out):
                 )
 
             def left_on_act(gi, tau):
-                return gi < 4 or tau != 1
+                return gi < 5 or tau % 2 == 0
 
             def centre_on_act(gi, tau):
                 return gi == 3
@@ -350,9 +361,9 @@ def tile_shiftedpatchtokenization_pa_t_kernel(tc, x, ln1_g, ln1_b, w1, b1, out):
                 nc.sync.dma_start(out=out_v[gi // 4, 4 * (gi % 4) + tau], in_=res[:])
 
             rest = many_sums(0, 5, 16)
-            for call in many_sums(0, 0, 5):
-                call()
-            first = stats(0, 0, 4, 0, 5)
+            for cq in range(2):
+                first_sums(cq)
+            first = stats(0, 0, 4, 0, 5, bs_first[:].rearrange("p h s q v -> p h s (q v)"), 32)
             for call in first[0:6]:
                 call()
             gb_ps = hop_ps.tile([P, 512], F32, name="bank")
@@ -371,6 +382,9 @@ def tile_shiftedpatchtokenization_pa_t_kernel(tc, x, ln1_g, ln1_b, w1, b1, out):
             for tau in range(4):
                 norm_vector(0, tau)
                 norm_scalar(0, tau, 4)
+            nc.vector.tensor_scalar(
+                out=hh[0][:, :, 6:10, 0], in0=hh[0][:, :, 6:10, 0], scalar1=0.5, scalar2=None, op0=ALU.mult
+            )
             for call in rest[6:]:
                 call()
         zpool = ctx.enter_context(tc.tile_pool(name="zpool", bufs=5))
@@ -379,7 +393,7 @@ def tile_shiftedpatchtokenization_pa_t_kernel(tc, x, ln1_g, ln1_b, w1, b1, out):
         fill = {}
         for n in range(8):
             fill[5 + n] = many_sums(1, 2 * n, 2 * n + 2)
-        chains = {2: stats(0, 4, 16, 5, 16), 12: stats(1, 0, 16, 0, 16)}
+        chains = {2: stats(0, 4, 16, 5, 16, bs[0][:, :, 10:32, :], 64), 12: stats(1, 0, 16, 0, 16, bs[1][:], 64)}
         for sl in range(NS + LAG_M + 1):
             chain = chains.get(sl - 1, [])
             for t in range(4):

@@ -46,17 +46,24 @@ def tile_shiftedpatchtokenization_pa_t_kernel(tc, x, ln1_g, ln1_b, w1, b1, out):
         xs = [xpool.tile([P, 8, 16, 128], BF16, name="x%d" % a) for a in range(2)]
         x_v = x.rearrange("(a b) c (i r) w -> a c i b (r w)", a=2, r=8)
 
-        def clear_edges(a):
-            for c in range(8):
-                xz = xs[a][:, c].rearrange("p r w -> p (r w)").bitcast(U32)
-                nc.gpsimd.memset(xz[0:8, 0:256], 0)
-                nc.gpsimd.memset(xz[96:128, 768:1024], 0)
+        x_b = x.rearrange("b c h w -> b (c h w)")
 
-        def load_halos(a):
-            for c in range(8):
-                rows = xs[a][:, c].rearrange("p r w -> p (r w)")
-                nc.sync.dma_start(out=rows[8:128, 0:512], in_=x_v[a, c, 0:15, :, 512:1024])
+        def clear_above(a, c):
+            nc.gpsimd.memset(xs[a][:, c].rearrange("p r w -> p (r w)").bitcast(U32)[0:8, 0:256], 0)
+
+        def clear_below(a, c):
+            nc.gpsimd.memset(xs[a][:, c].rearrange("p r w -> p (r w)").bitcast(U32)[96:128, 768:1024], 0)
+
+        def load_halo(a, c, below, wrapped):
+            rows = xs[a][:, c].rearrange("p r w -> p (r w)")
+            if wrapped:
+                start = c * 16384 + (1024 if below else -512)
+                src = x_b[8 * a:8 * a + 8, start:start + 16384].rearrange("b (i r) -> i b r", r=1024)[:, :, 0:512]
+                nc.sync.dma_start(out=rows[:, 1536:2048] if below else rows[:, 0:512], in_=src)
+            elif below:
                 nc.sync.dma_start(out=rows[0:120, 1536:2048], in_=x_v[a, c, 1:16, :, 0:512])
+            else:
+                nc.sync.dma_start(out=rows[8:128, 0:512], in_=x_v[a, c, 0:15, :, 512:1024])
 
         with tc.tile_pool(name="xcpool", bufs=1) as xcpool:
             xc = xcpool.tile([P, 8, 8, 128], BF16, name="xc")
@@ -94,9 +101,6 @@ def tile_shiftedpatchtokenization_pa_t_kernel(tc, x, ln1_g, ln1_b, w1, b1, out):
             nc.scalar.activation(out=one[:], in_=one[:], func=ACTF.Sqrt)
             gb_bf = const.tile([P, P], BF16, name="gb_bf")
             nc.gpsimd.memset(gb_bf[:], 0.0)
-            nc.sync.dma_start(out=gb_bf[0:KT, :], in_=ln1_g.rearrange("(c p) -> c p", p=P))
-            nc.sync.dma_start(out=gb_bf[32:32 + KT, :], in_=ln1_b.rearrange("(c p) -> c p", p=P))
-            clear_edges(0)
             ident = const.tile([P, P], F32, name="ident")
             make_identity(nc, ident[:])
             l1 = const.tile([P, P], F32, name="l1")
@@ -115,20 +119,39 @@ def tile_shiftedpatchtokenization_pa_t_kernel(tc, x, ln1_g, ln1_b, w1, b1, out):
                 in_=ident[:].rearrange("p (i b) -> p b i", b=8),
             )
             gb_f = const.tile([P, P], F32, name="gb_f")
-            nc.gpsimd.tensor_copy(out=gb_f[:], in_=gb_bf[:])
             zt = const.tile([P, 8, 4, 8], BF16, name="zt")
             nc.gpsimd.memset(zt[:], 0.0)
-            clear_edges(1)
+            inside = const.tile([P, 1], F32, name="inside")
+            nc.vector.tensor_reduce(out=inside[:], in_=ident[:, 0:120], op=ALU.add, axis=AX.X)
+            clear_below(0, 7)
 
             gbt = const.tile([P, P], F32, name="gbt")
             b_bf = const.tile([P, DIM], BF16, name="b_bf")
             bias = const.tile([P, DIM], F32, name="bias")
             load_w(0)
-            load_halos(0)
+            for c in range(7):
+                load_halo(0, c, True, True)
+                if c < 4:
+                    nc.gpsimd.tensor_scalar(
+                        out=xs[0][96:128, c, 12:16, :], in0=xs[0][96:128, c, 12:16, :],
+                        scalar1=inside[96:128, :], scalar2=0.0, op0=ALU.mult, op1=ALU.add,
+                    )
+            for c in range(1, 8):
+                load_halo(0, c, False, True)
+                clear_above(0, c)
+            clear_above(0, 0)
+            load_halo(0, 7, True, False)
+            load_halo(0, 0, False, False)
+            nc.sync.dma_start(out=gb_bf[0:KT, :], in_=ln1_g.rearrange("(c p) -> c p", p=P))
+            nc.sync.dma_start(out=gb_bf[32:32 + KT, :], in_=ln1_b.rearrange("(c p) -> c p", p=P))
+            nc.gpsimd.tensor_copy(out=gb_f[:], in_=gb_bf[:])
             load_w(1)
             load_w(2)
             nc.sync.dma_start(out=b_bf[:], in_=b1.partition_broadcast(P))
             nc.gpsimd.tensor_copy(out=bias[:], in_=b_bf[:])
+            for c in range(8):
+                clear_above(1, c)
+                clear_below(1, c)
             for c in range(6):
                 nc.scalar.copy(out=xs[0][:, c, 4:12, :], in_=xc[:, c])
             regroup_w(0, True)
@@ -281,7 +304,7 @@ def tile_shiftedpatchtokenization_pa_t_kernel(tc, x, ln1_g, ln1_b, w1, b1, out):
                 )
 
             def left_on_act(gi, tau):
-                return gi < 5 or tau % 2 == 0
+                return gi < 4 or tau != 1
 
             def centre_on_act(gi, tau):
                 return gi == 3
@@ -366,8 +389,6 @@ def tile_shiftedpatchtokenization_pa_t_kernel(tc, x, ln1_g, ln1_b, w1, b1, out):
             first = stats(0, 0, 4, 0, 5, bs_first[:].rearrange("p h s q v -> p h s (q v)"), 32)
             for call in first[0:6]:
                 call()
-            gb_ps = hop_ps.tile([P, 512], F32, name="bank")
-            nc.tensor.transpose(out=gb_ps[:, 0:P], in_=gb_f[:], identity=ident[:])
             for c in range(6, 8):
                 nc.vector.tensor_copy(out=xs[0][:, c, 4:12, :], in_=xc[:, c])
             for n in range(4):
@@ -376,12 +397,18 @@ def tile_shiftedpatchtokenization_pa_t_kernel(tc, x, ln1_g, ln1_b, w1, b1, out):
                 call()
             rest[4]()
             rest[5]()
-            nc.scalar.copy(out=gbt[:], in_=gb_ps[:, 0:P])
             for call in first[10:]:
                 call()
+            nc.vector.tensor_scalar(
+                out=xs[0][96:128, 4:7, 12:16, :], in0=xs[0][96:128, 4:7, 12:16, :],
+                scalar1=inside[96:128, :], scalar2=None, op0=ALU.mult,
+            )
             for tau in range(4):
                 norm_vector(0, tau)
                 norm_scalar(0, tau, 4)
+            gb_ps = hop_ps.tile([P, 512], F32, name="bank")
+            nc.tensor.transpose(out=gb_ps[:, 0:P], in_=gb_f[:], identity=ident[:])
+            nc.scalar.copy(out=gbt[:], in_=gb_ps[:, 0:P])
             nc.vector.tensor_scalar(
                 out=hh[0][:, :, 6:10, 0], in0=hh[0][:, :, 6:10, 0], scalar1=0.5, scalar2=None, op0=ALU.mult
             )
@@ -391,14 +418,16 @@ def tile_shiftedpatchtokenization_pa_t_kernel(tc, x, ln1_g, ln1_b, w1, b1, out):
         rpool = ctx.enter_context(tc.tile_pool(name="rpool", bufs=4))
 
         fill = {}
-        for n in range(8):
-            fill[5 + n] = many_sums(1, 2 * n, 2 * n + 2)
-        chains = {2: stats(0, 4, 16, 5, 16, bs[0][:, :, 10:32, :], 64), 12: stats(1, 0, 16, 0, 16, bs[1][:], 64)}
+        for n, sl in enumerate((5, 6, 7, 8, 9, 10, 11, 12)):
+            fill[sl] = many_sums(1, 2 * n, 2 * n + 2)
+        opens = {2: stats(0, 4, 16, 5, 16, bs[0][:, :, 10:32, :], 64), 12: stats(1, 0, 16, 0, 16, bs[1][:], 64)}
+        wins = {(3, 1): opens[2][5], (14, 1): opens[12][5]}
+        closes = {3: opens[2], 14: opens[12]}
         for sl in range(NS + LAG_M + 1):
-            chain = chains.get(sl - 1, [])
+            chain = closes.get(sl, [])
             for t in range(4):
-                if t == CHAIN_T.get(sl, 4):
-                    chain[5]()
+                if (sl, t) in wins:
+                    wins[(sl, t)]()
                 if sl < NS:
                     hop(sl // 5, sl % 5, t)
                 if t == 1 and 0 <= sl - LAG_M < NS and sl < 34:
@@ -414,7 +443,9 @@ def tile_shiftedpatchtokenization_pa_t_kernel(tc, x, ln1_g, ln1_b, w1, b1, out):
                 load_w(4)
                 for c in range(8):
                     nc.sync.dma_start(out=xs[1][:, c, 4:12, :].rearrange("p r w -> p (r w)"), in_=x_v[1, c])
-                load_halos(1)
+                for c in range(8):
+                    load_halo(1, c, False, False)
+                    load_halo(1, c, True, False)
             if sl < PASSES - 1:
                 regroup_w(sl + 1, sl < 2)
             if 1 <= sl <= PASSES:
@@ -441,7 +472,7 @@ def tile_shiftedpatchtokenization_pa_t_kernel(tc, x, ln1_g, ln1_b, w1, b1, out):
                 if 0 < n < 4:
                     norm_vector(nxt, n)
                 norm_scalar(nxt, n, 5)
-            opening = chains.get(sl, [])
+            opening = opens.get(sl, [])
             for call in opening[0:1]:
                 call()
             if 0 <= sl - LAG_Q < NS - 1 and not chain:

from contextlib import ExitStack

import concourse.mybir as mybir
from concourse.masks import make_identity

FP8X4 = mybir.dt.float8_e4m3fn_x4
BF16 = mybir.dt.bfloat16
F32 = mybir.dt.float32
U32 = mybir.dt.uint32
U8 = mybir.dt.uint8
ALU = mybir.AluOpType
ACTF = mybir.ActivationFunctionType
AX = mybir.AxisListType

P = 128
PD = 2560
DIM = 512
KT = PD // P
PASSES = 5
EPS = 1e-5
FLOPS = 2 * 4096 * PD * DIM
NG = 8
NS = NG * PASSES
CHAIN_T = {3: 0, 13: 2}
WHOLE = slice(0, 512)
HALVES = (slice(0, 256), slice(256, 512))
LAG_R = 1
LAG_Q = 2
LAG_M = 4


def tile_shiftedpatchtokenization_pa_t_kernel(tc, x, ln1_g, ln1_b, w1, b1, out):
    nc = tc.nc
    with ExitStack() as ctx:
        ctx.enter_context(tc.manual_schedule())
        const = ctx.enter_context(tc.tile_pool(name="const", bufs=1))
        xpool = ctx.enter_context(tc.tile_pool(name="xpool", bufs=1))
        wst = ctx.enter_context(tc.tile_pool(name="wst", bufs=3))
        wgp = ctx.enter_context(tc.tile_pool(name="wgp", bufs=3))
        npool = ctx.enter_context(tc.tile_pool(name="npool", bufs=8))
        ppool = ctx.enter_context(tc.tile_pool(name="ppool", bufs=3))
        gpool = ctx.enter_context(tc.tile_pool(name="gpool", bufs=2))
        hop_ps = ctx.enter_context(tc.psum_pool(name="hop_ps", bufs=4))
        acc_ps = ctx.enter_context(tc.psum_pool(name="acc_ps", bufs=4))

        xs = [xpool.tile([P, 8, 16, 128], BF16, name="x%d" % a) for a in range(2)]
        x_v = x.rearrange("(a b) c (i r) w -> a c i b (r w)", a=2, r=8)

        x_b = x.rearrange("b c h w -> b (c h w)")

        def clear_above(a, c):
            nc.gpsimd.memset(xs[a][:, c].rearrange("p r w -> p (r w)").bitcast(U32)[0:8, 0:256], 0)

        def clear_below(a, c):
            nc.gpsimd.memset(xs[a][:, c].rearrange("p r w -> p (r w)").bitcast(U32)[96:128, 768:1024], 0)

        def load_halo(a, c, below, wrapped):
            rows = xs[a][:, c].rearrange("p r w -> p (r w)")
            if wrapped:
                start = c * 16384 + (1024 if below else -512)
                src = x_b[8 * a:8 * a + 8, start:start + 16384].rearrange("b (i r) -> i b r", r=1024)[:, :, 0:512]
                nc.sync.dma_start(out=rows[:, 1536:2048] if below else rows[:, 0:512], in_=src)
            elif below:
                nc.sync.dma_start(out=rows[0:120, 1536:2048], in_=x_v[a, c, 1:16, :, 0:512])
            else:
                nc.sync.dma_start(out=rows[8:128, 0:512], in_=x_v[a, c, 0:15, :, 512:1024])

        with tc.tile_pool(name="xcpool", bufs=1) as xcpool:
            xc = xcpool.tile([P, 8, 8, 128], BF16, name="xc")
            for c in range(8):
                nc.sync.dma_start(out=xc[:, c].rearrange("p r w -> p (r w)"), in_=x_v[0, c])

            wc = const.tile([P, PASSES, DIM], U32, name="wc", align_bytes=64)
            ws = const.tile([P, PASSES, DIM], U8, name="ws", align_bytes=64)
            w_v = w1.rearrange("(g t p) n -> g p t n", t=4, p=P)
            raws = []
            wgs = []

            def load_w(g):
                raw = wst.tile([P, 4, DIM], BF16, name="raw")
                nc.sync.dma_start(out=raw[:], in_=w_v[g])
                raws.append(raw)

            def regroup_w(g, on_act):
                wg = wgp.tile([P, DIM, 4], BF16, name="wg", align_bytes=64)
                dst = wg[:].rearrange("p (c i) t -> p c t i", i=4)
                src = raws[g][:].rearrange("p t (c i) -> p c t i", i=4)
                if on_act:
                    nc.scalar.copy(out=dst, in_=src)
                else:
                    nc.vector.tensor_copy(out=dst, in_=src)
                wgs.append(wg)

            def quant_w(g):
                nc.vector.quantize_mx(
                    out=wc[:, g, :].bitcast(FP8X4), scales=ws[:, g, :], in_=wgs[g][:].rearrange("p w t -> p (w t)"),
                )

            one = const.tile([P, 1], F32, name="one")
            nc.vector.memset(one[:], 1.0)
            nc.scalar.activation(out=one[:], in_=one[:], func=ACTF.Sqrt)
            gb_bf = const.tile([P, P], BF16, name="gb_bf")
            nc.gpsimd.memset(gb_bf[:], 0.0)
            ident = const.tile([P, P], F32, name="ident")
            make_identity(nc, ident[:])
            l1 = const.tile([P, P], F32, name="l1")
            l0 = const.tile([P, P], F32, name="l0")
            l1c = const.tile([P, P], F32, name="l1c")
            l0c = const.tile([P, P], F32, name="l0c")
            nc.gpsimd.tensor_copy(out=l1[:], in_=ident[:])
            nc.gpsimd.tensor_tensor(out=l1[:, 8:128], in0=l1[:, 8:128], in1=ident[:, 0:120], op=ALU.add)
            nc.gpsimd.tensor_copy(out=l0[:], in_=ident[:])
            nc.gpsimd.tensor_tensor(out=l0[:, 0:120], in0=l0[:, 0:120], in1=ident[:, 8:128], op=ALU.add)
            nc.gpsimd.tensor_tensor(out=l1c[:], in0=l1[:], in1=ident[:], op=ALU.add)
            nc.gpsimd.tensor_tensor(out=l0c[:], in0=l0[:], in1=ident[:], op=ALU.add)
            perm = const.tile([P, P], F32, name="perm")
            nc.gpsimd.tensor_copy(
                out=perm[:].rearrange("p (b i) -> p b i", b=8),
                in_=ident[:].rearrange("p (i b) -> p b i", b=8),
            )
            gb_f = const.tile([P, P], F32, name="gb_f")
            zt = const.tile([P, 8, 4, 8], BF16, name="zt")
            nc.gpsimd.memset(zt[:], 0.0)
            inside = const.tile([P, 1], F32, name="inside")
            nc.vector.tensor_reduce(out=inside[:], in_=ident[:, 0:120], op=ALU.add, axis=AX.X)
            clear_below(0, 7)

            gbt = const.tile([P, P], F32, name="gbt")
            b_bf = const.tile([P, DIM], BF16, name="b_bf")
            bias = const.tile([P, DIM], F32, name="bias")
            load_w(0)
            for c in range(7):
                load_halo(0, c, True, True)
                if c < 4:
                    nc.gpsimd.tensor_scalar(
                        out=xs[0][96:128, c, 12:16, :], in0=xs[0][96:128, c, 12:16, :],
                        scalar1=inside[96:128, :], scalar2=0.0, op0=ALU.mult, op1=ALU.add,
                    )
            for c in range(1, 8):
                load_halo(0, c, False, True)
                clear_above(0, c)
            clear_above(0, 0)
            load_halo(0, 7, True, False)
            load_halo(0, 0, False, False)
            nc.sync.dma_start(out=gb_bf[0:KT, :], in_=ln1_g.rearrange("(c p) -> c p", p=P))
            nc.sync.dma_start(out=gb_bf[32:32 + KT, :], in_=ln1_b.rearrange("(c p) -> c p", p=P))
            nc.gpsimd.tensor_copy(out=gb_f[:], in_=gb_bf[:])
            load_w(1)
            load_w(2)
            nc.sync.dma_start(out=b_bf[:], in_=b1.partition_broadcast(P))
            nc.gpsimd.tensor_copy(out=bias[:], in_=b_bf[:])
            for c in range(8):
                clear_above(1, c)
                clear_below(1, c)
            for c in range(6):
                nc.scalar.copy(out=xs[0][:, c, 4:12, :], in_=xc[:, c])
            regroup_w(0, True)
            load_w(3)

            mean = const.tile([P, 32], F32, name="mean")
            rstd = const.tile([P, 32], F32, name="rstd")
            nmr = const.tile([P, 32], F32, name="nmr")
            own = (xc, xs[1][:, :, 4:12, :])
            bs = [const.tile([P, 2, 32, 6], F32, name="bs%d" % a) for a in range(2)]
            hh = [const.tile([P, 2, 32, 2], F32, name="hh%d" % a) for a in range(2)]
            sq = const.tile([P, 2, 2, 64], F32, name="sq")
            pair = const.tile([P, 2, 2, 16, 2], F32, name="pair")
            near = const.tile([P, 2, 2, 16, 2], F32, name="near")
            msq = const.tile([P, 32], F32, name="msq")
            ve = const.tile([P, 32], F32, name="ve")
            sd = const.tile([P, 32], F32, name="sd")

            def sums(a, j):
                def one_block(h, s):
                    nc.vector.bn_stats(
                        out=bs[a][:, h, s, :], in_=own[a][:, :, 4 * h:4 * h + 4, 4 * s:4 * s + 4],
                    )
                return [lambda h=h, s=s: one_block(h, s) for h in range(2) for s in (2 * j, 2 * j + 1)]

            bs_first = const.tile([P, 2, 10, 2, 6], F32, name="bs_first")

            def first_sums(cq):
                for h in range(2):
                    for s in range(10):
                        nc.vector.bn_stats(
                            out=bs_first[:, h, s, cq, :],
                            in_=xc[:, 4 * cq:4 * cq + 4, 4 * h:4 * h + 4, 4 * s:4 * s + 4],
                        )

            def many_sums(a, j_lo, j_hi):
                return [call for j in range(j_lo, j_hi) for call in sums(a, j)]

            def stats(a, j_lo, j_hi, s_lo, s_hi, blocks, count):
                nj = j_hi - j_lo
                fresh = slice(2 * s_lo, 2 * s_hi)
                split = blocks.shape[3] // 3
                new = blocks.rearrange("p h s (o v) -> p h (s o) v", v=3)
                sqv = sq[:, a, :, split * 2 * s_lo:split * 2 * s_hi]
                bv = hh[a][:].rearrange("p h (j e) v -> p h j e v", e=2)
                pv = pair[:, a, :, j_lo:j_hi, :]
                nv = near[:, a, :, :, :]
                left = max(j_lo, 1)
                right = min(j_hi, 15)
                cols = slice(16 * a + j_lo, 16 * a + j_hi)
                psum = {}

                def neighbours():
                    nc.vector.tensor_tensor(
                        out=nv[:, :, left:right, :], in0=bv[:, :, left - 1:right - 1, 1, :],
                        in1=bv[:, :, left + 1:right + 1, 0, :], op=ALU.add,
                    )
                    if j_lo == 0:
                        nc.vector.tensor_copy(out=nv[:, :, 0, :], in_=bv[:, :, 1, 0, :])
                    if j_hi == 16:
                        nc.vector.tensor_copy(out=nv[:, :, 15, :], in_=bv[:, :, 14, 1, :])

                def windows():
                    st = hop_ps.tile([P, 512], F32, name="bank")
                    sv = st[:, 0:2 * nj].rearrange("p (j v) -> p j v", v=2)
                    terms = ((l1c, pair, 1), (l0c, pair, 0), (l1, near, 1), (l0, near, 0))
                    for n, (lhs, part, h) in enumerate(terms):
                        nc.tensor.matmul(
                            out=sv, lhsT=lhs[:], rhs=part[:, a, h, j_lo:j_hi, :], start=(n == 0), stop=(n == 3),
                        )
                    psum["sv"] = sv

                return [
                    lambda: nc.vector.tensor_tensor(out=sqv, in0=new[:, :, :, 1], in1=new[:, :, :, 1], op=ALU.mult),
                    lambda: nc.vector.scalar_tensor_tensor(
                        out=new[:, :, :, 2], in0=sqv, scalar=float(count), in1=new[:, :, :, 2], op0=ALU.mult, op1=ALU.add
                    ),
                    lambda: nc.vector.tensor_reduce(
                        out=hh[a][:, :, fresh, :],
                        in_=blocks.rearrange("p h s (o v) -> p h s v o", v=3)[:, :, :, 1:3, :],
                        op=ALU.add, axis=AX.X,
                    ),
                    lambda: nc.vector.tensor_tensor(
                        out=pv, in0=bv[:, :, j_lo:j_hi, 0, :], in1=bv[:, :, j_lo:j_hi, 1, :], op=ALU.add
                    ),
                    neighbours,
                    windows,
                    lambda: nc.vector.tensor_scalar(
                        out=mean[:, cols], in0=psum["sv"][:, :, 0], scalar1=float(count) / PD, scalar2=None, op0=ALU.mult
                    ),
                    lambda: nc.vector.tensor_tensor(out=msq[:, cols], in0=mean[:, cols], in1=mean[:, cols], op=ALU.mult),
                    lambda: nc.vector.scalar_tensor_tensor(
                        out=ve[:, cols], in0=psum["sv"][:, :, 1], scalar=1.0 / PD, in1=msq[:, cols],
                        op0=ALU.mult, op1=ALU.subtract,
                    ),
                    lambda: nc.scalar.activation(out=sd[:, cols], in_=ve[:, cols], func=ACTF.Sqrt, bias=EPS),
                    lambda: nc.vector.reciprocal(out=rstd[:, cols], in_=sd[:, cols]),
                    lambda: nc.vector.scalar_tensor_tensor(
                        out=nmr[:, cols], in0=mean[:, cols], scalar=-1.0, in1=rstd[:, cols], op0=ALU.mult, op1=ALU.mult
                    ),
                ]

            out_v = out.flatten_outer_dims().rearrange("(a n j) d -> a j n d", a=2, j=16)
            ntiles = {}
            ztiles = {}
            planes_of = {}
            grouped_of = {}
            accs = {}

            def affine(on_act, dst, src, col):
                if on_act:
                    nc.scalar.activation(
                        out=dst, in_=src, func=ACTF.Identity,
                        scale=rstd[:, col:col + 1], bias=nmr[:, col:col + 1],
                    )
                else:
                    nc.vector.tensor_scalar(
                        out=dst, in0=src, scalar1=mean[:, col:col + 1], scalar2=rstd[:, col:col + 1],
                        op0=ALU.subtract, op1=ALU.mult,
                    )

            def window(gi, tau):
                if (gi, tau) not in ntiles:
                    ntiles[(gi, tau)] = npool.tile([P, PD], F32, name="nt")
                nv = ntiles[(gi, tau)][:].rearrange("p (h w s c) -> p h w s c", h=8, w=8, s=5)
                return gi // 4, 4 * (gi % 4) + tau, 4 * gi + tau, nv

            def side(gi, tau, dx, cq, on_act):
                a, j, col, nv = window(gi, tau)
                c0 = 8 * j - 4 + 8 * dx
                lo = max(0, -c0)
                hi = min(8, 128 - c0)
                src = xs[a][:, 4 * cq:4 * cq + 4, :, c0 + lo:c0 + hi].rearrange("p c (d h) w -> p d h w c", d=2)
                dst = nv[:, :, lo:hi, 1 + dx:5:2, 4 * cq:4 * cq + 4].rearrange("p h w d c -> p d h w c")
                if hi - lo == 8:
                    affine(on_act, dst, src, col)
                else:
                    pad = slice(0, lo) if lo > 0 else slice(hi, 8)
                    for d in range(2):
                        affine(on_act, dst[:, d], src[:, d], col)
                        affine(
                            on_act, nv[:, :, pad, 1 + 2 * d + dx, 4 * cq:4 * cq + 4], zt[:, :, :, 4 * cq:4 * cq + 4], col,
                        )

            def centre(gi, tau, cq, on_act):
                a, j, col, nv = window(gi, tau)
                affine(
                    on_act, nv[:, :, :, 0, 4 * cq:4 * cq + 4],
                    xs[a][:, 4 * cq:4 * cq + 4, 4:12, 8 * j:8 * j + 8].rearrange("p c h w -> p h w c"), col,
                )

            def left_on_act(gi, tau):
                return gi < 4 or tau != 1

            def centre_on_act(gi, tau):
                return gi == 3

            def norm_vector(gi, tau):
                for cq in range(2):
                    side(gi, tau, 1, cq, False)
                for cq in range(2):
                    if not left_on_act(gi, tau):
                        side(gi, tau, 0, cq, False)
                for cq in range(2):
                    if not centre_on_act(gi, tau):
                        centre(gi, tau, cq, False)

            def norm_scalar(gi, n, parts):
                pieces = [(tau, cq) for tau in range(4) for cq in range(2)]
                for of_act, piece in ((left_on_act, lambda tau, cq: side(gi, tau, 0, cq, True)),
                                      (centre_on_act, lambda tau, cq: centre(gi, tau, cq, True))):
                    mine = [(tau, cq) for tau, cq in pieces if of_act(gi, tau)]
                    for i, (tau, cq) in enumerate(mine):
                        if i * parts // len(mine) == n:
                            piece(tau, cq)

            def hop(gi, g, t):
                if t == 0:
                    planes_of[(gi, g)] = ppool.tile([P, 4, 512], BF16, name="planes")
                planes = planes_of[(gi, g)]
                kt = 4 * g + t
                bank = hop_ps.tile([P, 512], F32, name="bank")
                for tau in range(4):
                    nc.tensor.transpose(
                        out=bank[:, tau * P:(tau + 1) * P],
                        in_=ntiles[(gi, tau)][:, kt * P:(kt + 1) * P],
                        identity=perm[:],
                    )
                nc.scalar.activation(
                    out=planes[:, t, :], in_=bank[:], func=ACTF.Identity,
                    scale=gbt[:, kt:kt + 1], bias=gbt[:, 32 + kt:33 + kt],
                )

            def regroup(gi, g, cols):
                if cols.start == 0:
                    grouped_of[(gi, g)] = gpool.tile([P, 512, 4], BF16, name="grouped", align_bytes=64)
                dst = grouped_of[(gi, g)][:, cols, :].rearrange("p (c i) t -> p c t i", i=4)
                src = planes_of[(gi, g)][:, :, cols].rearrange("p t (c i) -> p c t i", i=4)
                nc.vector.tensor_copy(out=dst, in_=src)

            def quant(gi, g, cols):
                if cols.start == 0:
                    ztiles[(gi, g)] = (
                        zpool.tile([P, 512], U32, name="zc", align_bytes=64),
                        zpool.tile([P, 512], U8, name="zs", align_bytes=64),
                    )
                zc, zs = ztiles[(gi, g)]
                nc.vector.quantize_mx(
                    out=zc[:, cols].bitcast(FP8X4), scales=zs[:, cols],
                    in_=grouped_of[(gi, g)][:, cols, :].rearrange("p w t -> p (w t)"),
                )

            def mx(gi, g, tau):
                zc, zs = ztiles[(gi, g)]
                if g == 0:
                    accs[(gi, tau)] = acc_ps.tile([P, DIM], F32, name="acc")
                nc.tensor.matmul_mx(
                    out=accs[(gi, tau)][:],
                    lhsT=zc[:, tau * P:(tau + 1) * P].bitcast(FP8X4),
                    lhsT_scale=zs[:, tau * P:(tau + 1) * P],
                    rhs=wc[:, g, :].bitcast(FP8X4),
                    rhs_scale=ws[:, g, :],
                    start=(g == 0),
                    stop=(g == PASSES - 1),
                )

            def finish(gi, tau):
                res = rpool.tile([P, DIM], F32, name="res")
                nc.vector.tensor_tensor(out=res[:], in0=accs[(gi, tau)][:], in1=bias[:], op=ALU.add)
                nc.sync.dma_start(out=out_v[gi // 4, 4 * (gi % 4) + tau], in_=res[:])

            rest = many_sums(0, 5, 16)
            for cq in range(2):
                first_sums(cq)
            first = stats(0, 0, 4, 0, 5, bs_first[:].rearrange("p h s q v -> p h s (q v)"), 32)
            for call in first[0:6]:
                call()
            for c in range(6, 8):
                nc.vector.tensor_copy(out=xs[0][:, c, 4:12, :], in_=xc[:, c])
            for n in range(4):
                rest[n]()
            for call in first[6:10]:
                call()
            rest[4]()
            rest[5]()
            for call in first[10:]:
                call()
            nc.vector.tensor_scalar(
                out=xs[0][96:128, 4:7, 12:16, :], in0=xs[0][96:128, 4:7, 12:16, :],
                scalar1=inside[96:128, :], scalar2=None, op0=ALU.mult,
            )
            for tau in range(4):
                norm_vector(0, tau)
                norm_scalar(0, tau, 4)
            gb_ps = hop_ps.tile([P, 512], F32, name="bank")
            nc.tensor.transpose(out=gb_ps[:, 0:P], in_=gb_f[:], identity=ident[:])
            nc.scalar.copy(out=gbt[:], in_=gb_ps[:, 0:P])
            nc.vector.tensor_scalar(
                out=hh[0][:, :, 6:10, 0], in0=hh[0][:, :, 6:10, 0], scalar1=0.5, scalar2=None, op0=ALU.mult
            )
            for call in rest[6:]:
                call()
        zpool = ctx.enter_context(tc.tile_pool(name="zpool", bufs=5))
        rpool = ctx.enter_context(tc.tile_pool(name="rpool", bufs=4))

        fill = {}
        for n, sl in enumerate((5, 6, 7, 8, 9, 10, 11, 12)):
            fill[sl] = many_sums(1, 2 * n, 2 * n + 2)
        opens = {2: stats(0, 4, 16, 5, 16, bs[0][:, :, 10:32, :], 64), 12: stats(1, 0, 16, 0, 16, bs[1][:], 64)}
        wins = {(3, 1): opens[2][5], (14, 1): opens[12][5]}
        closes = {3: opens[2], 14: opens[12]}
        for sl in range(NS + LAG_M + 1):
            chain = closes.get(sl, [])
            for t in range(4):
                if (sl, t) in wins:
                    wins[(sl, t)]()
                if sl < NS:
                    hop(sl // 5, sl % 5, t)
                if t == 1 and 0 <= sl - LAG_M < NS and sl < 34:
                    mx((sl - LAG_M) // 5, (sl - LAG_M) % 5, t - 1)
                    mx((sl - LAG_M) // 5, (sl - LAG_M) % 5, t)
                if t == 3 and 0 <= sl - LAG_M < NS:
                    for tau in range(2 if sl < 34 else 0, 4):
                        mx((sl - LAG_M) // 5, (sl - LAG_M) % 5, tau)
            if sl - LAG_M - 1 >= 0 and (sl - LAG_M - 1) % 5 == 4:
                for tau in range(4):
                    finish((sl - LAG_M - 1) // 5, tau)
            if sl == 1:
                load_w(4)
                for c in range(8):
                    nc.sync.dma_start(out=xs[1][:, c, 4:12, :].rearrange("p r w -> p (r w)"), in_=x_v[1, c])
                for c in range(8):
                    load_halo(1, c, False, False)
                    load_halo(1, c, True, False)
            if sl < PASSES - 1:
                regroup_w(sl + 1, sl < 2)
            if 1 <= sl <= PASSES:
                quant_w(sl - 1)
            for call in chain[6:10]:
                call()
            for call in fill.get(sl, []):
                call()
            if chain:
                quant((sl - LAG_Q) // 5, (sl - LAG_Q) % 5, WHOLE)
                regroup((sl - LAG_R) // 5, (sl - LAG_R) % 5, WHOLE)
            for call in chain[10:]:
                call()
            if sl in (3, 4):
                for tau in (2 * sl - 6, 2 * sl - 5):
                    norm_vector(1, tau)
                    norm_scalar(1, tau, 4)
            elif 4 < sl < 34:
                nxt = (sl + 1) // 5 + 1
                n = (sl + 1) % 5
                if sl == 5:
                    norm_vector(nxt, 0)
                    norm_scalar(nxt, 0, 5)
                if 0 < n < 4:
                    norm_vector(nxt, n)
                norm_scalar(nxt, n, 5)
            opening = opens.get(sl, [])
            for call in opening[0:1]:
                call()
            if 0 <= sl - LAG_Q < NS - 1 and not chain:
                quant((sl - LAG_Q) // 5, (sl - LAG_Q) % 5, WHOLE)
            for call in opening[1:2]:
                call()
            if 0 <= sl - LAG_R < NS - 1 and not chain:
                regroup((sl - LAG_R) // 5, (sl - LAG_R) % 5, WHOLE)
            for call in opening[2:5]:
                call()
            if 5 < sl < 34 and sl % 5 == 4:
                norm_vector((sl + 1) // 5 + 1, 0)
            if sl - LAG_R == NS - 1:
                for cols in HALVES:
                    regroup(NG - 1, PASSES - 1, cols)
                for cols in HALVES:
                    quant(NG - 1, PASSES - 1, cols)
